import numpy as np
import ml_dtypes


def mxq(x, axis, fmt="e4m3"):
    dtype, down = {"e4m3": (ml_dtypes.float8_e4m3fn, 7), "e5m2": (ml_dtypes.float8_e5m2, 14)}[fmt]
    v = np.moveaxis(np.asarray(x, np.float32).astype(ml_dtypes.bfloat16).astype(np.float64), axis, -1)
    blocks = v.reshape(v.shape[:-1] + (-1, 32))
    amax = np.abs(blocks).max(-1, keepdims=True)
    byte = np.maximum(np.where(amax > 0, np.frexp(amax)[1] - 1 + 127, 0) - down, 1)
    scale = np.exp2(byte - 127.0)
    codes = (blocks / scale).astype(np.float32).astype(dtype).astype(np.float64)
    return np.moveaxis((codes * scale).reshape(v.shape), -1, axis)


WIDE = False


def mx_kscale(k):
    if not WIDE:
        return np.ones(k)
    levels = np.array([10, -10, 5, -5, 0])
    a = np.random.permutation(np.resize(levels, k // 512 * 4)).reshape(k // 512, 4)
    idx = np.arange(k)
    return np.exp2(a[idx // 512, idx % 128 // 32])


BF16 = ml_dtypes.bfloat16


def bf(x):
    return np.asarray(x, np.float32).astype(BF16)


def f64(x):
    return np.asarray(x).astype(np.float64)


E2M1 = np.array([0.0, 0.5, 1.0, 1.5, 2.0, 3.0, 4.0, 6.0, -0.0, -0.5, -1.0, -1.5, -2.0, -3.0, -4.0, -6.0])


def pack_weight(w, fmt):
    k, n = w.shape
    w = f64(bf(w)).reshape(k // 32, 32, n)
    amax = np.abs(w).max(1)
    if fmt == "e4m3":
        byte = np.frexp(amax)[1] - 1 + 127 - 7
    else:
        mant, ex = np.frexp(amax / 6.0)
        byte = np.where(mant > 0.5, ex, ex - 1) + 127
    byte = np.clip(np.where(amax > 0, byte, 1), 1, 254)
    scaled = (w * np.exp2(127.0 - byte)[:, None, :]).reshape(k, n).astype(np.float32)
    by_word = np.ascontiguousarray(scaled.reshape(k // 512, 128, 4, n).transpose(0, 1, 3, 2))
    if fmt == "e4m3":
        words = by_word.astype(ml_dtypes.float8_e4m3fn).view(np.uint8)
    else:
        c = by_word.astype(ml_dtypes.float4_e2m1fn).view(np.uint8) & 0xF
        words = c[..., 0::2] | (c[..., 1::2] << 4)
    return np.ascontiguousarray(words), np.ascontiguousarray(byte.astype(np.uint8).reshape(k // 512, 16, n))


def unpack_weight(words, scales, fmt):
    g, p, n, _ = words.shape
    if fmt == "e4m3":
        vals = np.ascontiguousarray(words).view(ml_dtypes.float8_e4m3fn).astype(np.float64)
    else:
        nib = np.empty((g, p, n, 4), np.uint8)
        nib[..., 0::2] = words & 0xF
        nib[..., 1::2] = words >> 4
        vals = E2M1[nib]
    vals = vals * np.repeat(np.exp2(scales.astype(np.float64) - 127.0), 8, axis=1)[..., None]
    return vals.transpose(0, 1, 3, 2).reshape(g * 512, n)


B, CIN, CO, H, W, G, KT, KF = 1, 512, 128, 128, 128, 8, 3, 3
CG = CO // G
HALF = CO // 2
WIN = KT * KF
FMT = "e4m3"
A = np.sqrt(1.5) / (2.0 * CG) ** 0.25


def unfold(t):
    wins = [t[:, :, i:i + H, j:j + W] for i in range(KT) for j in range(KF)]
    return np.stack(wins, axis=-1).reshape(B, CO, H, W, KT, KF)


def setup_inputs():
    s = mx_kscale(CIN)
    x = bf(np.random.standard_normal((B, CIN, H, W)) * s[None, :, None, None])
    Wq_words, Wq_scales = pack_weight((np.random.standard_normal((CO, CIN)) * A / np.sqrt(CIN) / s[None, :]).T, FMT)
    Wk_words, Wk_scales = pack_weight((np.random.standard_normal((CO, CIN)) * A / np.sqrt(CIN) / s[None, :]).T, FMT)
    Wv_words, Wv_scales = pack_weight((np.random.standard_normal((CO, CIN)) / np.sqrt(CIN) / s[None, :]).T, FMT)
    rel_t = bf(np.random.standard_normal((HALF, KT)) * A)
    rel_f = bf(np.random.standard_normal((HALF, KF)) * A)
    return {
        "x": x,
        "Wq_words": Wq_words,
        "Wq_scales": Wq_scales,
        "Wk_words": Wk_words,
        "Wk_scales": Wk_scales,
        "Wv_words": Wv_words,
        "Wv_scales": Wv_scales,
        "rel_t": rel_t,
        "rel_f": rel_f,
    }


def reference(x, Wq_words, Wq_scales, Wk_words, Wk_scales, Wv_words, Wv_scales, rel_t, rel_f):
    pt, pf = (KT - 1) // 2, (KF - 1) // 2
    xq = mxq(f64(x).reshape(B, CIN, H * W), 1, "e4m3")
    q = (unpack_weight(Wq_words, Wq_scales, FMT).T @ xq).reshape(B, CO, H, W)
    k = (unpack_weight(Wk_words, Wk_scales, FMT).T @ xq).reshape(B, CO, H, W)
    v = (unpack_weight(Wv_words, Wv_scales, FMT).T @ xq).reshape(B, CO, H, W)
    pad = ((0, 0), (0, 0), (pt, pt), (pf, pf))
    kw = unfold(np.pad(k, pad))
    vw = unfold(np.pad(v, pad))
    kw = np.concatenate([
        kw[:, :HALF] + f64(rel_t)[None, :, None, None, :, None],
        kw[:, HALF:] + f64(rel_f)[None, :, None, None, None, :],
    ], axis=1)
    kw = kw.reshape(B, G, CG, H, W, WIN)
    vw = vw.reshape(B, G, CG, H, W, WIN)
    qg = q.reshape(B, G, CG, H, W, 1)
    energy = np.sum(qg * kw, axis=2)
    e = np.exp(energy - energy.max(-1, keepdims=True))
    attn = e / e.sum(-1, keepdims=True)
    out = np.sum(attn[:, :, None] * vw, axis=-1)
    return out.reshape(B, CO, H, W), attn

@@ -1,0 +1,409 @@
+from contextlib import ExitStack
+
+import concourse.mybir as mybir
+from concourse.masks import make_identity
+
+F32 = mybir.dt.float32
+BF16 = mybir.dt.bfloat16
+U32 = mybir.dt.uint32
+U8 = mybir.dt.uint8
+I32 = mybir.dt.int32
+FP8X4 = mybir.dt.float8_e4m3fn_x4
+ALU = mybir.AluOpType
+AXIS_X = mybir.AxisListType.X
+EXP = mybir.ActivationFunctionType.Exp
+
+P = 128
+PACK = 4
+C_IN = P * PACK
+C_OUT = 128
+H = 128
+W = 128
+GROUPS = 8
+CG = C_OUT // GROUPS
+K3 = 3
+NWIN = K3 * K3
+ROWS = P // GROUPS
+BLOCKS = H // ROWS
+CHUNK_ROWS = 4
+CHUNK = CHUNK_ROWS * W
+CHUNKS = ROWS // CHUNK_ROWS
+WPAD = W + 2
+STORE_ROWS = 8
+ACC_ROWS = 4
+
+FLOPS = 2 * C_IN * 3 * C_OUT * H * W + 2 * 2 * NWIN * C_OUT * H * W
+
+Q_IDX, K_IDX, V_IDX = 0, 1, 2
+
+
+def tile_mutliheadattention2d_kernel(
+    tc, x, wq_words, wq_scales, wk_words, wk_scales, wv_words, wv_scales, rel_t, rel_f, out, attn
+):
+    nc = tc.nc
+    with ExitStack() as ctx:
+        const = ctx.enter_context(tc.tile_pool(name="const", bufs=1))
+        xin = ctx.enter_context(tc.tile_pool(name="xin", bufs=4))
+        grp = ctx.enter_context(tc.tile_pool(name="grp", bufs=2))
+        quant = ctx.enter_context(tc.tile_pool(name="quant", bufs=2))
+        one = ctx.enter_context(tc.tile_pool(name="one", bufs=1))
+        ring3 = ctx.enter_context(tc.tile_pool(name="ring3", bufs=3))
+        two = ctx.enter_context(tc.tile_pool(name="two", bufs=2))
+        ps_mx = ctx.enter_context(tc.psum_pool(name="ps_mx", bufs=3))
+        ps_kt = ctx.enter_context(tc.psum_pool(name="ps_kt", bufs=2))
+        ps_ea = ctx.enter_context(tc.psum_pool(name="ps_ea", bufs=2))
+        ps_acc = ctx.enter_context(tc.psum_pool(name="ps_acc", bufs=1))
+
+        ident = const.tile([P, P], F32)
+        make_identity(nc, ident[:])
+        perm = const.tile([P, P], F32)
+        nc.vector.tensor_copy(
+            out=perm[:].rearrange("p (c g) -> p c g", g=GROUPS),
+            in_=ident[:].rearrange("p (g c) -> p c g", c=CG),
+        )
+        shift_up = const.tile([P, P], F32)
+        nc.vector.tensor_copy(out=shift_up[:, 1:P], in_=ident[:, 0 : P - 1])
+        nc.vector.tensor_copy(out=shift_up[:, 0:1], in_=ident[:, P - 1 : P])
+        shift_down = const.tile([P, P], F32)
+        nc.vector.tensor_copy(out=shift_down[:, 0 : P - 1], in_=ident[:, 1:P])
+        nc.vector.tensor_copy(out=shift_down[:, P - 1 : P], in_=ident[:, 0:1])
+        shift = (shift_up, ident, shift_down)
+
+        zeros = const.tile([P, 2 * ROWS], F32)
+        nc.vector.memset(zeros[:], 0.0)
+
+        rel3 = const.tile([P, K3], BF16)
+        nc.sync.dma_start(out=rel3[0 : P // 2, :], in_=rel_t)
+        nc.sync.dma_start(out=rel3[P // 2 : P, :], in_=rel_f)
+        rel9 = const.tile([P, K3, K3], F32)
+        half = P // 2
+        nc.vector.tensor_copy(
+            out=rel9[0:half], in_=rel3[0:half, :].unsqueeze(2).to_broadcast([half, K3, K3])
+        )
+        nc.vector.tensor_copy(
+            out=rel9[half:P], in_=rel3[half:P, :].unsqueeze(1).to_broadcast([half, K3, K3])
+        )
+        in_group = const.tile([P, GROUPS], F32)
+        nc.vector.tensor_reduce(
+            out=in_group[:], in_=ident[:].rearrange("p (g c) -> p g c", c=CG), axis=AXIS_X, op=ALU.add
+        )
+        rel_by_place = const.tile([P, NWIN, GROUPS], F32)
+        nc.vector.tensor_tensor(
+            out=rel_by_place[:],
+            in0=rel9[:].rearrange("p i j -> p (i j)").unsqueeze(2).to_broadcast([P, NWIN, GROUPS]),
+            in1=in_group[:].unsqueeze(1).to_broadcast([P, NWIN, GROUPS]),
+            op=ALU.mult,
+        )
+
+        w_codes = const.tile([P, 3, C_OUT], U32, align_bytes=64)
+        w_scales = const.tile([P, 3, C_OUT], U8, align_bytes=64)
+        nc.vector.memset(w_scales[:].rearrange("p a n -> p (a n)").bitcast(I32), 0)
+        for idx, (words, scales) in enumerate(
+            ((wq_words, wq_scales), (wk_words, wk_scales), (wv_words, wv_scales))
+        ):
+            nc.sync.dma_start(
+                out=w_codes[:, idx, :].bitcast(I32),
+                in_=words[0].rearrange("p n t -> p (n t)").bitcast(I32),
+            )
+            for quad in range(4):
+                nc.sync.dma_start(
+                    out=w_scales[32 * quad : 32 * quad + 4, idx, :].bitcast(I32),
+                    in_=scales[0, 4 * quad : 4 * quad + 4, :].bitcast(I32),
+                )
+
+        x_by_word = x[0].rearrange("(p t) h w -> p t (h w)", t=PACK)
+
+        raw_of = {}
+        codes_of = {}
+        k_of = {}
+        v_of = {}
+        q_of = {}
+
+        def load_x(b):
+            for k in range(CHUNKS):
+                raw = xin.tile([P, PACK, CHUNK], BF16, name="raw")
+                first = (b * CHUNKS + k) * CHUNK
+                nc.sync.dma_start(out=raw[:], in_=x_by_word[:, :, first : first + CHUNK])
+                raw_of[(b, k)] = raw
+
+        def quantise(b):
+            codes = quant.tile([P, ROWS * W], U32, name="codes", align_bytes=64)
+            scales = quant.tile([P, ROWS * W], U8, name="scales", align_bytes=64)
+            for k in range(CHUNKS):
+                raw = raw_of[(b, k)]
+                grouped = grp.tile([P, CHUNK, PACK], BF16, name="grouped", align_bytes=64)
+                nc.scalar.copy(
+                    out=grouped[:].rearrange("p (c i) t -> p c t i", i=4),
+                    in_=raw[:].rearrange("p t (c i) -> p c t i", i=4),
+                )
+                cols = slice(k * CHUNK, (k + 1) * CHUNK)
+                nc.vector.quantize_mx(
+                    out=codes[:, cols].bitcast(FP8X4),
+                    scales=scales[:, cols],
+                    in_=grouped[:].rearrange("p w t -> p (w t)"),
+                )
+            codes_of[b] = (codes, scales)
+
+        def project_by_channel(b, idx, k):
+            codes, scales = codes_of[b]
+            cols = slice(k * CHUNK, (k + 1) * CHUNK)
+            acc = ps_mx.tile([P, CHUNK], F32, name="mx", tag="mx")
+            nc.tensor.matmul_mx(
+                out=acc[:],
+                lhsT=w_codes[:, idx, :].bitcast(FP8X4),
+                lhsT_scale=w_scales[:, idx, :],
+                rhs=codes[:, cols].bitcast(FP8X4),
+                rhs_scale=scales[:, cols],
+                start=True,
+                stop=True,
+            )
+            return acc
+
+        def project_k(b):
+            k_rows = ring3.tile([P, ROWS, WPAD], F32, name="k_rows")
+            nc.scalar.copy(
+                out=k_rows[:, :, 0 : WPAD : WPAD - 1],
+                in_=zeros[:].rearrange("p (r e) -> p r e", e=2),
+            )
+            for k in range(CHUNKS):
+                acc = project_by_channel(b, K_IDX, k)
+                nc.scalar.copy(
+                    out=k_rows[:, k * CHUNK_ROWS : (k + 1) * CHUNK_ROWS, 1 : W + 1],
+                    in_=acc[:].rearrange("p (r w) -> p r w", w=W),
+                )
+            k_of[b] = k_rows
+
+        def project_q(b):
+            q_rows = one.tile([P, ROWS, W], F32, name="q_rows")
+            q_pix = one.tile([P, ROWS, C_OUT], F32, name="q_pix")
+            qr_pix = one.tile([P, NWIN, ROWS, GROUPS], F32, name="qr_pix")
+            for k in range(CHUNKS):
+                acc = project_by_channel(b, Q_IDX, k)
+                nc.scalar.copy(
+                    out=q_rows[:, k * CHUNK_ROWS : (k + 1) * CHUNK_ROWS, :],
+                    in_=acc[:].rearrange("p (r w) -> p r w", w=W),
+                )
+            for k in range(CHUNKS):
+                rows = slice(k * CHUNK_ROWS, (k + 1) * CHUNK_ROWS)
+                turned = ps_mx.tile([P, CHUNK], F32, name="turned", tag="mx")
+                for r in range(CHUNK_ROWS):
+                    nc.tensor.transpose(
+                        turned[:, r * P : (r + 1) * P], q_rows[:, k * CHUNK_ROWS + r, :], perm[:]
+                    )
+                nc.scalar.copy(
+                    out=q_pix[:, rows, :], in_=turned[:].rearrange("p (r o) -> p r o", o=C_OUT)
+                )
+                width = NWIN * GROUPS
+                qr = ps_mx.tile([P, CHUNK], F32, name="qr", tag="mx")
+                for r in range(CHUNK_ROWS):
+                    nc.tensor.matmul(
+                        out=qr[:, r * width : (r + 1) * width],
+                        lhsT=q_rows[:, k * CHUNK_ROWS + r, :],
+                        rhs=rel_by_place[:].rearrange("p n g -> p (n g)"),
+                        start=True,
+                        stop=True,
+                    )
+                nc.scalar.copy(
+                    out=qr_pix[:, :, rows, :].rearrange("p n r g -> p r n g"),
+                    in_=qr[:, 0 : CHUNK_ROWS * width].rearrange(
+                        "p (r n g) -> p r n g", n=NWIN, g=GROUPS
+                    ),
+                )
+            q_of[b] = (q_pix, qr_pix)
+
+        def project_v(b):
+            codes, scales = codes_of[b]
+            v_pix = ring3.tile([P, ROWS, C_OUT], F32, name="v_pix")
+            for k in range(CHUNKS):
+                acc = ps_mx.tile([P, CHUNK], F32, name="mxv", tag="mx")
+                for r in range(CHUNK_ROWS):
+                    cols = slice((k * CHUNK_ROWS + r) * W, (k * CHUNK_ROWS + r + 1) * W)
+                    nc.tensor.matmul_mx(
+                        out=acc[:, r * C_OUT : (r + 1) * C_OUT],
+                        lhsT=codes[:, cols].bitcast(FP8X4),
+                        lhsT_scale=scales[:, cols],
+                        rhs=w_codes[:, V_IDX, :].bitcast(FP8X4),
+                        rhs_scale=w_scales[:, V_IDX, :],
+                        start=True,
+                        stop=True,
+                    )
+                nc.scalar.copy(
+                    out=v_pix[:, k * CHUNK_ROWS : (k + 1) * CHUNK_ROWS, :],
+                    in_=acc[:].rearrange("p (r o) -> p r o", o=C_OUT),
+                )
+            v_of[b] = v_pix
+
+        qk = one.tile([P, NWIN, CG, ROWS, GROUPS], F32, name="qk")
+
+        def energy_products(b):
+            q_pix = q_of[b][0]
+            if b == 0:
+                nc.gpsimd.memset(qk[:, 0:K3, :, 0, :], 0.0)
+            if b == BLOCKS - 1:
+                nc.gpsimd.memset(qk[:, NWIN - K3 : NWIN, :, ROWS - 1, :], 0.0)
+            for s in range(-1, ROWS + 1):
+                src = b * ROWS + s
+                if src < 0 or src >= H:
+                    continue
+                k_row = k_of[src // ROWS][:, src % ROWS, :]
+                k_pix = ps_kt.tile([P, K3, C_OUT], F32, name="k_pix")
+                for j in range(K3):
+                    nc.tensor.transpose(k_pix[:, j, :], k_row[:, j : j + W], perm[:])
+                for i in range(K3):
+                    t = s - i + 1
+                    if t < 0 or t >= ROWS:
+                        continue
+                    nc.vector.tensor_tensor(
+                        out=qk[:, K3 * i : K3 * i + K3, :, t, :],
+                        in0=k_pix[:].rearrange("p j (c g) -> p j c g", g=GROUPS),
+                        in1=q_pix[:, t, :]
+                        .rearrange("p (c g) -> p c g", g=GROUPS)
+                        .unsqueeze(1)
+                        .to_broadcast([P, K3, CG, GROUPS]),
+                        op=ALU.mult,
+                    )
+
+        energy_of = {}
+
+        def energy_sums(b, i):
+            if i == 0:
+                energy_of[b] = one.tile([P, NWIN, W], F32, name="energy")
+            qr_pix = q_of[b][1]
+            e_ps = ps_ea.tile([P, K3, W], F32, name="e_ps", tag="ea")
+            for j in range(K3):
+                n = K3 * i + j
+                for c in range(CG):
+                    nc.tensor.matmul(
+                        out=e_ps[:, j, :],
+                        lhsT=qk[:, n, c, :, :].rearrange("p r g -> p (r g)"),
+                        rhs=ident[:],
+                        is_transpose=True,
+                        start=(c == 0),
+                        stop=False,
+                    )
+                nc.tensor.matmul(
+                    out=e_ps[:, j, :],
+                    lhsT=qr_pix[:, n, :, :].rearrange("p r g -> p (r g)"),
+                    rhs=ident[:],
+                    is_transpose=True,
+                    start=False,
+                    stop=True,
+                )
+            nc.scalar.copy(out=energy_of[b][:, K3 * i : K3 * i + K3, :], in_=e_ps[:])
+
+        attn_pix_of = {}
+
+        def softmax(b):
+            energy = energy_of[b]
+            by_pixel = energy[:].rearrange("p n w -> p w n")
+            top = one.tile([P, W], F32, name="top")
+            nc.vector.tensor_reduce(out=top[:], in_=by_pixel, axis=AXIS_X, op=ALU.max)
+            nc.vector.tensor_tensor(
+                out=energy[:],
+                in0=energy[:],
+                in1=top[:].unsqueeze(1).to_broadcast([P, NWIN, W]),
+                op=ALU.subtract,
+            )
+            nc.scalar.activation(out=energy[:], in_=energy[:], func=EXP)
+            total = one.tile([P, W], F32, name="total")
+            nc.vector.tensor_reduce(out=total[:], in_=by_pixel, axis=AXIS_X, op=ALU.add)
+            inverse = one.tile([P, W], F32, name="inverse")
+            nc.vector.reciprocal(out=inverse[:], in_=total[:])
+            attn_rows = one.tile([P, NWIN, WPAD], F32, name="attn_rows")
+            nc.vector.memset(attn_rows[:, :, 0 : WPAD : WPAD - 1], 0.0)
+            nc.vector.tensor_tensor(
+                out=attn_rows[:, :, 1 : W + 1],
+                in0=energy[:],
+                in1=inverse[:].unsqueeze(1).to_broadcast([P, NWIN, W]),
+                op=ALU.mult,
+            )
+            attn_store = one.tile([P, W, NWIN], F32, name="attn_store")
+            nc.scalar.copy(
+                out=attn_store[:], in_=attn_rows[:, :, 1 : W + 1].rearrange("p n w -> p w n")
+            )
+            nc.sync.dma_start(
+                out=attn[0, :, b * ROWS : (b + 1) * ROWS, :, :].rearrange("g h w n -> h g (w n)"),
+                in_=attn_store[:].rearrange("p w n -> p (w n)"),
+            )
+            attn_pix = one.tile([P, NWIN, P], F32, name="attn_pix")
+            for i in range(K3):
+                a_ps = ps_ea.tile([P, K3, P], F32, name="a_ps", tag="ea")
+                for j in range(K3):
+                    nc.tensor.transpose(
+                        a_ps[:, j, :], attn_rows[:, K3 * i + j, 2 - j : 2 - j + W], ident[:]
+                    )
+                nc.scalar.copy(out=attn_pix[:, K3 * i : K3 * i + K3, :], in_=a_ps[:])
+            attn_pix_of[b] = attn_pix
+
+        out_of = {}
+        acc_of = {}
+
+        def weighted_sum_row(b, t):
+            attn_pix = attn_pix_of[b]
+            row = b * ROWS + t
+            av = two.tile([P, NWIN, C_OUT], F32, name="av")
+            places = []
+            for i in range(K3):
+                src = row + i - 1
+                if src < 0 or src >= H:
+                    continue
+                nc.vector.tensor_tensor(
+                    out=av[:, K3 * i : K3 * i + K3, :].rearrange("p j (g c) -> p j g c", c=CG),
+                    in0=v_of[src // ROWS][:, src % ROWS, :]
+                    .rearrange("p (g c) -> p g c", c=CG)
+                    .unsqueeze(1)
+                    .to_broadcast([P, K3, GROUPS, CG]),
+                    in1=attn_pix[:, K3 * i : K3 * i + K3, t * GROUPS : (t + 1) * GROUPS]
+                    .unsqueeze(3)
+                    .to_broadcast([P, K3, GROUPS, CG]),
+                    op=ALU.mult,
+                )
+                places.extend([(i, j) for j in range(K3)])
+            if t % ACC_ROWS == 0:
+                acc_of[0] = ps_acc.tile([P, ACC_ROWS, W], F32, name="acc")
+            acc = acc_of[0]
+            a = t % ACC_ROWS
+            for order, (i, j) in enumerate(places):
+                nc.tensor.matmul(
+                    out=acc[:, a, :],
+                    lhsT=av[:, K3 * i + j, :],
+                    rhs=shift[j][:],
+                    is_transpose=True,
+                    start=(order == 0),
+                    stop=(order == len(places) - 1),
+                )
+            if t % STORE_ROWS == 0:
+                out_of[0] = two.tile([P, STORE_ROWS, W], F32, name="out_rows")
+            out_rows = out_of[0]
+            if a == ACC_ROWS - 1:
+                last = t % STORE_ROWS
+                nc.scalar.copy(
+                    out=out_rows[:, last - ACC_ROWS + 1 : last + 1, :], in_=acc[:]
+                )
+            if t % STORE_ROWS == STORE_ROWS - 1:
+                nc.sync.dma_start(out=out[0, :, row - STORE_ROWS + 1 : row + 1, :], in_=out_rows[:])
+
+        load_x(0)
+        quantise(0)
+        load_x(1)
+        project_k(0)
+        project_q(0)
+        project_v(0)
+        for b in range(BLOCKS):
+            if b + 1 < BLOCKS:
+                quantise(b + 1)
+                if b + 2 < BLOCKS:
+                    load_x(b + 2)
+                project_k(b + 1)
+            energy_products(b)
+            for t in range(ROWS):
+                if b > 0:
+                    weighted_sum_row(b - 1, t)
+                if t < K3:
+                    energy_sums(b, t)
+            softmax(b)
+            if b + 1 < BLOCKS:
+                project_q(b + 1)
+                project_v(b + 1)
+        for t in range(ROWS):
+            weighted_sum_row(BLOCKS - 1, t)

@@ -29,7 +29,9 @@ CHUNK_ROWS = 4
 CHUNK = CHUNK_ROWS * W
 CHUNKS = ROWS // CHUNK_ROWS
 WPAD = W + 2
-STORE_ROWS = 8
+STORE_ROWS = 4
+V_ROWS = 3
+CG_HALF = CG // 2
 ACC_ROWS = 4
 
 FLOPS = 2 * C_IN * 3 * C_OUT * H * W + 2 * 2 * NWIN * C_OUT * H * W
@@ -45,10 +47,11 @@ def tile_mutliheadattention2d_kernel(
         const = ctx.enter_context(tc.tile_pool(name="const", bufs=1))
         xin = ctx.enter_context(tc.tile_pool(name="xin", bufs=4))
         grp = ctx.enter_context(tc.tile_pool(name="grp", bufs=2))
-        quant = ctx.enter_context(tc.tile_pool(name="quant", bufs=2))
+        quant = ctx.enter_context(tc.tile_pool(name="quant", bufs=4))
         one = ctx.enter_context(tc.tile_pool(name="one", bufs=1))
         ring3 = ctx.enter_context(tc.tile_pool(name="ring3", bufs=3))
         two = ctx.enter_context(tc.tile_pool(name="two", bufs=2))
+        ring4 = ctx.enter_context(tc.tile_pool(name="ring4", bufs=4))
         ps_mx = ctx.enter_context(tc.psum_pool(name="ps_mx", bufs=3))
         ps_kt = ctx.enter_context(tc.psum_pool(name="ps_kt", bufs=2))
         ps_ea = ctx.enter_context(tc.psum_pool(name="ps_ea", bufs=2))
@@ -116,7 +119,6 @@ def tile_mutliheadattention2d_kernel(
         raw_of = {}
         codes_of = {}
         k_of = {}
-        v_of = {}
         q_of = {}
 
         def load_x(b):
@@ -211,28 +213,6 @@ def tile_mutliheadattention2d_kernel(
                 )
             q_of[b] = (q_pix, qr_pix)
 
-        def project_v(b):
-            codes, scales = codes_of[b]
-            v_pix = ring3.tile([P, ROWS, C_OUT], F32, name="v_pix")
-            for k in range(CHUNKS):
-                acc = ps_mx.tile([P, CHUNK], F32, name="mxv", tag="mx")
-                for r in range(CHUNK_ROWS):
-                    cols = slice((k * CHUNK_ROWS + r) * W, (k * CHUNK_ROWS + r + 1) * W)
-                    nc.tensor.matmul_mx(
-                        out=acc[:, r * C_OUT : (r + 1) * C_OUT],
-                        lhsT=codes[:, cols].bitcast(FP8X4),
-                        lhsT_scale=scales[:, cols],
-                        rhs=w_codes[:, V_IDX, :].bitcast(FP8X4),
-                        rhs_scale=w_scales[:, V_IDX, :],
-                        start=True,
-                        stop=True,
-                    )
-                nc.scalar.copy(
-                    out=v_pix[:, k * CHUNK_ROWS : (k + 1) * CHUNK_ROWS, :],
-                    in_=acc[:].rearrange("p (r o) -> p r o", o=C_OUT),
-                )
-            v_of[b] = v_pix
-
         qk = one.tile([P, NWIN, CG, ROWS, GROUPS], F32, name="qk")
 
         def energy_products(b):
@@ -243,24 +223,31 @@ def tile_mutliheadattention2d_kernel(
                 nc.gpsimd.memset(qk[:, NWIN - K3 : NWIN, :, ROWS - 1, :], 0.0)
             for s in range(-1, ROWS + 1):
                 src = b * ROWS + s
-                if src < 0 or src >= H:
-                    continue
-                k_row = k_of[src // ROWS][:, src % ROWS, :]
-                k_pix = ps_kt.tile([P, K3, C_OUT], F32, name="k_pix")
-                for j in range(K3):
-                    nc.tensor.transpose(k_pix[:, j, :], k_row[:, j : j + W], perm[:])
-                for i in range(K3):
-                    t = s - i + 1
-                    if t < 0 or t >= ROWS:
-                        continue
-                    nc.vector.tensor_tensor(
-                        out=qk[:, K3 * i : K3 * i + K3, :, t, :],
-                        in0=k_pix[:].rearrange("p j (c g) -> p j c g", g=GROUPS),
-                        in1=q_pix[:, t, :]
-                        .rearrange("p (c g) -> p c g", g=GROUPS)
-                        .unsqueeze(1)
-                        .to_broadcast([P, K3, CG, GROUPS]),
-                        op=ALU.mult,
+                if 0 <= src < H:
+                    k_row = k_of[src // ROWS][:, src % ROWS, :]
+                    k_pix = ps_kt.tile([P, K3, C_OUT], F32, name="k_pix")
+                    for j in range(K3):
+                        nc.tensor.transpose(k_pix[:, j, :], k_row[:, j : j + W], perm[:])
+                    for i in range(K3):
+                        t = s - i + 1
+                        if t < 0 or t >= ROWS:
+                            continue
+                        nc.vector.tensor_tensor(
+                            out=qk[:, K3 * i : K3 * i + K3, :, t, :],
+                            in0=k_pix[:].rearrange("p j (c g) -> p j c g", g=GROUPS),
+                            in1=q_pix[:, t, :]
+                            .rearrange("p (c g) -> p c g", g=GROUPS)
+                            .unsqueeze(1)
+                            .to_broadcast([P, K3, CG, GROUPS]),
+                            op=ALU.mult,
+                        )
+                done = s - 1
+                if done >= 0:
+                    nc.gpsimd.tensor_tensor(
+                        out=qk[:, :, 0:CG_HALF, done, :],
+                        in0=qk[:, :, 0:CG_HALF, done, :],
+                        in1=qk[:, :, CG_HALF:CG, done, :],
+                        op=ALU.add,
                     )
 
         energy_of = {}
@@ -272,7 +259,7 @@ def tile_mutliheadattention2d_kernel(
             e_ps = ps_ea.tile([P, K3, W], F32, name="e_ps", tag="ea")
             for j in range(K3):
                 n = K3 * i + j
-                for c in range(CG):
+                for c in range(CG_HALF):
                     nc.tensor.matmul(
                         out=e_ps[:, j, :],
                         lhsT=qk[:, n, c, :, :].rearrange("p r g -> p (r g)"),
@@ -335,52 +322,82 @@ def tile_mutliheadattention2d_kernel(
                 nc.scalar.copy(out=attn_pix[:, K3 * i : K3 * i + K3, :], in_=a_ps[:])
             attn_pix_of[b] = attn_pix
 
-        out_of = {}
         acc_of = {}
 
-        def weighted_sum_row(b, t):
+        av_of = {}
+        v_of = {}
+
+        def weighted_sum_step(b, s):
             attn_pix = attn_pix_of[b]
+            codes_row = b * ROWS + s
+            if (s + 1) % V_ROWS == 0:
+                v_of[0] = ps_mx.tile([P, CHUNK], F32, name="v_pix", tag="mx")
+                for r in range(V_ROWS):
+                    src = codes_row + r
+                    if src < 0 or src >= H:
+                        continue
+                    codes, scales = codes_of[src // ROWS]
+                    cols = slice((src % ROWS) * W, (src % ROWS + 1) * W)
+                    nc.tensor.matmul_mx(
+                        out=v_of[0][:, r * C_OUT : (r + 1) * C_OUT],
+                        lhsT=codes[:, cols].bitcast(FP8X4),
+                        lhsT_scale=scales[:, cols],
+                        rhs=w_codes[:, V_IDX, :].bitcast(FP8X4),
+                        rhs_scale=w_scales[:, V_IDX, :],
+                        start=True,
+                        stop=True,
+                    )
+            if s + 1 < ROWS:
+                av_of[s + 1] = ring4.tile([P, NWIN, C_OUT], F32, name="av")
+            if 0 <= codes_row < H:
+                r = (s + 1) % V_ROWS
+                for i in range(K3):
+                    t = s - i + 1
+                    if t < 0 or t >= ROWS:
+                        continue
+                    nc.vector.tensor_tensor(
+                        out=av_of[t][:, K3 * i : K3 * i + K3, :].rearrange(
+                            "p j (g c) -> p j g c", c=CG
+                        ),
+                        in0=v_of[0][:, r * C_OUT : (r + 1) * C_OUT]
+                        .rearrange("p (g c) -> p g c", c=CG)
+                        .unsqueeze(1)
+                        .to_broadcast([P, K3, GROUPS, CG]),
+                        in1=attn_pix[:, K3 * i : K3 * i + K3, t * GROUPS : (t + 1) * GROUPS]
+                        .unsqueeze(3)
+                        .to_broadcast([P, K3, GROUPS, CG]),
+                        op=ALU.mult,
+                    )
+            t = s - 1
+            if t < 0:
+                return
             row = b * ROWS + t
-            av = two.tile([P, NWIN, C_OUT], F32, name="av")
-            places = []
-            for i in range(K3):
-                src = row + i - 1
-                if src < 0 or src >= H:
-                    continue
-                nc.vector.tensor_tensor(
-                    out=av[:, K3 * i : K3 * i + K3, :].rearrange("p j (g c) -> p j g c", c=CG),
-                    in0=v_of[src // ROWS][:, src % ROWS, :]
-                    .rearrange("p (g c) -> p g c", c=CG)
-                    .unsqueeze(1)
-                    .to_broadcast([P, K3, GROUPS, CG]),
-                    in1=attn_pix[:, K3 * i : K3 * i + K3, t * GROUPS : (t + 1) * GROUPS]
-                    .unsqueeze(3)
-                    .to_broadcast([P, K3, GROUPS, CG]),
-                    op=ALU.mult,
+            av = av_of[t]
+            window_rows = [i for i in range(K3) if 0 <= row + i - 1 < H]
+            base = K3 * window_rows[0]
+            for i in window_rows[1:]:
+                nc.gpsimd.tensor_tensor(
+                    out=av[:, base : base + K3, :],
+                    in0=av[:, base : base + K3, :],
+                    in1=av[:, K3 * i : K3 * i + K3, :],
+                    op=ALU.add,
                 )
-                places.extend([(i, j) for j in range(K3)])
             if t % ACC_ROWS == 0:
                 acc_of[0] = ps_acc.tile([P, ACC_ROWS, W], F32, name="acc")
             acc = acc_of[0]
             a = t % ACC_ROWS
-            for order, (i, j) in enumerate(places):
+            for j in range(K3):
                 nc.tensor.matmul(
                     out=acc[:, a, :],
-                    lhsT=av[:, K3 * i + j, :],
+                    lhsT=av[:, base + j, :],
                     rhs=shift[j][:],
                     is_transpose=True,
-                    start=(order == 0),
-                    stop=(order == len(places) - 1),
+                    start=(j == 0),
+                    stop=(j == K3 - 1),
                 )
-            if t % STORE_ROWS == 0:
-                out_of[0] = two.tile([P, STORE_ROWS, W], F32, name="out_rows")
-            out_rows = out_of[0]
             if a == ACC_ROWS - 1:
-                last = t % STORE_ROWS
-                nc.scalar.copy(
-                    out=out_rows[:, last - ACC_ROWS + 1 : last + 1, :], in_=acc[:]
-                )
-            if t % STORE_ROWS == STORE_ROWS - 1:
+                out_rows = two.tile([P, STORE_ROWS, W], F32, name="out_rows")
+                nc.scalar.copy(out=out_rows[:], in_=acc[:])
                 nc.sync.dma_start(out=out[0, :, row - STORE_ROWS + 1 : row + 1, :], in_=out_rows[:])
 
         load_x(0)
@@ -388,7 +405,6 @@ def tile_mutliheadattention2d_kernel(
         load_x(1)
         project_k(0)
         project_q(0)
-        project_v(0)
         for b in range(BLOCKS):
             if b + 1 < BLOCKS:
                 quantise(b + 1)
@@ -396,14 +412,13 @@ def tile_mutliheadattention2d_kernel(
                     load_x(b + 2)
                 project_k(b + 1)
             energy_products(b)
-            for t in range(ROWS):
+            for step in range(ROWS + 2):
                 if b > 0:
-                    weighted_sum_row(b - 1, t)
-                if t < K3:
-                    energy_sums(b, t)
+                    weighted_sum_step(b - 1, step - 1)
+                if step < K3:
+                    energy_sums(b, step)
             softmax(b)
             if b + 1 < BLOCKS:
                 project_q(b + 1)
-                project_v(b + 1)
-        for t in range(ROWS):
-            weighted_sum_row(BLOCKS - 1, t)
+        for step in range(ROWS + 2):
+            weighted_sum_step(BLOCKS - 1, step - 1)

@@ -21,18 +21,23 @@ H = 128
 W = 128
 GROUPS = 8
 CG = C_OUT // GROUPS
+CG_HALF = CG // 2
 K3 = 3
 NWIN = K3 * K3
 ROWS = P // GROUPS
 BLOCKS = H // ROWS
 CHUNK_ROWS = 4
 CHUNK = CHUNK_ROWS * W
-CHUNKS = ROWS // CHUNK_ROWS
+CHUNKS = H // CHUNK_ROWS
 WPAD = W + 2
-STORE_ROWS = 4
-V_ROWS = 3
-CG_HALF = CG // 2
-ACC_ROWS = 4
+QR = NWIN * GROUPS
+
+LEAD = 6
+SUMS_AT = ROWS + 2
+TOP_AT = SUMS_AT + NWIN
+NORM_AT = TOP_AT + 2
+TURN_AT = NORM_AT + 2
+LAG = TURN_AT + K3 + 2
 
 FLOPS = 2 * C_IN * 3 * C_OUT * H * W + 2 * 2 * NWIN * C_OUT * H * W
 
@@ -45,16 +50,16 @@ def tile_mutliheadattention2d_kernel(
     nc = tc.nc
     with ExitStack() as ctx:
         const = ctx.enter_context(tc.tile_pool(name="const", bufs=1))
-        xin = ctx.enter_context(tc.tile_pool(name="xin", bufs=4))
-        grp = ctx.enter_context(tc.tile_pool(name="grp", bufs=2))
-        quant = ctx.enter_context(tc.tile_pool(name="quant", bufs=4))
         one = ctx.enter_context(tc.tile_pool(name="one", bufs=1))
-        ring3 = ctx.enter_context(tc.tile_pool(name="ring3", bufs=3))
         two = ctx.enter_context(tc.tile_pool(name="two", bufs=2))
-        ring4 = ctx.enter_context(tc.tile_pool(name="ring4", bufs=4))
-        ps_mx = ctx.enter_context(tc.psum_pool(name="ps_mx", bufs=3))
+        three = ctx.enter_context(tc.tile_pool(name="three", bufs=3))
+        four = ctx.enter_context(tc.tile_pool(name="four", bufs=4))
+        five = ctx.enter_context(tc.tile_pool(name="five", bufs=5))
+        quant = ctx.enter_context(tc.tile_pool(name="quant", bufs=(LAG + LEAD + 3 * CHUNK_ROWS) // CHUNK_ROWS))
+        ps_mx = ctx.enter_context(tc.psum_pool(name="ps_mx", bufs=2))
+        ps_v = ctx.enter_context(tc.psum_pool(name="ps_v", bufs=2))
         ps_kt = ctx.enter_context(tc.psum_pool(name="ps_kt", bufs=2))
-        ps_ea = ctx.enter_context(tc.psum_pool(name="ps_ea", bufs=2))
+        ps_ea = ctx.enter_context(tc.psum_pool(name="ps_ea", bufs=1))
         ps_acc = ctx.enter_context(tc.psum_pool(name="ps_acc", bufs=1))
 
         ident = const.tile([P, P], F32)
@@ -71,15 +76,14 @@ def tile_mutliheadattention2d_kernel(
         nc.vector.tensor_copy(out=shift_down[:, 0 : P - 1], in_=ident[:, 1:P])
         nc.vector.tensor_copy(out=shift_down[:, P - 1 : P], in_=ident[:, 0:1])
         shift = (shift_up, ident, shift_down)
-
-        zeros = const.tile([P, 2 * ROWS], F32)
+        zeros = const.tile([P, 2 * CHUNK_ROWS], F32)
         nc.vector.memset(zeros[:], 0.0)
 
-        rel3 = const.tile([P, K3], BF16)
-        nc.sync.dma_start(out=rel3[0 : P // 2, :], in_=rel_t)
-        nc.sync.dma_start(out=rel3[P // 2 : P, :], in_=rel_f)
-        rel9 = const.tile([P, K3, K3], F32)
         half = P // 2
+        rel3 = const.tile([P, K3], BF16)
+        nc.sync.dma_start(out=rel3[0:half, :], in_=rel_t)
+        nc.sync.dma_start(out=rel3[half:P, :], in_=rel_f)
+        rel9 = const.tile([P, K3, K3], F32)
         nc.vector.tensor_copy(
             out=rel9[0:half], in_=rel3[0:half, :].unsqueeze(2).to_broadcast([half, K3, K3])
         )
@@ -90,7 +94,7 @@ def tile_mutliheadattention2d_kernel(
         nc.vector.tensor_reduce(
             out=in_group[:], in_=ident[:].rearrange("p (g c) -> p g c", c=CG), axis=AXIS_X, op=ALU.add
         )
-        rel_by_place = const.tile([P, NWIN, GROUPS], F32)
+        rel_by_place = const.tile([P, NWIN, GROUPS], BF16)
         nc.vector.tensor_tensor(
             out=rel_by_place[:],
             in0=rel9[:].rearrange("p i j -> p (i j)").unsqueeze(2).to_broadcast([P, NWIN, GROUPS]),
@@ -117,193 +121,213 @@ def tile_mutliheadattention2d_kernel(
         x_by_word = x[0].rearrange("(p t) h w -> p t (h w)", t=PACK)
 
         raw_of = {}
+        grouped_of = {}
+        q_parts_of = {}
+        k_pix_of = {}
+        qr_ps_of = {}
         codes_of = {}
-        k_of = {}
-        q_of = {}
+        k_rows_of = {}
+        q_pix_of = {}
+        qr_pix_of = {}
+        qk_of = {}
+        folded_of = {}
+        energy_of = {}
+        e_ps_of = {}
+        attn_rows_of = {}
+        attn_pix_of = {}
+        v_pix_of = {}
+        av_of = {}
+        acc_of = {}
 
-        def load_x(b):
-            for k in range(CHUNKS):
-                raw = xin.tile([P, PACK, CHUNK], BF16, name="raw")
-                first = (b * CHUNKS + k) * CHUNK
-                nc.sync.dma_start(out=raw[:], in_=x_by_word[:, :, first : first + CHUNK])
-                raw_of[(b, k)] = raw
+        def load_x(c):
+            raw = three.tile([P, PACK, CHUNK], BF16, name="raw")
+            nc.sync.dma_start(out=raw[:], in_=x_by_word[:, :, c * CHUNK : (c + 1) * CHUNK])
+            raw_of[c] = raw
 
-        def quantise(b):
-            codes = quant.tile([P, ROWS * W], U32, name="codes", align_bytes=64)
-            scales = quant.tile([P, ROWS * W], U8, name="scales", align_bytes=64)
-            for k in range(CHUNKS):
-                raw = raw_of[(b, k)]
-                grouped = grp.tile([P, CHUNK, PACK], BF16, name="grouped", align_bytes=64)
-                nc.scalar.copy(
-                    out=grouped[:].rearrange("p (c i) t -> p c t i", i=4),
-                    in_=raw[:].rearrange("p t (c i) -> p c t i", i=4),
-                )
-                cols = slice(k * CHUNK, (k + 1) * CHUNK)
-                nc.vector.quantize_mx(
-                    out=codes[:, cols].bitcast(FP8X4),
-                    scales=scales[:, cols],
-                    in_=grouped[:].rearrange("p w t -> p (w t)"),
-                )
-            codes_of[b] = (codes, scales)
+        def regroup(c):
+            grouped = two.tile([P, CHUNK, PACK], BF16, name="grouped", align_bytes=64)
+            nc.scalar.copy(
+                out=grouped[:].rearrange("p (c i) t -> p c t i", i=4),
+                in_=raw_of[c][:].rearrange("p t (c i) -> p c t i", i=4),
+            )
+            grouped_of[c] = grouped
 
-        def project_by_channel(b, idx, k):
-            codes, scales = codes_of[b]
-            cols = slice(k * CHUNK, (k + 1) * CHUNK)
+        def quantise(c):
+            grouped = grouped_of[c]
+            codes = quant.tile([P, CHUNK], U32, name="codes", align_bytes=64)
+            scales = quant.tile([P, CHUNK], U8, name="scales", align_bytes=64)
+            nc.vector.quantize_mx(
+                out=codes[:].bitcast(FP8X4),
+                scales=scales[:],
+                in_=grouped[:].rearrange("p w t -> p (w t)"),
+            )
+            codes_of[c] = (codes, scales)
+
+        def project_by_channel(c, idx):
+            codes, scales = codes_of[c]
             acc = ps_mx.tile([P, CHUNK], F32, name="mx", tag="mx")
             nc.tensor.matmul_mx(
                 out=acc[:],
                 lhsT=w_codes[:, idx, :].bitcast(FP8X4),
                 lhsT_scale=w_scales[:, idx, :],
-                rhs=codes[:, cols].bitcast(FP8X4),
-                rhs_scale=scales[:, cols],
+                rhs=codes[:].bitcast(FP8X4),
+                rhs_scale=scales[:],
                 start=True,
                 stop=True,
             )
-            return acc
+            return acc[:].rearrange("p (r w) -> p r w", w=W)
 
-        def project_k(b):
-            k_rows = ring3.tile([P, ROWS, WPAD], F32, name="k_rows")
+        def project_k(c):
+            k_ps = project_by_channel(c, K_IDX)
+            k_rows = four.tile([P, CHUNK_ROWS, WPAD], F32, name="k_rows")
             nc.scalar.copy(
-                out=k_rows[:, :, 0 : WPAD : WPAD - 1],
-                in_=zeros[:].rearrange("p (r e) -> p r e", e=2),
+                out=k_rows[:, :, 0 : WPAD : WPAD - 1], in_=zeros[:].rearrange("p (r e) -> p r e", e=2)
             )
-            for k in range(CHUNKS):
-                acc = project_by_channel(b, K_IDX, k)
-                nc.scalar.copy(
-                    out=k_rows[:, k * CHUNK_ROWS : (k + 1) * CHUNK_ROWS, 1 : W + 1],
-                    in_=acc[:].rearrange("p (r w) -> p r w", w=W),
-                )
-            k_of[b] = k_rows
+            nc.scalar.copy(out=k_rows[:, :, 1 : W + 1], in_=k_ps)
+            k_rows_of[c] = k_rows
 
-        def project_q(b):
-            q_rows = one.tile([P, ROWS, W], F32, name="q_rows")
-            q_pix = one.tile([P, ROWS, C_OUT], F32, name="q_pix")
-            qr_pix = one.tile([P, NWIN, ROWS, GROUPS], F32, name="qr_pix")
-            for k in range(CHUNKS):
-                acc = project_by_channel(b, Q_IDX, k)
-                nc.scalar.copy(
-                    out=q_rows[:, k * CHUNK_ROWS : (k + 1) * CHUNK_ROWS, :],
-                    in_=acc[:].rearrange("p (r w) -> p r w", w=W),
-                )
-            for k in range(CHUNKS):
-                rows = slice(k * CHUNK_ROWS, (k + 1) * CHUNK_ROWS)
-                turned = ps_mx.tile([P, CHUNK], F32, name="turned", tag="mx")
-                for r in range(CHUNK_ROWS):
-                    nc.tensor.transpose(
-                        turned[:, r * P : (r + 1) * P], q_rows[:, k * CHUNK_ROWS + r, :], perm[:]
-                    )
-                nc.scalar.copy(
-                    out=q_pix[:, rows, :], in_=turned[:].rearrange("p (r o) -> p r o", o=C_OUT)
-                )
-                width = NWIN * GROUPS
-                qr = ps_mx.tile([P, CHUNK], F32, name="qr", tag="mx")
-                for r in range(CHUNK_ROWS):
+        def project_q(c):
+            q_ps = project_by_channel(c, Q_IDX)
+            q_rows = two.tile([P, CHUNK_ROWS, W], F32, name="q_rows")
+            nc.scalar.copy(out=q_rows[:], in_=q_ps)
+            q_head = two.tile([P, CHUNK_ROWS, W], BF16, name="q_head")
+            nc.scalar.copy(out=q_head[:], in_=q_ps)
+            q_rest = two.tile([P, CHUNK_ROWS, W], BF16, name="q_rest")
+            nc.gpsimd.tensor_tensor(out=q_rest[:], in0=q_rows[:], in1=q_head[:], op=ALU.subtract)
+            q_parts_of[c] = (q_rows, q_head, q_rest)
+
+        def turn_q(c):
+            q_rows = q_parts_of[c][0]
+            turned = ps_mx.tile([P, CHUNK], F32, name="turned", tag="mx")
+            for r in range(CHUNK_ROWS):
+                nc.tensor.transpose(turned[:, r * P : (r + 1) * P], q_rows[:, r, :], perm[:])
+            q_pix = four.tile([P, CHUNK_ROWS, C_OUT], F32, name="q_pix")
+            nc.scalar.copy(out=q_pix[:], in_=turned[:].rearrange("p (r o) -> p r o", o=C_OUT))
+            q_pix_of[c] = q_pix
+
+        def q_dot_rel(c, first_row):
+            q_head, q_rest = q_parts_of[c][1:]
+            if first_row == 0:
+                qr_ps_of[0] = ps_mx.tile([P, CHUNK], F32, name="qr", tag="mx")
+            qr = qr_ps_of[0]
+            for r in range(first_row, first_row + CHUNK_ROWS // 2):
+                for part, q_part in enumerate((q_head, q_rest)):
                     nc.tensor.matmul(
-                        out=qr[:, r * width : (r + 1) * width],
-                        lhsT=q_rows[:, k * CHUNK_ROWS + r, :],
+                        out=qr[:, r * QR : (r + 1) * QR],
+                        lhsT=q_part[:, r, :],
                         rhs=rel_by_place[:].rearrange("p n g -> p (n g)"),
-                        start=True,
-                        stop=True,
+                        start=(part == 0),
+                        stop=(part == 1),
                     )
-                nc.scalar.copy(
-                    out=qr_pix[:, :, rows, :].rearrange("p n r g -> p r n g"),
-                    in_=qr[:, 0 : CHUNK_ROWS * width].rearrange(
-                        "p (r n g) -> p r n g", n=NWIN, g=GROUPS
-                    ),
-                )
-            q_of[b] = (q_pix, qr_pix)
+            if first_row == 0:
+                return
+            b = c * CHUNK_ROWS // ROWS
+            first = c * CHUNK_ROWS % ROWS
+            if first == 0:
+                qr_pix_of[b] = two.tile([P, NWIN, ROWS, GROUPS], F32, name="qr_pix")
+            nc.scalar.copy(
+                out=qr_pix_of[b][:, :, first : first + CHUNK_ROWS, :].rearrange("p n r g -> p r n g"),
+                in_=qr[:, 0 : CHUNK_ROWS * QR].rearrange("p (r n g) -> p r n g", n=NWIN, g=GROUPS),
+            )
 
-        qk = one.tile([P, NWIN, CG, ROWS, GROUPS], F32, name="qk")
+        def turn_k(s):
+            k_row = k_rows_of[s // CHUNK_ROWS][:, s % CHUNK_ROWS, :]
+            k_pix = ps_kt.tile([P, K3, C_OUT], F32, name="k_pix")
+            for j in range(K3):
+                nc.tensor.transpose(k_pix[:, j, :], k_row[:, j : j + W], perm[:])
+            k_pix_of[s] = k_pix
 
-        def energy_products(b):
-            q_pix = q_of[b][0]
-            if b == 0:
-                nc.gpsimd.memset(qk[:, 0:K3, :, 0, :], 0.0)
-            if b == BLOCKS - 1:
-                nc.gpsimd.memset(qk[:, NWIN - K3 : NWIN, :, ROWS - 1, :], 0.0)
-            for s in range(-1, ROWS + 1):
-                src = b * ROWS + s
-                if 0 <= src < H:
-                    k_row = k_of[src // ROWS][:, src % ROWS, :]
-                    k_pix = ps_kt.tile([P, K3, C_OUT], F32, name="k_pix")
-                    for j in range(K3):
-                        nc.tensor.transpose(k_pix[:, j, :], k_row[:, j : j + W], perm[:])
-                    for i in range(K3):
-                        t = s - i + 1
-                        if t < 0 or t >= ROWS:
-                            continue
+        def energy_step(s):
+            if s + 1 < H:
+                qk_of[s + 1] = four.tile([P, NWIN, C_OUT], F32, name="qk")
+            if s == -1:
+                nc.gpsimd.memset(qk_of[0][:, 0:K3, :], 0.0)
+            if s == H - 2:
+                nc.gpsimd.memset(qk_of[H - 1][:, NWIN - K3 : NWIN, :], 0.0)
+            if 0 <= s < H:
+                k_pix = k_pix_of[s]
+                for i in range(K3):
+                    t = s - i + 1
+                    if 0 <= t < H:
                         nc.vector.tensor_tensor(
-                            out=qk[:, K3 * i : K3 * i + K3, :, t, :],
-                            in0=k_pix[:].rearrange("p j (c g) -> p j c g", g=GROUPS),
-                            in1=q_pix[:, t, :]
-                            .rearrange("p (c g) -> p c g", g=GROUPS)
+                            out=qk_of[t][:, K3 * i : K3 * i + K3, :],
+                            in0=k_pix[:],
+                            in1=q_pix_of[t // CHUNK_ROWS][:, t % CHUNK_ROWS, :]
                             .unsqueeze(1)
-                            .to_broadcast([P, K3, CG, GROUPS]),
+                            .to_broadcast([P, K3, C_OUT]),
                             op=ALU.mult,
                         )
-                done = s - 1
-                if done >= 0:
-                    nc.gpsimd.tensor_tensor(
-                        out=qk[:, :, 0:CG_HALF, done, :],
-                        in0=qk[:, :, 0:CG_HALF, done, :],
-                        in1=qk[:, :, CG_HALF:CG, done, :],
-                        op=ALU.add,
-                    )
+            t = s - 1
+            if 0 <= t < H:
+                b = t // ROWS
+                if t % ROWS == 0:
+                    folded_of[b] = two.tile([P, NWIN, CG_HALF, ROWS, GROUPS], F32, name="folded")
+                by_plane = qk_of[t][:].rearrange("p n (c g) -> p n c g", g=GROUPS)
+                nc.gpsimd.tensor_tensor(
+                    out=folded_of[b][:, :, :, t % ROWS, :],
+                    in0=by_plane[:, :, 0:CG_HALF, :],
+                    in1=by_plane[:, :, CG_HALF:CG, :],
+                    op=ALU.add,
+                )
 
-        energy_of = {}
-
-        def energy_sums(b, i):
-            if i == 0:
+        def energy_sums(b, n):
+            i, j = n // K3, n % K3
+            if n == 0:
                 energy_of[b] = one.tile([P, NWIN, W], F32, name="energy")
-            qr_pix = q_of[b][1]
-            e_ps = ps_ea.tile([P, K3, W], F32, name="e_ps", tag="ea")
-            for j in range(K3):
-                n = K3 * i + j
-                for c in range(CG_HALF):
-                    nc.tensor.matmul(
-                        out=e_ps[:, j, :],
-                        lhsT=qk[:, n, c, :, :].rearrange("p r g -> p (r g)"),
-                        rhs=ident[:],
-                        is_transpose=True,
-                        start=(c == 0),
-                        stop=False,
-                    )
+            if j == 0:
+                e_ps_of[0] = ps_ea.tile([P, K3, W], F32, name="e_ps", tag="ea")
+            e_ps = e_ps_of[0]
+            for c in range(CG_HALF):
                 nc.tensor.matmul(
                     out=e_ps[:, j, :],
-                    lhsT=qr_pix[:, n, :, :].rearrange("p r g -> p (r g)"),
+                    lhsT=folded_of[b][:, n, c, :, :].rearrange("p r g -> p (r g)"),
                     rhs=ident[:],
                     is_transpose=True,
-                    start=False,
-                    stop=True,
+                    start=(c == 0),
+                    stop=False,
                 )
-            nc.scalar.copy(out=energy_of[b][:, K3 * i : K3 * i + K3, :], in_=e_ps[:])
+            nc.tensor.matmul(
+                out=e_ps[:, j, :],
+                lhsT=qr_pix_of[b][:, n, :, :].rearrange("p r g -> p (r g)"),
+                rhs=ident[:],
+                is_transpose=True,
+                start=False,
+                stop=True,
+            )
+            if j == K3 - 1:
+                nc.scalar.copy(out=energy_of[b][:, K3 * i : K3 * i + K3, :], in_=e_ps[:])
 
-        attn_pix_of = {}
-
-        def softmax(b):
+        def softmax_top(b):
             energy = energy_of[b]
-            by_pixel = energy[:].rearrange("p n w -> p w n")
             top = one.tile([P, W], F32, name="top")
-            nc.vector.tensor_reduce(out=top[:], in_=by_pixel, axis=AXIS_X, op=ALU.max)
-            nc.vector.tensor_tensor(
+            nc.vector.tensor_reduce(
+                out=top[:], in_=energy[:].rearrange("p n w -> p w n"), axis=AXIS_X, op=ALU.max
+            )
+            nc.gpsimd.tensor_tensor(
                 out=energy[:],
                 in0=energy[:],
                 in1=top[:].unsqueeze(1).to_broadcast([P, NWIN, W]),
                 op=ALU.subtract,
             )
             nc.scalar.activation(out=energy[:], in_=energy[:], func=EXP)
+
+        def softmax_norm(b):
+            energy = energy_of[b]
             total = one.tile([P, W], F32, name="total")
-            nc.vector.tensor_reduce(out=total[:], in_=by_pixel, axis=AXIS_X, op=ALU.add)
+            nc.vector.tensor_reduce(
+                out=total[:], in_=energy[:].rearrange("p n w -> p w n"), axis=AXIS_X, op=ALU.add
+            )
             inverse = one.tile([P, W], F32, name="inverse")
             nc.vector.reciprocal(out=inverse[:], in_=total[:])
             attn_rows = one.tile([P, NWIN, WPAD], F32, name="attn_rows")
-            nc.vector.memset(attn_rows[:, :, 0 : WPAD : WPAD - 1], 0.0)
-            nc.vector.tensor_tensor(
+            nc.gpsimd.memset(attn_rows[:, :, 0 : WPAD : WPAD - 1], 0.0)
+            nc.gpsimd.tensor_tensor(
                 out=attn_rows[:, :, 1 : W + 1],
                 in0=energy[:],
                 in1=inverse[:].unsqueeze(1).to_broadcast([P, NWIN, W]),
                 op=ALU.mult,
             )
+            attn_rows_of[b] = attn_rows
             attn_store = one.tile([P, W, NWIN], F32, name="attn_store")
             nc.scalar.copy(
                 out=attn_store[:], in_=attn_rows[:, :, 1 : W + 1].rearrange("p n w -> p w n")
@@ -312,113 +336,115 @@ def tile_mutliheadattention2d_kernel(
                 out=attn[0, :, b * ROWS : (b + 1) * ROWS, :, :].rearrange("g h w n -> h g (w n)"),
                 in_=attn_store[:].rearrange("p w n -> p (w n)"),
             )
-            attn_pix = one.tile([P, NWIN, P], F32, name="attn_pix")
-            for i in range(K3):
-                a_ps = ps_ea.tile([P, K3, P], F32, name="a_ps", tag="ea")
-                for j in range(K3):
-                    nc.tensor.transpose(
-                        a_ps[:, j, :], attn_rows[:, K3 * i + j, 2 - j : 2 - j + W], ident[:]
-                    )
-                nc.scalar.copy(out=attn_pix[:, K3 * i : K3 * i + K3, :], in_=a_ps[:])
-            attn_pix_of[b] = attn_pix
 
-        acc_of = {}
+        def turn_weights(b, i):
+            if i == 0:
+                attn_pix_of[b] = two.tile([P, NWIN, P], F32, name="attn_pix")
+            a_ps = ps_ea.tile([P, K3, P], F32, name="a_ps", tag="ea")
+            for j in range(K3):
+                nc.tensor.transpose(
+                    a_ps[:, j, :], attn_rows_of[b][:, K3 * i + j, 2 - j : 2 - j + W], ident[:]
+                )
+            nc.scalar.copy(out=attn_pix_of[b][:, K3 * i : K3 * i + K3, :], in_=a_ps[:])
 
-        av_of = {}
-        v_of = {}
+        def project_v(c):
+            codes, scales = codes_of[c]
+            v_pix = ps_v.tile([P, CHUNK_ROWS, C_OUT], F32, name="v_pix")
+            for r in range(CHUNK_ROWS):
+                nc.tensor.matmul_mx(
+                    out=v_pix[:, r, :],
+                    lhsT=codes[:, r * W : (r + 1) * W].bitcast(FP8X4),
+                    lhsT_scale=scales[:, r * W : (r + 1) * W],
+                    rhs=w_codes[:, V_IDX, :].bitcast(FP8X4),
+                    rhs_scale=w_scales[:, V_IDX, :],
+                    start=True,
+                    stop=True,
+                )
+            v_pix_of[c] = v_pix
 
-        def weighted_sum_step(b, s):
-            attn_pix = attn_pix_of[b]
-            codes_row = b * ROWS + s
-            if (s + 1) % V_ROWS == 0:
-                v_of[0] = ps_mx.tile([P, CHUNK], F32, name="v_pix", tag="mx")
-                for r in range(V_ROWS):
-                    src = codes_row + r
-                    if src < 0 or src >= H:
-                        continue
-                    codes, scales = codes_of[src // ROWS]
-                    cols = slice((src % ROWS) * W, (src % ROWS + 1) * W)
-                    nc.tensor.matmul_mx(
-                        out=v_of[0][:, r * C_OUT : (r + 1) * C_OUT],
-                        lhsT=codes[:, cols].bitcast(FP8X4),
-                        lhsT_scale=scales[:, cols],
-                        rhs=w_codes[:, V_IDX, :].bitcast(FP8X4),
-                        rhs_scale=w_scales[:, V_IDX, :],
-                        start=True,
-                        stop=True,
-                    )
-            if s + 1 < ROWS:
-                av_of[s + 1] = ring4.tile([P, NWIN, C_OUT], F32, name="av")
-            if 0 <= codes_row < H:
-                r = (s + 1) % V_ROWS
+        def weighted_products(s):
+            if s == 0:
+                av_of[0] = five.tile([P, NWIN, C_OUT], F32, name="av")
+            if s + 1 < H:
+                av_of[s + 1] = five.tile([P, NWIN, C_OUT], F32, name="av")
+            if s < H:
                 for i in range(K3):
                     t = s - i + 1
-                    if t < 0 or t >= ROWS:
-                        continue
-                    nc.vector.tensor_tensor(
-                        out=av_of[t][:, K3 * i : K3 * i + K3, :].rearrange(
-                            "p j (g c) -> p j g c", c=CG
-                        ),
-                        in0=v_of[0][:, r * C_OUT : (r + 1) * C_OUT]
-                        .rearrange("p (g c) -> p g c", c=CG)
-                        .unsqueeze(1)
-                        .to_broadcast([P, K3, GROUPS, CG]),
-                        in1=attn_pix[:, K3 * i : K3 * i + K3, t * GROUPS : (t + 1) * GROUPS]
-                        .unsqueeze(3)
-                        .to_broadcast([P, K3, GROUPS, CG]),
-                        op=ALU.mult,
-                    )
-            t = s - 1
-            if t < 0:
-                return
-            row = b * ROWS + t
-            av = av_of[t]
-            window_rows = [i for i in range(K3) if 0 <= row + i - 1 < H]
-            base = K3 * window_rows[0]
-            for i in window_rows[1:]:
-                nc.gpsimd.tensor_tensor(
-                    out=av[:, base : base + K3, :],
-                    in0=av[:, base : base + K3, :],
-                    in1=av[:, K3 * i : K3 * i + K3, :],
-                    op=ALU.add,
-                )
-            if t % ACC_ROWS == 0:
-                acc_of[0] = ps_acc.tile([P, ACC_ROWS, W], F32, name="acc")
+                    if 0 <= t < H:
+                        first = (t % ROWS) * GROUPS
+                        nc.vector.tensor_tensor(
+                            out=av_of[t][:, K3 * i : K3 * i + K3, :].rearrange(
+                                "p j (g c) -> p j g c", c=CG
+                            ),
+                            in0=v_pix_of[s // CHUNK_ROWS][:, s % CHUNK_ROWS, :]
+                            .rearrange("p (g c) -> p g c", c=CG)
+                            .unsqueeze(1)
+                            .to_broadcast([P, K3, GROUPS, CG]),
+                            in1=attn_pix_of[t // ROWS][:, K3 * i : K3 * i + K3, first : first + GROUPS]
+                            .unsqueeze(3)
+                            .to_broadcast([P, K3, GROUPS, CG]),
+                            op=ALU.mult,
+                        )
+
+        def weighted_sums(t):
+            places = [K3 * i + j for i in range(K3) if 0 <= t + i - 1 < H for j in range(K3)]
+            a = t % CHUNK_ROWS
+            if a == 0:
+                acc_of[0] = ps_acc.tile([P, CHUNK_ROWS, W], F32, name="acc")
             acc = acc_of[0]
-            a = t % ACC_ROWS
-            for j in range(K3):
+            for n in places:
                 nc.tensor.matmul(
                     out=acc[:, a, :],
-                    lhsT=av[:, base + j, :],
-                    rhs=shift[j][:],
+                    lhsT=av_of[t][:, n, :],
+                    rhs=shift[n % K3][:],
                     is_transpose=True,
-                    start=(j == 0),
-                    stop=(j == K3 - 1),
+                    start=(n == places[0]),
+                    stop=(n == places[-1]),
                 )
-            if a == ACC_ROWS - 1:
-                out_rows = two.tile([P, STORE_ROWS, W], F32, name="out_rows")
+            if a == CHUNK_ROWS - 1:
+                out_rows = two.tile([P, CHUNK_ROWS, W], F32, name="out_rows")
                 nc.scalar.copy(out=out_rows[:], in_=acc[:])
-                nc.sync.dma_start(out=out[0, :, row - STORE_ROWS + 1 : row + 1, :], in_=out_rows[:])
+                nc.sync.dma_start(out=out[0, :, t - CHUNK_ROWS + 1 : t + 1, :], in_=out_rows[:])
 
-        load_x(0)
+        for c in range(3):
+            load_x(c)
+        regroup(0)
         quantise(0)
-        load_x(1)
-        project_k(0)
-        project_q(0)
-        for b in range(BLOCKS):
-            if b + 1 < BLOCKS:
-                quantise(b + 1)
-                if b + 2 < BLOCKS:
-                    load_x(b + 2)
-                project_k(b + 1)
-            energy_products(b)
-            for step in range(ROWS + 2):
-                if b > 0:
-                    weighted_sum_step(b - 1, step - 1)
-                if step < K3:
-                    energy_sums(b, step)
-            softmax(b)
-            if b + 1 < BLOCKS:
-                project_q(b + 1)
-        for step in range(ROWS + 2):
-            weighted_sum_step(BLOCKS - 1, step - 1)
+        for step in range(-LEAD, H + LAG + 3):
+            if 0 <= step + 1 < H:
+                turn_k(step + 1)
+            if -1 <= step <= H:
+                energy_step(step)
+            source = step - LAG
+            if 0 <= source < H:
+                weighted_products(source)
+            if 0 <= source - 2 < H:
+                weighted_sums(source - 2)
+            if 0 <= source + 1 < H and (source + 1) % CHUNK_ROWS == 0:
+                project_v((source + 1) // CHUNK_ROWS)
+            for block in range(BLOCKS):
+                since = step - block * ROWS
+                if SUMS_AT <= since < SUMS_AT + NWIN:
+                    energy_sums(block, since - SUMS_AT)
+                if since == TOP_AT:
+                    softmax_top(block)
+                if since == NORM_AT:
+                    softmax_norm(block)
+                if TURN_AT <= since < TURN_AT + K3:
+                    turn_weights(block, since - TURN_AT)
+            c, stage = divmod(step + LEAD, CHUNK_ROWS)
+            if stage == 0:
+                if c < CHUNKS:
+                    project_k(c)
+                    project_q(c)
+                if c + 3 < CHUNKS:
+                    load_x(c + 3)
+                if c + 1 < CHUNKS:
+                    regroup(c + 1)
+            if stage == 1:
+                if c < CHUNKS:
+                    turn_q(c)
+                if c + 1 < CHUNKS:
+                    quantise(c + 1)
+            if stage >= 2 and c < CHUNKS:
+                q_dot_rel(c, (stage - 2) * (CHUNK_ROWS // 2))

@@ -15,6 +15,7 @@ EXP = mybir.ActivationFunctionType.Exp
 
 P = 128
 PACK = 4
+RUN = 4
 C_IN = P * PACK
 C_OUT = 128
 H = 128
@@ -25,23 +26,36 @@ CG_HALF = CG // 2
 K3 = 3
 NWIN = K3 * K3
 ROWS = P // GROUPS
-BLOCKS = H // ROWS
+BANDS = H // ROWS
 CHUNK_ROWS = 4
 CHUNK = CHUNK_ROWS * W
 CHUNKS = H // CHUNK_ROWS
-WPAD = W + 2
-QR = NWIN * GROUPS
+PADS = 2
+WPAD = W + PADS
+QUADRANTS = 4
+LIVE = 4
 
-LEAD = 6
-SUMS_AT = ROWS + 2
+SLACK = 2
+LEAD = CHUNK_ROWS + SLACK
+SUMS_AT = ROWS + SLACK
 TOP_AT = SUMS_AT + NWIN
-NORM_AT = TOP_AT + 2
-TURN_AT = NORM_AT + 2
-LAG = TURN_AT + K3 + 2
+NORM_AT = TOP_AT + SLACK
+TURN_AT = NORM_AT + SLACK
+LAG = TURN_AT + K3 + SLACK
+LAST = H + LAG + 1
 
-FLOPS = 2 * C_IN * 3 * C_OUT * H * W + 2 * 2 * NWIN * C_OUT * H * W
+SINGLE = 1
+DOUBLE = 2
+RAW_BUFS = 3
+CHUNK_BUFS = 4
+QK_BUFS = 4
+AV_BUFS = 5
+CODES_BUFS = (LAG + LEAD + CHUNK_ROWS) // CHUNK_ROWS + 2
 
+PROJECTIONS = 3
 Q_IDX, K_IDX, V_IDX = 0, 1, 2
+
+FLOPS = 2 * C_IN * PROJECTIONS * C_OUT * H * W + 2 * 2 * NWIN * C_OUT * H * W
 
 
 def tile_mutliheadattention2d_kernel(
@@ -49,52 +63,47 @@ def tile_mutliheadattention2d_kernel(
 ):
     nc = tc.nc
     with ExitStack() as ctx:
-        const = ctx.enter_context(tc.tile_pool(name="const", bufs=1))
-        one = ctx.enter_context(tc.tile_pool(name="one", bufs=1))
-        two = ctx.enter_context(tc.tile_pool(name="two", bufs=2))
-        three = ctx.enter_context(tc.tile_pool(name="three", bufs=3))
-        four = ctx.enter_context(tc.tile_pool(name="four", bufs=4))
-        five = ctx.enter_context(tc.tile_pool(name="five", bufs=5))
-        quant = ctx.enter_context(tc.tile_pool(name="quant", bufs=(LAG + LEAD + 3 * CHUNK_ROWS) // CHUNK_ROWS))
-        ps_mx = ctx.enter_context(tc.psum_pool(name="ps_mx", bufs=2))
+        depths = sorted({SINGLE, DOUBLE, RAW_BUFS, CHUNK_BUFS, QK_BUFS, AV_BUFS, CODES_BUFS})
+        sbuf = {n: ctx.enter_context(tc.tile_pool(name="sbuf%d" % n, bufs=n)) for n in depths}
+        ps_proj = ctx.enter_context(tc.psum_pool(name="ps_proj", bufs=2))
         ps_v = ctx.enter_context(tc.psum_pool(name="ps_v", bufs=2))
-        ps_kt = ctx.enter_context(tc.psum_pool(name="ps_kt", bufs=2))
-        ps_ea = ctx.enter_context(tc.psum_pool(name="ps_ea", bufs=1))
-        ps_acc = ctx.enter_context(tc.psum_pool(name="ps_acc", bufs=1))
+        ps_k = ctx.enter_context(tc.psum_pool(name="ps_k", bufs=2))
+        ps_soft = ctx.enter_context(tc.psum_pool(name="ps_soft", bufs=1))
+        ps_out = ctx.enter_context(tc.psum_pool(name="ps_out", bufs=1))
 
-        ident = const.tile([P, P], F32)
+        ident = sbuf[SINGLE].tile([P, P], F32, name="ident")
         make_identity(nc, ident[:])
-        perm = const.tile([P, P], F32)
+        by_plane = sbuf[SINGLE].tile([P, P], F32, name="by_plane")
         nc.vector.tensor_copy(
-            out=perm[:].rearrange("p (c g) -> p c g", g=GROUPS),
+            out=by_plane[:].rearrange("p (c g) -> p c g", g=GROUPS),
             in_=ident[:].rearrange("p (g c) -> p c g", c=CG),
         )
-        shift_up = const.tile([P, P], F32)
-        nc.vector.tensor_copy(out=shift_up[:, 1:P], in_=ident[:, 0 : P - 1])
-        nc.vector.tensor_copy(out=shift_up[:, 0:1], in_=ident[:, P - 1 : P])
-        shift_down = const.tile([P, P], F32)
-        nc.vector.tensor_copy(out=shift_down[:, 0 : P - 1], in_=ident[:, 1:P])
-        nc.vector.tensor_copy(out=shift_down[:, P - 1 : P], in_=ident[:, 0:1])
-        shift = (shift_up, ident, shift_down)
-        zeros = const.tile([P, 2 * CHUNK_ROWS], F32)
+        rotate_up = sbuf[SINGLE].tile([P, P], F32, name="rotate_up")
+        nc.vector.tensor_copy(out=rotate_up[:, 1:P], in_=ident[:, 0 : P - 1])
+        nc.vector.tensor_copy(out=rotate_up[:, 0:1], in_=ident[:, P - 1 : P])
+        rotate_down = sbuf[SINGLE].tile([P, P], F32, name="rotate_down")
+        nc.vector.tensor_copy(out=rotate_down[:, 0 : P - 1], in_=ident[:, 1:P])
+        nc.vector.tensor_copy(out=rotate_down[:, P - 1 : P], in_=ident[:, 0:1])
+        rotate = (rotate_up, ident, rotate_down)
+        zeros = sbuf[SINGLE].tile([P, CHUNK_ROWS, PADS], F32, name="zeros")
         nc.vector.memset(zeros[:], 0.0)
 
-        half = P // 2
-        rel3 = const.tile([P, K3], BF16)
+        half = C_OUT // 2
+        rel3 = sbuf[SINGLE].tile([P, K3], BF16, name="rel3")
         nc.sync.dma_start(out=rel3[0:half, :], in_=rel_t)
         nc.sync.dma_start(out=rel3[half:P, :], in_=rel_f)
-        rel9 = const.tile([P, K3, K3], F32)
+        rel9 = sbuf[SINGLE].tile([P, K3, K3], F32, name="rel9")
         nc.vector.tensor_copy(
             out=rel9[0:half], in_=rel3[0:half, :].unsqueeze(2).to_broadcast([half, K3, K3])
         )
         nc.vector.tensor_copy(
             out=rel9[half:P], in_=rel3[half:P, :].unsqueeze(1).to_broadcast([half, K3, K3])
         )
-        in_group = const.tile([P, GROUPS], F32)
+        in_group = sbuf[SINGLE].tile([P, GROUPS], F32, name="in_group")
         nc.vector.tensor_reduce(
             out=in_group[:], in_=ident[:].rearrange("p (g c) -> p g c", c=CG), axis=AXIS_X, op=ALU.add
         )
-        rel_by_place = const.tile([P, NWIN, GROUPS], BF16)
+        rel_by_place = sbuf[SINGLE].tile([P, NWIN, GROUPS], F32, name="rel_by_place")
         nc.vector.tensor_tensor(
             out=rel_by_place[:],
             in0=rel9[:].rearrange("p i j -> p (i j)").unsqueeze(2).to_broadcast([P, NWIN, GROUPS]),
@@ -102,72 +111,71 @@ def tile_mutliheadattention2d_kernel(
             op=ALU.mult,
         )
 
-        w_codes = const.tile([P, 3, C_OUT], U32, align_bytes=64)
-        w_scales = const.tile([P, 3, C_OUT], U8, align_bytes=64)
+        w_codes = sbuf[SINGLE].tile([P, PROJECTIONS, C_OUT], U32, name="w_codes", align_bytes=64)
+        w_scales = sbuf[SINGLE].tile([P, PROJECTIONS, C_OUT], U8, name="w_scales", align_bytes=64)
         nc.vector.memset(w_scales[:].rearrange("p a n -> p (a n)").bitcast(I32), 0)
         for idx, (words, scales) in enumerate(
             ((wq_words, wq_scales), (wk_words, wk_scales), (wv_words, wv_scales))
         ):
             nc.sync.dma_start(
                 out=w_codes[:, idx, :].bitcast(I32),
-                in_=words[0].rearrange("p n t -> p (n t)").bitcast(I32),
+                in_=words[0].rearrange("p n e -> p (n e)").bitcast(I32),
             )
-            for quad in range(4):
+            for quad in range(QUADRANTS):
+                first_partition = quad * (P // QUADRANTS)
                 nc.sync.dma_start(
-                    out=w_scales[32 * quad : 32 * quad + 4, idx, :].bitcast(I32),
-                    in_=scales[0, 4 * quad : 4 * quad + 4, :].bitcast(I32),
+                    out=w_scales[first_partition : first_partition + LIVE, idx, :].bitcast(I32),
+                    in_=scales[0, quad * LIVE : (quad + 1) * LIVE, :].bitcast(I32),
                 )
 
-        x_by_word = x[0].rearrange("(p t) h w -> p t (h w)", t=PACK)
+        x_by_word = x[0].rearrange("(p e) h w -> p e (h w)", e=PACK)
 
         raw_of = {}
         grouped_of = {}
-        q_parts_of = {}
-        k_pix_of = {}
-        qr_ps_of = {}
         codes_of = {}
         k_rows_of = {}
+        q_rows_of = {}
         q_pix_of = {}
         qr_pix_of = {}
+        k_pix_of = {}
         qk_of = {}
         folded_of = {}
-        energy_of = {}
         e_ps_of = {}
+        energy_of = {}
         attn_rows_of = {}
         attn_pix_of = {}
         v_pix_of = {}
         av_of = {}
-        acc_of = {}
+        out_ps_of = {}
 
         def load_x(c):
-            raw = three.tile([P, PACK, CHUNK], BF16, name="raw")
+            raw = sbuf[RAW_BUFS].tile([P, PACK, CHUNK], BF16, name="raw")
             nc.sync.dma_start(out=raw[:], in_=x_by_word[:, :, c * CHUNK : (c + 1) * CHUNK])
             raw_of[c] = raw
 
         def regroup(c):
-            grouped = two.tile([P, CHUNK, PACK], BF16, name="grouped", align_bytes=64)
+            grouped = sbuf[DOUBLE].tile([P, CHUNK, PACK], BF16, name="grouped", align_bytes=64)
             nc.scalar.copy(
-                out=grouped[:].rearrange("p (c i) t -> p c t i", i=4),
-                in_=raw_of[c][:].rearrange("p t (c i) -> p c t i", i=4),
+                out=grouped[:].rearrange("p (u i) e -> p u e i", i=RUN),
+                in_=raw_of[c][:].rearrange("p e (u i) -> p u e i", i=RUN),
             )
             grouped_of[c] = grouped
 
         def quantise(c):
-            grouped = grouped_of[c]
-            codes = quant.tile([P, CHUNK], U32, name="codes", align_bytes=64)
-            scales = quant.tile([P, CHUNK], U8, name="scales", align_bytes=64)
+            codes = sbuf[CODES_BUFS].tile([P, CHUNK], U32, name="codes", align_bytes=64)
+            scales = sbuf[CODES_BUFS].tile([P, CHUNK], U8, name="scales", align_bytes=64)
             nc.vector.quantize_mx(
                 out=codes[:].bitcast(FP8X4),
                 scales=scales[:],
-                in_=grouped[:].rearrange("p w t -> p (w t)"),
+                in_=grouped_of[c][:].rearrange("p w e -> p (w e)"),
             )
             codes_of[c] = (codes, scales)
 
         def project_by_channel(c, idx):
             codes, scales = codes_of[c]
-            acc = ps_mx.tile([P, CHUNK], F32, name="mx", tag="mx")
+            proj = ps_proj.tile([P, CHUNK], F32, name="proj", tag="proj")
             nc.tensor.matmul_mx(
-                out=acc[:],
+                out=proj[:],
                 lhsT=w_codes[:, idx, :].bitcast(FP8X4),
                 lhsT_scale=w_scales[:, idx, :],
                 rhs=codes[:].bitcast(FP8X4),
@@ -175,115 +183,101 @@ def tile_mutliheadattention2d_kernel(
                 start=True,
                 stop=True,
             )
-            return acc[:].rearrange("p (r w) -> p r w", w=W)
+            return proj[:].rearrange("p (r w) -> p r w", w=W)
 
         def project_k(c):
             k_ps = project_by_channel(c, K_IDX)
-            k_rows = four.tile([P, CHUNK_ROWS, WPAD], F32, name="k_rows")
-            nc.scalar.copy(
-                out=k_rows[:, :, 0 : WPAD : WPAD - 1], in_=zeros[:].rearrange("p (r e) -> p r e", e=2)
-            )
+            k_rows = sbuf[CHUNK_BUFS].tile([P, CHUNK_ROWS, WPAD], F32, name="k_rows")
+            nc.scalar.copy(out=k_rows[:, :, 0 : WPAD : WPAD - 1], in_=zeros[:])
             nc.scalar.copy(out=k_rows[:, :, 1 : W + 1], in_=k_ps)
             k_rows_of[c] = k_rows
 
         def project_q(c):
-            q_ps = project_by_channel(c, Q_IDX)
-            q_rows = two.tile([P, CHUNK_ROWS, W], F32, name="q_rows")
-            nc.scalar.copy(out=q_rows[:], in_=q_ps)
-            q_head = two.tile([P, CHUNK_ROWS, W], BF16, name="q_head")
-            nc.scalar.copy(out=q_head[:], in_=q_ps)
-            q_rest = two.tile([P, CHUNK_ROWS, W], BF16, name="q_rest")
-            nc.gpsimd.tensor_tensor(out=q_rest[:], in0=q_rows[:], in1=q_head[:], op=ALU.subtract)
-            q_parts_of[c] = (q_rows, q_head, q_rest)
+            q_rows = sbuf[DOUBLE].tile([P, CHUNK_ROWS, W], F32, name="q_rows")
+            nc.scalar.copy(out=q_rows[:], in_=project_by_channel(c, Q_IDX))
+            q_rows_of[c] = q_rows
 
         def turn_q(c):
-            q_rows = q_parts_of[c][0]
-            turned = ps_mx.tile([P, CHUNK], F32, name="turned", tag="mx")
+            turned = ps_proj.tile([P, CHUNK_ROWS, C_OUT], F32, name="turned", tag="proj")
             for r in range(CHUNK_ROWS):
-                nc.tensor.transpose(turned[:, r * P : (r + 1) * P], q_rows[:, r, :], perm[:])
-            q_pix = four.tile([P, CHUNK_ROWS, C_OUT], F32, name="q_pix")
-            nc.scalar.copy(out=q_pix[:], in_=turned[:].rearrange("p (r o) -> p r o", o=C_OUT))
+                nc.tensor.transpose(turned[:, r, :], q_rows_of[c][:, r, :], by_plane[:])
+            q_pix = sbuf[CHUNK_BUFS].tile([P, CHUNK_ROWS, C_OUT], F32, name="q_pix")
+            nc.scalar.copy(out=q_pix[:], in_=turned[:])
             q_pix_of[c] = q_pix
 
-        def q_dot_rel(c, first_row):
-            q_head, q_rest = q_parts_of[c][1:]
+        def q_dot_rel(c):
+            qr = ps_proj.tile([P, CHUNK_ROWS, NWIN, GROUPS], F32, name="qr", tag="proj")
+            for r in range(CHUNK_ROWS):
+                nc.tensor.matmul(
+                    out=qr[:, r, :, :].rearrange("p n g -> p (n g)"),
+                    lhsT=q_rows_of[c][:, r, :],
+                    rhs=rel_by_place[:].rearrange("p n g -> p (n g)"),
+                    start=True,
+                    stop=True,
+                )
+            b, first_row = divmod(c * CHUNK_ROWS, ROWS)
             if first_row == 0:
-                qr_ps_of[0] = ps_mx.tile([P, CHUNK], F32, name="qr", tag="mx")
-            qr = qr_ps_of[0]
-            for r in range(first_row, first_row + CHUNK_ROWS // 2):
-                for part, q_part in enumerate((q_head, q_rest)):
-                    nc.tensor.matmul(
-                        out=qr[:, r * QR : (r + 1) * QR],
-                        lhsT=q_part[:, r, :],
-                        rhs=rel_by_place[:].rearrange("p n g -> p (n g)"),
-                        start=(part == 0),
-                        stop=(part == 1),
-                    )
-            if first_row == 0:
-                return
-            b = c * CHUNK_ROWS // ROWS
-            first = c * CHUNK_ROWS % ROWS
-            if first == 0:
-                qr_pix_of[b] = two.tile([P, NWIN, ROWS, GROUPS], F32, name="qr_pix")
+                qr_pix_of[b] = sbuf[DOUBLE].tile([P, NWIN, ROWS, GROUPS], F32, name="qr_pix")
             nc.scalar.copy(
-                out=qr_pix_of[b][:, :, first : first + CHUNK_ROWS, :].rearrange("p n r g -> p r n g"),
-                in_=qr[:, 0 : CHUNK_ROWS * QR].rearrange("p (r n g) -> p r n g", n=NWIN, g=GROUPS),
+                out=qr_pix_of[b][:, :, first_row : first_row + CHUNK_ROWS, :].rearrange(
+                    "p n r g -> p r n g"
+                ),
+                in_=qr[:],
             )
 
         def turn_k(s):
             k_row = k_rows_of[s // CHUNK_ROWS][:, s % CHUNK_ROWS, :]
-            k_pix = ps_kt.tile([P, K3, C_OUT], F32, name="k_pix")
+            k_pix = ps_k.tile([P, K3, C_OUT], F32, name="k_pix")
             for j in range(K3):
-                nc.tensor.transpose(k_pix[:, j, :], k_row[:, j : j + W], perm[:])
+                nc.tensor.transpose(k_pix[:, j, :], k_row[:, j : j + W], by_plane[:])
             k_pix_of[s] = k_pix
 
-        def energy_step(s):
+        def energy_products(s):
             if s + 1 < H:
-                qk_of[s + 1] = four.tile([P, NWIN, C_OUT], F32, name="qk")
+                qk_of[s + 1] = sbuf[QK_BUFS].tile([P, NWIN, C_OUT], F32, name="qk")
             if s == -1:
                 nc.gpsimd.memset(qk_of[0][:, 0:K3, :], 0.0)
             if s == H - 2:
                 nc.gpsimd.memset(qk_of[H - 1][:, NWIN - K3 : NWIN, :], 0.0)
             if 0 <= s < H:
-                k_pix = k_pix_of[s]
                 for i in range(K3):
                     t = s - i + 1
                     if 0 <= t < H:
                         nc.vector.tensor_tensor(
                             out=qk_of[t][:, K3 * i : K3 * i + K3, :],
-                            in0=k_pix[:],
+                            in0=k_pix_of[s][:],
                             in1=q_pix_of[t // CHUNK_ROWS][:, t % CHUNK_ROWS, :]
                             .unsqueeze(1)
                             .to_broadcast([P, K3, C_OUT]),
                             op=ALU.mult,
                         )
-            t = s - 1
-            if 0 <= t < H:
-                b = t // ROWS
-                if t % ROWS == 0:
-                    folded_of[b] = two.tile([P, NWIN, CG_HALF, ROWS, GROUPS], F32, name="folded")
-                by_plane = qk_of[t][:].rearrange("p n (c g) -> p n c g", g=GROUPS)
-                nc.gpsimd.tensor_tensor(
-                    out=folded_of[b][:, :, :, t % ROWS, :],
-                    in0=by_plane[:, :, 0:CG_HALF, :],
-                    in1=by_plane[:, :, CG_HALF:CG, :],
-                    op=ALU.add,
-                )
+
+        def fold(t):
+            b, r = divmod(t, ROWS)
+            if r == 0:
+                folded_of[b] = sbuf[DOUBLE].tile([P, NWIN, CG_HALF, ROWS, GROUPS], F32, name="folded")
+            planes = qk_of[t][:].rearrange("p n (c g) -> p n c g", g=GROUPS)
+            nc.gpsimd.tensor_tensor(
+                out=folded_of[b][:, :, :, r, :],
+                in0=planes[:, :, 0:CG_HALF, :],
+                in1=planes[:, :, CG_HALF:CG, :],
+                op=ALU.add,
+            )
 
         def energy_sums(b, n):
-            i, j = n // K3, n % K3
+            i, j = divmod(n, K3)
             if n == 0:
-                energy_of[b] = one.tile([P, NWIN, W], F32, name="energy")
+                energy_of[b] = sbuf[SINGLE].tile([P, NWIN, W], F32, name="energy")
             if j == 0:
-                e_ps_of[0] = ps_ea.tile([P, K3, W], F32, name="e_ps", tag="ea")
-            e_ps = e_ps_of[0]
-            for c in range(CG_HALF):
+                e_ps_of[(b, i)] = ps_soft.tile([P, K3, W], F32, name="e_ps", tag="soft")
+            e_ps = e_ps_of[(b, i)]
+            for plane in range(CG_HALF):
                 nc.tensor.matmul(
                     out=e_ps[:, j, :],
-                    lhsT=folded_of[b][:, n, c, :, :].rearrange("p r g -> p (r g)"),
+                    lhsT=folded_of[b][:, n, plane, :, :].rearrange("p r g -> p (r g)"),
                     rhs=ident[:],
                     is_transpose=True,
-                    start=(c == 0),
+                    start=(plane == 0),
                     stop=False,
                 )
             nc.tensor.matmul(
@@ -299,7 +293,7 @@ def tile_mutliheadattention2d_kernel(
 
         def softmax_top(b):
             energy = energy_of[b]
-            top = one.tile([P, W], F32, name="top")
+            top = sbuf[SINGLE].tile([P, W], F32, name="top")
             nc.vector.tensor_reduce(
                 out=top[:], in_=energy[:].rearrange("p n w -> p w n"), axis=AXIS_X, op=ALU.max
             )
@@ -313,13 +307,13 @@ def tile_mutliheadattention2d_kernel(
 
         def softmax_norm(b):
             energy = energy_of[b]
-            total = one.tile([P, W], F32, name="total")
+            total = sbuf[SINGLE].tile([P, W], F32, name="total")
             nc.vector.tensor_reduce(
                 out=total[:], in_=energy[:].rearrange("p n w -> p w n"), axis=AXIS_X, op=ALU.add
             )
-            inverse = one.tile([P, W], F32, name="inverse")
+            inverse = sbuf[SINGLE].tile([P, W], F32, name="inverse")
             nc.vector.reciprocal(out=inverse[:], in_=total[:])
-            attn_rows = one.tile([P, NWIN, WPAD], F32, name="attn_rows")
+            attn_rows = sbuf[SINGLE].tile([P, NWIN, WPAD], F32, name="attn_rows")
             nc.gpsimd.memset(attn_rows[:, :, 0 : WPAD : WPAD - 1], 0.0)
             nc.gpsimd.tensor_tensor(
                 out=attn_rows[:, :, 1 : W + 1],
@@ -328,7 +322,7 @@ def tile_mutliheadattention2d_kernel(
                 op=ALU.mult,
             )
             attn_rows_of[b] = attn_rows
-            attn_store = one.tile([P, W, NWIN], F32, name="attn_store")
+            attn_store = sbuf[SINGLE].tile([P, W, NWIN], F32, name="attn_store")
             nc.scalar.copy(
                 out=attn_store[:], in_=attn_rows[:, :, 1 : W + 1].rearrange("p n w -> p w n")
             )
@@ -337,13 +331,14 @@ def tile_mutliheadattention2d_kernel(
                 in_=attn_store[:].rearrange("p w n -> p (w n)"),
             )
 
-        def turn_weights(b, i):
+        def turn_attn(b, i):
             if i == 0:
-                attn_pix_of[b] = two.tile([P, NWIN, P], F32, name="attn_pix")
-            a_ps = ps_ea.tile([P, K3, P], F32, name="a_ps", tag="ea")
+                attn_pix_of[b] = sbuf[DOUBLE].tile([P, NWIN, P], F32, name="attn_pix")
+            a_ps = ps_soft.tile([P, K3, P], F32, name="a_ps", tag="soft")
             for j in range(K3):
+                padded_col = 1 - (j - 1)
                 nc.tensor.transpose(
-                    a_ps[:, j, :], attn_rows_of[b][:, K3 * i + j, 2 - j : 2 - j + W], ident[:]
+                    a_ps[:, j, :], attn_rows_of[b][:, K3 * i + j, padded_col : padded_col + W], ident[:]
                 )
             nc.scalar.copy(out=attn_pix_of[b][:, K3 * i : K3 * i + K3, :], in_=a_ps[:])
 
@@ -362,83 +357,90 @@ def tile_mutliheadattention2d_kernel(
                 )
             v_pix_of[c] = v_pix
 
-        def weighted_products(s):
+        def attn_v_products(s):
             if s == 0:
-                av_of[0] = five.tile([P, NWIN, C_OUT], F32, name="av")
+                av_of[0] = sbuf[AV_BUFS].tile([P, NWIN, C_OUT], F32, name="av")
             if s + 1 < H:
-                av_of[s + 1] = five.tile([P, NWIN, C_OUT], F32, name="av")
-            if s < H:
-                for i in range(K3):
-                    t = s - i + 1
-                    if 0 <= t < H:
-                        first = (t % ROWS) * GROUPS
-                        nc.vector.tensor_tensor(
-                            out=av_of[t][:, K3 * i : K3 * i + K3, :].rearrange(
-                                "p j (g c) -> p j g c", c=CG
-                            ),
-                            in0=v_pix_of[s // CHUNK_ROWS][:, s % CHUNK_ROWS, :]
-                            .rearrange("p (g c) -> p g c", c=CG)
-                            .unsqueeze(1)
-                            .to_broadcast([P, K3, GROUPS, CG]),
-                            in1=attn_pix_of[t // ROWS][:, K3 * i : K3 * i + K3, first : first + GROUPS]
-                            .unsqueeze(3)
-                            .to_broadcast([P, K3, GROUPS, CG]),
-                            op=ALU.mult,
-                        )
+                av_of[s + 1] = sbuf[AV_BUFS].tile([P, NWIN, C_OUT], F32, name="av")
+            for i in range(K3):
+                t = s - i + 1
+                if 0 <= t < H:
+                    first_col = (t % ROWS) * GROUPS
+                    nc.vector.tensor_tensor(
+                        out=av_of[t][:, K3 * i : K3 * i + K3, :].rearrange(
+                            "p j (g c) -> p j g c", c=CG
+                        ),
+                        in0=v_pix_of[s // CHUNK_ROWS][:, s % CHUNK_ROWS, :]
+                        .rearrange("p (g c) -> p g c", c=CG)
+                        .unsqueeze(1)
+                        .to_broadcast([P, K3, GROUPS, CG]),
+                        in1=attn_pix_of[t // ROWS][
+                            :, K3 * i : K3 * i + K3, first_col : first_col + GROUPS
+                        ]
+                        .unsqueeze(3)
+                        .to_broadcast([P, K3, GROUPS, CG]),
+                        op=ALU.mult,
+                    )
 
-        def weighted_sums(t):
+        def attn_v_sums(t):
             places = [K3 * i + j for i in range(K3) if 0 <= t + i - 1 < H for j in range(K3)]
-            a = t % CHUNK_ROWS
-            if a == 0:
-                acc_of[0] = ps_acc.tile([P, CHUNK_ROWS, W], F32, name="acc")
-            acc = acc_of[0]
+            c, r = divmod(t, CHUNK_ROWS)
+            if r == 0:
+                out_ps_of[c] = ps_out.tile([P, CHUNK_ROWS, W], F32, name="out_ps")
             for n in places:
                 nc.tensor.matmul(
-                    out=acc[:, a, :],
+                    out=out_ps_of[c][:, r, :],
                     lhsT=av_of[t][:, n, :],
-                    rhs=shift[n % K3][:],
+                    rhs=rotate[n % K3][:],
                     is_transpose=True,
                     start=(n == places[0]),
                     stop=(n == places[-1]),
                 )
-            if a == CHUNK_ROWS - 1:
-                out_rows = two.tile([P, CHUNK_ROWS, W], F32, name="out_rows")
-                nc.scalar.copy(out=out_rows[:], in_=acc[:])
-                nc.sync.dma_start(out=out[0, :, t - CHUNK_ROWS + 1 : t + 1, :], in_=out_rows[:])
+            if r == CHUNK_ROWS - 1:
+                out_rows = sbuf[DOUBLE].tile([P, CHUNK_ROWS, W], F32, name="out_rows")
+                nc.scalar.copy(out=out_rows[:], in_=out_ps_of[c][:])
+                nc.sync.dma_start(
+                    out=out[0, :, c * CHUNK_ROWS : (c + 1) * CHUNK_ROWS, :], in_=out_rows[:]
+                )
 
-        for c in range(3):
+        for c in range(RAW_BUFS):
             load_x(c)
         regroup(0)
         quantise(0)
-        for step in range(-LEAD, H + LAG + 3):
+        for step in range(-LEAD, LAST + 1):
             if 0 <= step + 1 < H:
                 turn_k(step + 1)
-            if -1 <= step <= H:
-                energy_step(step)
+            if -1 <= step < H:
+                energy_products(step)
+            if 0 <= step - 1 < H:
+                fold(step - 1)
+
             source = step - LAG
             if 0 <= source < H:
-                weighted_products(source)
+                attn_v_products(source)
             if 0 <= source - 2 < H:
-                weighted_sums(source - 2)
+                attn_v_sums(source - 2)
             if 0 <= source + 1 < H and (source + 1) % CHUNK_ROWS == 0:
                 project_v((source + 1) // CHUNK_ROWS)
-            for block in range(BLOCKS):
-                since = step - block * ROWS
+
+            for b in range(BANDS):
+                since = step - b * ROWS
                 if SUMS_AT <= since < SUMS_AT + NWIN:
-                    energy_sums(block, since - SUMS_AT)
+                    energy_sums(b, since - SUMS_AT)
                 if since == TOP_AT:
-                    softmax_top(block)
+                    softmax_top(b)
                 if since == NORM_AT:
-                    softmax_norm(block)
+                    softmax_norm(b)
                 if TURN_AT <= since < TURN_AT + K3:
-                    turn_weights(block, since - TURN_AT)
+                    turn_attn(b, since - TURN_AT)
+
             c, stage = divmod(step + LEAD, CHUNK_ROWS)
             if stage == 0:
                 if c < CHUNKS:
                     project_k(c)
                     project_q(c)
-                if c + 3 < CHUNKS:
-                    load_x(c + 3)
+                if c + RAW_BUFS < CHUNKS:
+                    load_x(c + RAW_BUFS)
                 if c + 1 < CHUNKS:
                     regroup(c + 1)
             if stage == 1:
@@ -446,5 +448,5 @@ def tile_mutliheadattention2d_kernel(
                     turn_q(c)
                 if c + 1 < CHUNKS:
                     quantise(c + 1)
-            if stage >= 2 and c < CHUNKS:
-                q_dot_rel(c, (stage - 2) * (CHUNK_ROWS // 2))
+            if stage == 2 and c < CHUNKS:
+                q_dot_rel(c)

@@ -52,6 +52,8 @@ QK_BUFS = 4
 AV_BUFS = 5
 CODES_BUFS = (LAG + LEAD + CHUNK_ROWS) // CHUNK_ROWS + 2
 
+AHEAD = 4
+
 PROJECTIONS = 3
 Q_IDX, K_IDX, V_IDX = 0, 1, 2
 
@@ -66,10 +68,10 @@ def tile_mutliheadattention2d_kernel(
         depths = sorted({SINGLE, DOUBLE, RAW_BUFS, CHUNK_BUFS, QK_BUFS, AV_BUFS, CODES_BUFS})
         sbuf = {n: ctx.enter_context(tc.tile_pool(name="sbuf%d" % n, bufs=n)) for n in depths}
         ps_proj = ctx.enter_context(tc.psum_pool(name="ps_proj", bufs=2))
-        ps_v = ctx.enter_context(tc.psum_pool(name="ps_v", bufs=2))
-        ps_k = ctx.enter_context(tc.psum_pool(name="ps_k", bufs=2))
+        ps_kv = ctx.enter_context(tc.psum_pool(name="ps_kv", bufs=2))
+        ps_qr = ctx.enter_context(tc.psum_pool(name="ps_qr", bufs=1))
         ps_soft = ctx.enter_context(tc.psum_pool(name="ps_soft", bufs=1))
-        ps_out = ctx.enter_context(tc.psum_pool(name="ps_out", bufs=1))
+        ps_out = ctx.enter_context(tc.psum_pool(name="ps_out", bufs=2))
 
         ident = sbuf[SINGLE].tile([P, P], F32, name="ident")
         make_identity(nc, ident[:])
@@ -111,6 +113,12 @@ def tile_mutliheadattention2d_kernel(
             op=ALU.mult,
         )
 
+        rel_wide = sbuf[SINGLE].tile([P, C_OUT], F32, name="rel_wide")
+        nc.vector.memset(rel_wide[:], 0.0)
+        nc.vector.tensor_copy(
+            out=rel_wide[:, 0 : NWIN * GROUPS], in_=rel_by_place[:].rearrange("p n g -> p (n g)")
+        )
+
         w_codes = sbuf[SINGLE].tile([P, PROJECTIONS, C_OUT], U32, name="w_codes", align_bytes=64)
         w_scales = sbuf[SINGLE].tile([P, PROJECTIONS, C_OUT], U8, name="w_scales", align_bytes=64)
         nc.vector.memset(w_scales[:].rearrange("p a n -> p (a n)").bitcast(I32), 0)
@@ -128,23 +136,35 @@ def tile_mutliheadattention2d_kernel(
                     in_=scales[0, quad * LIVE : (quad + 1) * LIVE, :].bitcast(I32),
                 )
 
+        w_codes_pl = sbuf[SINGLE].tile([P, 2, C_OUT], U32, name="w_codes_pl", align_bytes=64)
+        w_scales_pl = sbuf[SINGLE].tile([P, 2, C_OUT], U8, name="w_scales_pl", align_bytes=64)
+        for idx in (Q_IDX, K_IDX):
+            nc.vector.tensor_copy(
+                out=w_codes_pl[:, idx, :].bitcast(I32).rearrange("p (c g) -> p g c", g=GROUPS),
+                in_=w_codes[:, idx, :].bitcast(I32).rearrange("p (g c) -> p g c", c=CG),
+            )
+            nc.vector.tensor_copy(
+                out=w_scales_pl[:, idx, :].rearrange("p (c g) -> p g c", g=GROUPS),
+                in_=w_scales[:, idx, :].rearrange("p (g c) -> p g c", c=CG),
+            )
+
         x_by_word = x[0].rearrange("(p e) h w -> p e (h w)", e=PACK)
 
         raw_of = {}
         grouped_of = {}
         codes_of = {}
-        k_rows_of = {}
-        q_rows_of = {}
+        proj_of = {}
+        kq_rows_of = {}
+        qr_of = {}
         q_pix_of = {}
         qr_pix_of = {}
-        k_pix_of = {}
+        kv_of = {}
         qk_of = {}
         folded_of = {}
         e_ps_of = {}
         energy_of = {}
         attn_rows_of = {}
         attn_pix_of = {}
-        v_pix_of = {}
         av_of = {}
         out_ps_of = {}
 
@@ -153,13 +173,13 @@ def tile_mutliheadattention2d_kernel(
             nc.sync.dma_start(out=raw[:], in_=x_by_word[:, :, c * CHUNK : (c + 1) * CHUNK])
             raw_of[c] = raw
 
-        def regroup(c):
-            grouped = sbuf[DOUBLE].tile([P, CHUNK, PACK], BF16, name="grouped", align_bytes=64)
+        def regroup(c, r):
+            if r == 0:
+                grouped_of[c] = sbuf[DOUBLE].tile([P, CHUNK, PACK], BF16, name="grouped", align_bytes=64)
             nc.scalar.copy(
-                out=grouped[:].rearrange("p (u i) e -> p u e i", i=RUN),
-                in_=raw_of[c][:].rearrange("p e (u i) -> p u e i", i=RUN),
+                out=grouped_of[c][:, r * W : (r + 1) * W, :].rearrange("p (u i) e -> p u e i", i=RUN),
+                in_=raw_of[c][:, :, r * W : (r + 1) * W].rearrange("p e (u i) -> p u e i", i=RUN),
             )
-            grouped_of[c] = grouped
 
         def quantise(c):
             codes = sbuf[CODES_BUFS].tile([P, CHUNK], U32, name="codes", align_bytes=64)
@@ -171,66 +191,85 @@ def tile_mutliheadattention2d_kernel(
             )
             codes_of[c] = (codes, scales)
 
-        def project_by_channel(c, idx):
-            codes, scales = codes_of[c]
-            proj = ps_proj.tile([P, CHUNK], F32, name="proj", tag="proj")
+        def x_row(t):
+            codes, scales = codes_of[t // CHUNK_ROWS]
+            cols = slice((t % CHUNK_ROWS) * W, (t % CHUNK_ROWS + 1) * W)
+            return codes[:, cols].bitcast(FP8X4), scales[:, cols]
+
+        def by_channel(out, t, idx):
+            x_codes, x_scales = x_row(t)
             nc.tensor.matmul_mx(
-                out=proj[:],
+                out=out,
                 lhsT=w_codes[:, idx, :].bitcast(FP8X4),
                 lhsT_scale=w_scales[:, idx, :],
-                rhs=codes[:].bitcast(FP8X4),
-                rhs_scale=scales[:],
+                rhs=x_codes,
+                rhs_scale=x_scales,
                 start=True,
                 stop=True,
             )
-            return proj[:].rearrange("p (r w) -> p r w", w=W)
 
-        def project_k(c):
-            k_ps = project_by_channel(c, K_IDX)
-            k_rows = sbuf[CHUNK_BUFS].tile([P, CHUNK_ROWS, WPAD], F32, name="k_rows")
-            nc.scalar.copy(out=k_rows[:, :, 0 : WPAD : WPAD - 1], in_=zeros[:])
-            nc.scalar.copy(out=k_rows[:, :, 1 : W + 1], in_=k_ps)
-            k_rows_of[c] = k_rows
-
-        def project_q(c):
-            q_rows = sbuf[DOUBLE].tile([P, CHUNK_ROWS, W], F32, name="q_rows")
-            nc.scalar.copy(out=q_rows[:], in_=project_by_channel(c, Q_IDX))
-            q_rows_of[c] = q_rows
-
-        def turn_q(c):
-            turned = ps_proj.tile([P, CHUNK_ROWS, C_OUT], F32, name="turned", tag="proj")
-            for r in range(CHUNK_ROWS):
-                nc.tensor.transpose(turned[:, r, :], q_rows_of[c][:, r, :], by_plane[:])
-            q_pix = sbuf[CHUNK_BUFS].tile([P, CHUNK_ROWS, C_OUT], F32, name="q_pix")
-            nc.scalar.copy(out=q_pix[:], in_=turned[:])
-            q_pix_of[c] = q_pix
-
-        def q_dot_rel(c):
-            qr = ps_proj.tile([P, CHUNK_ROWS, NWIN, GROUPS], F32, name="qr", tag="proj")
-            for r in range(CHUNK_ROWS):
-                nc.tensor.matmul(
-                    out=qr[:, r, :, :].rearrange("p n g -> p (n g)"),
-                    lhsT=q_rows_of[c][:, r, :],
-                    rhs=rel_by_place[:].rearrange("p n g -> p (n g)"),
-                    start=True,
-                    stop=True,
-                )
-            b, first_row = divmod(c * CHUNK_ROWS, ROWS)
-            if first_row == 0:
-                qr_pix_of[b] = sbuf[DOUBLE].tile([P, NWIN, ROWS, GROUPS], F32, name="qr_pix")
-            nc.scalar.copy(
-                out=qr_pix_of[b][:, :, first_row : first_row + CHUNK_ROWS, :].rearrange(
-                    "p n r g -> p r n g"
-                ),
-                in_=qr[:],
+        def by_pixel(out, t, codes_ap, scales_ap):
+            x_codes, x_scales = x_row(t)
+            nc.tensor.matmul_mx(
+                out=out,
+                lhsT=x_codes,
+                lhsT_scale=x_scales,
+                rhs=codes_ap.bitcast(FP8X4),
+                rhs_scale=scales_ap,
+                start=True,
+                stop=True,
             )
 
+        def mx_passes(a, s, v_row):
+            if 0 <= a < H:
+                proj = ps_proj.tile([P, PROJECTIONS, W], F32, name="proj")
+                by_channel(proj[:, 0, :], a, K_IDX)
+                by_channel(proj[:, 1, :], a, Q_IDX)
+                by_pixel(proj[:, 2, :], a, w_codes_pl[:, Q_IDX, :], w_scales_pl[:, Q_IDX, :])
+                proj_of[a] = proj
+            if 0 <= s < H or 0 <= v_row < H:
+                kv_of[s] = ps_kv.tile([P, K3 + 1, C_OUT], F32, name="kv")
+            if 0 <= s < H:
+                by_pixel(kv_of[s][:, 1, :], s, w_codes_pl[:, K_IDX, :], w_scales_pl[:, K_IDX, :])
+            if 0 <= v_row < H:
+                by_pixel(kv_of[s][:, K3, :], v_row, w_codes[:, V_IDX, :], w_scales[:, V_IDX, :])
+
+        def empty_proj(a):
+            c, r = divmod(a, CHUNK_ROWS)
+            if r == 0:
+                kq_rows = sbuf[CHUNK_BUFS].tile([P, 2, CHUNK_ROWS, WPAD], F32, name="kq_rows")
+                nc.scalar.copy(out=kq_rows[:, 0, :, 0 : WPAD : WPAD - 1], in_=zeros[:])
+                kq_rows_of[c] = kq_rows
+                q_pix_of[c] = sbuf[CHUNK_BUFS].tile([P, CHUNK_ROWS, C_OUT], F32, name="q_pix")
+            nc.scalar.copy(out=kq_rows_of[c][:, :, r, 1 : W + 1], in_=proj_of[a][:, 0:2, :])
+            nc.scalar.copy(out=q_pix_of[c][:, r, :], in_=proj_of[a][:, 2, :])
+
+        def q_dot_rel(t):
+            c, r = divmod(t, CHUNK_ROWS)
+            if r == 0:
+                qr_of[c] = ps_qr.tile([P, CHUNK_ROWS, C_OUT], F32, name="qr")
+            nc.tensor.matmul(
+                out=qr_of[c][:, r, :],
+                lhsT=kq_rows_of[c][:, 1, r, 1 : W + 1],
+                rhs=rel_wide[:],
+                start=True,
+                stop=True,
+            )
+            if r == CHUNK_ROWS - 1:
+                b, first_row = divmod(c * CHUNK_ROWS, ROWS)
+                if first_row == 0:
+                    qr_pix_of[b] = sbuf[DOUBLE].tile([P, NWIN, ROWS, GROUPS], F32, name="qr_pix")
+                nc.scalar.copy(
+                    out=qr_pix_of[b][:, :, first_row : first_row + CHUNK_ROWS, :].rearrange(
+                        "p n r g -> p r n g"
+                    ),
+                    in_=qr_of[c][:, :, 0 : NWIN * GROUPS].rearrange("p r (n g) -> p r n g", g=GROUPS),
+                )
+
         def turn_k(s):
-            k_row = k_rows_of[s // CHUNK_ROWS][:, s % CHUNK_ROWS, :]
-            k_pix = ps_k.tile([P, K3, C_OUT], F32, name="k_pix")
-            for j in range(K3):
-                nc.tensor.transpose(k_pix[:, j, :], k_row[:, j : j + W], by_plane[:])
-            k_pix_of[s] = k_pix
+            k_row = kq_rows_of[s // CHUNK_ROWS][:, 0, s % CHUNK_ROWS, :]
+            for j in (0, K3 - 1):
+                nc.tensor.transpose(kv_of[s][:, j, :], k_row[:, j : j + W], by_plane[:])
 
         def energy_products(s):
             if s + 1 < H:
@@ -245,7 +284,7 @@ def tile_mutliheadattention2d_kernel(
                     if 0 <= t < H:
                         nc.vector.tensor_tensor(
                             out=qk_of[t][:, K3 * i : K3 * i + K3, :],
-                            in0=k_pix_of[s][:],
+                            in0=kv_of[s][:, 0:K3, :],
                             in1=q_pix_of[t // CHUNK_ROWS][:, t % CHUNK_ROWS, :]
                             .unsqueeze(1)
                             .to_broadcast([P, K3, C_OUT]),
@@ -342,21 +381,6 @@ def tile_mutliheadattention2d_kernel(
                 )
             nc.scalar.copy(out=attn_pix_of[b][:, K3 * i : K3 * i + K3, :], in_=a_ps[:])
 
-        def project_v(c):
-            codes, scales = codes_of[c]
-            v_pix = ps_v.tile([P, CHUNK_ROWS, C_OUT], F32, name="v_pix")
-            for r in range(CHUNK_ROWS):
-                nc.tensor.matmul_mx(
-                    out=v_pix[:, r, :],
-                    lhsT=codes[:, r * W : (r + 1) * W].bitcast(FP8X4),
-                    lhsT_scale=scales[:, r * W : (r + 1) * W],
-                    rhs=w_codes[:, V_IDX, :].bitcast(FP8X4),
-                    rhs_scale=w_scales[:, V_IDX, :],
-                    start=True,
-                    stop=True,
-                )
-            v_pix_of[c] = v_pix
-
         def attn_v_products(s):
             if s == 0:
                 av_of[0] = sbuf[AV_BUFS].tile([P, NWIN, C_OUT], F32, name="av")
@@ -370,7 +394,7 @@ def tile_mutliheadattention2d_kernel(
                         out=av_of[t][:, K3 * i : K3 * i + K3, :].rearrange(
                             "p j (g c) -> p j g c", c=CG
                         ),
-                        in0=v_pix_of[s // CHUNK_ROWS][:, s % CHUNK_ROWS, :]
+                        in0=kv_of[s + LAG][:, K3, :]
                         .rearrange("p (g c) -> p g c", c=CG)
                         .unsqueeze(1)
                         .to_broadcast([P, K3, GROUPS, CG]),
@@ -405,9 +429,14 @@ def tile_mutliheadattention2d_kernel(
 
         for c in range(RAW_BUFS):
             load_x(c)
-        regroup(0)
+        for r in range(CHUNK_ROWS):
+            regroup(0, r)
         quantise(0)
         for step in range(-LEAD, LAST + 1):
+            source = step - LAG
+            mx_passes(step + AHEAD, step + 1, source + 1)
+            if 0 <= step + AHEAD < H:
+                empty_proj(step + AHEAD)
             if 0 <= step + 1 < H:
                 turn_k(step + 1)
             if -1 <= step < H:
@@ -415,13 +444,12 @@ def tile_mutliheadattention2d_kernel(
             if 0 <= step - 1 < H:
                 fold(step - 1)
 
-            source = step - LAG
             if 0 <= source < H:
                 attn_v_products(source)
             if 0 <= source - 2 < H:
                 attn_v_sums(source - 2)
-            if 0 <= source + 1 < H and (source + 1) % CHUNK_ROWS == 0:
-                project_v((source + 1) // CHUNK_ROWS)
+            if 0 <= step + AHEAD - 1 < H:
+                q_dot_rel(step + AHEAD - 1)
 
             for b in range(BANDS):
                 since = step - b * ROWS
@@ -436,17 +464,9 @@ def tile_mutliheadattention2d_kernel(
 
             c, stage = divmod(step + LEAD, CHUNK_ROWS)
             if stage == 0:
-                if c < CHUNKS:
-                    project_k(c)
-                    project_q(c)
+                if 1 <= c < CHUNKS:
+                    quantise(c)
                 if c + RAW_BUFS < CHUNKS:
                     load_x(c + RAW_BUFS)
-                if c + 1 < CHUNKS:
-                    regroup(c + 1)
-            if stage == 1:
-                if c < CHUNKS:
-                    turn_q(c)
-                if c + 1 < CHUNKS:
-                    quantise(c + 1)
-            if stage == 2 and c < CHUNKS:
-                q_dot_rel(c)
+            if c + 1 < CHUNKS:
+                regroup(c + 1, stage)

@@ -36,11 +36,19 @@ QUADRANTS = 4
 LIVE = 4
 
 SLACK = 2
-LEAD = CHUNK_ROWS + SLACK
+Q_AHEAD = 4
+K_AHEAD = 6
+SHIFT_CUT = 112
+K_RING = 12
+LEAD = K_AHEAD + SLACK
 SUMS_AT = ROWS + SLACK
-TOP_AT = SUMS_AT + NWIN
-NORM_AT = TOP_AT + SLACK
-TURN_AT = NORM_AT + SLACK
+MAX_AT = SUMS_AT + NWIN + 1
+SUB_AT = MAX_AT + 1
+EXP_AT = SUB_AT + SLACK
+TOTAL_AT = EXP_AT + K3 + 1
+SCALE_AT = TOTAL_AT + 1
+TURN_AT = SCALE_AT + SLACK
+STORE_AT = TURN_AT + K3 - 1
 LAG = TURN_AT + K3 + SLACK
 LAST = H + LAG + 1
 
@@ -48,11 +56,10 @@ SINGLE = 1
 DOUBLE = 2
 RAW_BUFS = 3
 CHUNK_BUFS = 4
-QK_BUFS = 4
+QK_BUFS = 3
 AV_BUFS = 5
-CODES_BUFS = (LAG + LEAD + CHUNK_ROWS) // CHUNK_ROWS + 2
+CODES_BUFS = (LAG + LEAD + CHUNK_ROWS) // CHUNK_ROWS + 1
 
-AHEAD = 4
 
 PROJECTIONS = 3
 Q_IDX, K_IDX, V_IDX = 0, 1, 2
@@ -67,19 +74,14 @@ def tile_mutliheadattention2d_kernel(
     with ExitStack() as ctx:
         depths = sorted({SINGLE, DOUBLE, RAW_BUFS, CHUNK_BUFS, QK_BUFS, AV_BUFS, CODES_BUFS})
         sbuf = {n: ctx.enter_context(tc.tile_pool(name="sbuf%d" % n, bufs=n)) for n in depths}
-        ps_proj = ctx.enter_context(tc.psum_pool(name="ps_proj", bufs=2))
-        ps_kv = ctx.enter_context(tc.psum_pool(name="ps_kv", bufs=2))
+        ps_s = ctx.enter_context(tc.psum_pool(name="ps_s", bufs=2))
+        ps_v = ctx.enter_context(tc.psum_pool(name="ps_v", bufs=2))
         ps_qr = ctx.enter_context(tc.psum_pool(name="ps_qr", bufs=1))
         ps_soft = ctx.enter_context(tc.psum_pool(name="ps_soft", bufs=1))
         ps_out = ctx.enter_context(tc.psum_pool(name="ps_out", bufs=2))
 
         ident = sbuf[SINGLE].tile([P, P], F32, name="ident")
         make_identity(nc, ident[:])
-        by_plane = sbuf[SINGLE].tile([P, P], F32, name="by_plane")
-        nc.vector.tensor_copy(
-            out=by_plane[:].rearrange("p (c g) -> p c g", g=GROUPS),
-            in_=ident[:].rearrange("p (g c) -> p c g", c=CG),
-        )
         rotate_up = sbuf[SINGLE].tile([P, P], F32, name="rotate_up")
         nc.vector.tensor_copy(out=rotate_up[:, 1:P], in_=ident[:, 0 : P - 1])
         nc.vector.tensor_copy(out=rotate_up[:, 0:1], in_=ident[:, P - 1 : P])
@@ -87,8 +89,8 @@ def tile_mutliheadattention2d_kernel(
         nc.vector.tensor_copy(out=rotate_down[:, 0 : P - 1], in_=ident[:, 1:P])
         nc.vector.tensor_copy(out=rotate_down[:, P - 1 : P], in_=ident[:, 0:1])
         rotate = (rotate_up, ident, rotate_down)
-        zeros = sbuf[SINGLE].tile([P, CHUNK_ROWS, PADS], F32, name="zeros")
-        nc.vector.memset(zeros[:], 0.0)
+        k_ring = sbuf[SINGLE].tile([P, K3, K_RING, C_OUT], F32, name="k_ring")
+        nc.gpsimd.memset(k_ring[:], 0.0)
 
         half = C_OUT // 2
         rel3 = sbuf[SINGLE].tile([P, K3], BF16, name="rel3")
@@ -153,15 +155,16 @@ def tile_mutliheadattention2d_kernel(
         raw_of = {}
         grouped_of = {}
         codes_of = {}
-        proj_of = {}
-        kq_rows_of = {}
+        for_scalar_of = {}
+        for_vector_of = {}
+        q_rows_of = {}
         qr_of = {}
-        q_pix_of = {}
         qr_pix_of = {}
-        kv_of = {}
         qk_of = {}
         folded_of = {}
         e_ps_of = {}
+        top_of = {}
+        inverse_of = {}
         energy_of = {}
         attn_rows_of = {}
         attn_pix_of = {}
@@ -220,29 +223,40 @@ def tile_mutliheadattention2d_kernel(
                 stop=True,
             )
 
-        def mx_passes(a, s, v_row):
-            if 0 <= a < H:
-                proj = ps_proj.tile([P, PROJECTIONS, W], F32, name="proj")
-                by_channel(proj[:, 0, :], a, K_IDX)
-                by_channel(proj[:, 1, :], a, Q_IDX)
-                by_pixel(proj[:, 2, :], a, w_codes_pl[:, Q_IDX, :], w_scales_pl[:, Q_IDX, :])
-                proj_of[a] = proj
-            if 0 <= s < H or 0 <= v_row < H:
-                kv_of[s] = ps_kv.tile([P, K3 + 1, C_OUT], F32, name="kv")
-            if 0 <= s < H:
-                by_pixel(kv_of[s][:, 1, :], s, w_codes_pl[:, K_IDX, :], w_scales_pl[:, K_IDX, :])
+        def mx_passes(step):
+            q_row, k_row, v_row = step + Q_AHEAD, step + K_AHEAD, step - LAG + 1
+            if 0 <= q_row < H or 0 <= k_row < H:
+                for_scalar_of[step] = ps_s.tile([P, 2, W], F32, name="for_scalar")
+            if 0 <= q_row < H:
+                by_channel(for_scalar_of[step][:, 0, :], q_row, Q_IDX)
+            if 0 <= k_row < H:
+                by_pixel(for_scalar_of[step][:, 1, :], k_row, w_codes_pl[:, K_IDX, :], w_scales_pl[:, K_IDX, :])
+            if 0 <= step < H or 0 <= v_row < H:
+                for_vector_of[step] = ps_v.tile([P, 2, C_OUT], F32, name="for_vector")
+            if 0 <= step < H:
+                by_pixel(for_vector_of[step][:, 0, :], step, w_codes_pl[:, Q_IDX, :], w_scales_pl[:, Q_IDX, :])
             if 0 <= v_row < H:
-                by_pixel(kv_of[s][:, K3, :], v_row, w_codes[:, V_IDX, :], w_scales[:, V_IDX, :])
+                by_pixel(for_vector_of[step][:, 1, :], v_row, w_codes[:, V_IDX, :], w_scales[:, V_IDX, :])
 
-        def empty_proj(a):
-            c, r = divmod(a, CHUNK_ROWS)
-            if r == 0:
-                kq_rows = sbuf[CHUNK_BUFS].tile([P, 2, CHUNK_ROWS, WPAD], F32, name="kq_rows")
-                nc.scalar.copy(out=kq_rows[:, 0, :, 0 : WPAD : WPAD - 1], in_=zeros[:])
-                kq_rows_of[c] = kq_rows
-                q_pix_of[c] = sbuf[CHUNK_BUFS].tile([P, CHUNK_ROWS, C_OUT], F32, name="q_pix")
-            nc.scalar.copy(out=kq_rows_of[c][:, :, r, 1 : W + 1], in_=proj_of[a][:, 0:2, :])
-            nc.scalar.copy(out=q_pix_of[c][:, r, :], in_=proj_of[a][:, 2, :])
+        def empty_for_scalar(step):
+            q_row, k_row = step + Q_AHEAD, step + K_AHEAD
+            if 0 <= q_row < H:
+                c, r = divmod(q_row, CHUNK_ROWS)
+                if r == 0:
+                    q_rows_of[c] = sbuf[DOUBLE].tile([P, CHUNK_ROWS, W], F32, name="q_rows")
+                nc.scalar.copy(out=q_rows_of[c][:, r, :], in_=for_scalar_of[step][:, 0, :])
+            if 0 <= k_row < H:
+                nc.scalar.copy(out=k_ring[:, 1, k_row % K_RING, :], in_=for_scalar_of[step][:, 1, :])
+                if k_row % CHUNK_ROWS == CHUNK_ROWS - 1:
+                    last = k_row % K_RING + 1
+                    slots = slice(last - CHUNK_ROWS, last)
+                    for low, high in ((0, SHIFT_CUT), (SHIFT_CUT, P - 1)):
+                        nc.sync.dma_start(
+                            out=k_ring[low + 1 : high + 1, 0, slots, :], in_=k_ring[low:high, 1, slots, :]
+                        )
+                        nc.sync.dma_start(
+                            out=k_ring[low:high, 2, slots, :], in_=k_ring[low + 1 : high + 1, 1, slots, :]
+                        )
 
         def q_dot_rel(t):
             c, r = divmod(t, CHUNK_ROWS)
@@ -250,7 +264,7 @@ def tile_mutliheadattention2d_kernel(
                 qr_of[c] = ps_qr.tile([P, CHUNK_ROWS, C_OUT], F32, name="qr")
             nc.tensor.matmul(
                 out=qr_of[c][:, r, :],
-                lhsT=kq_rows_of[c][:, 1, r, 1 : W + 1],
+                lhsT=q_rows_of[c][:, r, :],
                 rhs=rel_wide[:],
                 start=True,
                 stop=True,
@@ -266,30 +280,29 @@ def tile_mutliheadattention2d_kernel(
                     in_=qr_of[c][:, :, 0 : NWIN * GROUPS].rearrange("p r (n g) -> p r n g", g=GROUPS),
                 )
 
-        def turn_k(s):
-            k_row = kq_rows_of[s // CHUNK_ROWS][:, 0, s % CHUNK_ROWS, :]
-            for j in (0, K3 - 1):
-                nc.tensor.transpose(kv_of[s][:, j, :], k_row[:, j : j + W], by_plane[:])
-
-        def energy_products(s):
-            if s + 1 < H:
-                qk_of[s + 1] = sbuf[QK_BUFS].tile([P, NWIN, C_OUT], F32, name="qk")
-            if s == -1:
-                nc.gpsimd.memset(qk_of[0][:, 0:K3, :], 0.0)
-            if s == H - 2:
-                nc.gpsimd.memset(qk_of[H - 1][:, NWIN - K3 : NWIN, :], 0.0)
-            if 0 <= s < H:
-                for i in range(K3):
-                    t = s - i + 1
-                    if 0 <= t < H:
-                        nc.vector.tensor_tensor(
-                            out=qk_of[t][:, K3 * i : K3 * i + K3, :],
-                            in0=kv_of[s][:, 0:K3, :],
-                            in1=q_pix_of[t // CHUNK_ROWS][:, t % CHUNK_ROWS, :]
-                            .unsqueeze(1)
-                            .to_broadcast([P, K3, C_OUT]),
-                            op=ALU.mult,
-                        )
+        def energy_products(t):
+            qk = sbuf[QK_BUFS].tile([P, NWIN, C_OUT], F32, name="qk")
+            qk_of[t] = qk
+            sources = [s for s in (t - 1, t, t + 1) if 0 <= s < H]
+            if t == 0:
+                nc.gpsimd.memset(qk[:, 0:K3, :], 0.0)
+            if t == H - 1:
+                nc.gpsimd.memset(qk[:, NWIN - K3 : NWIN, :], 0.0)
+            laps = sorted({s // K_RING for s in sources})
+            for run in [[s for s in sources if s // K_RING == lap] for lap in laps]:
+                first_i, count = run[0] - t + 1, len(run)
+                slot = run[0] % K_RING
+                nc.vector.tensor_tensor(
+                    out=qk[:, K3 * first_i : K3 * (first_i + count), :].rearrange(
+                        "p (i j) o -> p j i o", j=K3
+                    ),
+                    in0=k_ring[:, :, slot : slot + count, :],
+                    in1=for_vector_of[t][:, 0, :]
+                    .unsqueeze(1)
+                    .unsqueeze(1)
+                    .to_broadcast([P, K3, count, C_OUT]),
+                    op=ALU.mult,
+                )
 
         def fold(t):
             b, r = divmod(t, ROWS)
@@ -306,7 +319,7 @@ def tile_mutliheadattention2d_kernel(
         def energy_sums(b, n):
             i, j = divmod(n, K3)
             if n == 0:
-                energy_of[b] = sbuf[SINGLE].tile([P, NWIN, W], F32, name="energy")
+                energy_of[b] = sbuf[DOUBLE].tile([P, NWIN, W], F32, name="energy")
             if j == 0:
                 e_ps_of[(b, i)] = ps_soft.tile([P, K3, W], F32, name="e_ps", tag="soft")
             e_ps = e_ps_of[(b, i)]
@@ -330,40 +343,51 @@ def tile_mutliheadattention2d_kernel(
             if j == K3 - 1:
                 nc.scalar.copy(out=energy_of[b][:, K3 * i : K3 * i + K3, :], in_=e_ps[:])
 
-        def softmax_top(b):
-            energy = energy_of[b]
+        def window_row(tile, i):
+            return tile[:, K3 * i : K3 * i + K3, :]
+
+        def softmax_max(b):
             top = sbuf[SINGLE].tile([P, W], F32, name="top")
             nc.vector.tensor_reduce(
-                out=top[:], in_=energy[:].rearrange("p n w -> p w n"), axis=AXIS_X, op=ALU.max
+                out=top[:], in_=energy_of[b][:].rearrange("p n w -> p w n"), axis=AXIS_X, op=ALU.max
             )
+            top_of[b] = top
+
+        def softmax_subtract(b, i):
             nc.gpsimd.tensor_tensor(
-                out=energy[:],
-                in0=energy[:],
-                in1=top[:].unsqueeze(1).to_broadcast([P, NWIN, W]),
+                out=window_row(energy_of[b], i),
+                in0=window_row(energy_of[b], i),
+                in1=top_of[b][:].unsqueeze(1).to_broadcast([P, K3, W]),
                 op=ALU.subtract,
             )
-            nc.scalar.activation(out=energy[:], in_=energy[:], func=EXP)
 
-        def softmax_norm(b):
-            energy = energy_of[b]
+        def softmax_exp(b, i):
+            nc.scalar.activation(out=window_row(energy_of[b], i), in_=window_row(energy_of[b], i), func=EXP)
+
+        def softmax_total(b):
             total = sbuf[SINGLE].tile([P, W], F32, name="total")
             nc.vector.tensor_reduce(
-                out=total[:], in_=energy[:].rearrange("p n w -> p w n"), axis=AXIS_X, op=ALU.add
+                out=total[:], in_=energy_of[b][:].rearrange("p n w -> p w n"), axis=AXIS_X, op=ALU.add
             )
             inverse = sbuf[SINGLE].tile([P, W], F32, name="inverse")
             nc.vector.reciprocal(out=inverse[:], in_=total[:])
-            attn_rows = sbuf[SINGLE].tile([P, NWIN, WPAD], F32, name="attn_rows")
-            nc.gpsimd.memset(attn_rows[:, :, 0 : WPAD : WPAD - 1], 0.0)
+            inverse_of[b] = inverse
+
+        def softmax_scale(b, i):
+            if i == 0:
+                attn_rows_of[b] = sbuf[SINGLE].tile([P, NWIN, WPAD], F32, name="attn_rows")
+                nc.gpsimd.memset(attn_rows_of[b][:, :, 0 : WPAD : WPAD - 1], 0.0)
             nc.gpsimd.tensor_tensor(
-                out=attn_rows[:, :, 1 : W + 1],
-                in0=energy[:],
-                in1=inverse[:].unsqueeze(1).to_broadcast([P, NWIN, W]),
+                out=window_row(attn_rows_of[b], i)[:, :, 1 : W + 1],
+                in0=window_row(energy_of[b], i),
+                in1=inverse_of[b][:].unsqueeze(1).to_broadcast([P, K3, W]),
                 op=ALU.mult,
             )
-            attn_rows_of[b] = attn_rows
+
+        def store_attn(b):
             attn_store = sbuf[SINGLE].tile([P, W, NWIN], F32, name="attn_store")
             nc.scalar.copy(
-                out=attn_store[:], in_=attn_rows[:, :, 1 : W + 1].rearrange("p n w -> p w n")
+                out=attn_store[:], in_=attn_rows_of[b][:, :, 1 : W + 1].rearrange("p n w -> p w n")
             )
             nc.sync.dma_start(
                 out=attn[0, :, b * ROWS : (b + 1) * ROWS, :, :].rearrange("g h w n -> h g (w n)"),
@@ -394,7 +418,7 @@ def tile_mutliheadattention2d_kernel(
                         out=av_of[t][:, K3 * i : K3 * i + K3, :].rearrange(
                             "p j (g c) -> p j g c", c=CG
                         ),
-                        in0=kv_of[s + LAG][:, K3, :]
+                        in0=for_vector_of[s + LAG - 1][:, 1, :]
                         .rearrange("p (g c) -> p g c", c=CG)
                         .unsqueeze(1)
                         .to_broadcast([P, K3, GROUPS, CG]),
@@ -434,33 +458,37 @@ def tile_mutliheadattention2d_kernel(
         quantise(0)
         for step in range(-LEAD, LAST + 1):
             source = step - LAG
-            mx_passes(step + AHEAD, step + 1, source + 1)
-            if 0 <= step + AHEAD < H:
-                empty_proj(step + AHEAD)
-            if 0 <= step + 1 < H:
-                turn_k(step + 1)
-            if -1 <= step < H:
-                energy_products(step)
+            mx_passes(step)
+            empty_for_scalar(step)
             if 0 <= step - 1 < H:
+                energy_products(step - 1)
                 fold(step - 1)
 
             if 0 <= source < H:
                 attn_v_products(source)
             if 0 <= source - 2 < H:
                 attn_v_sums(source - 2)
-            if 0 <= step + AHEAD - 1 < H:
-                q_dot_rel(step + AHEAD - 1)
+            if 0 <= step + Q_AHEAD - 1 < H:
+                q_dot_rel(step + Q_AHEAD - 1)
 
             for b in range(BANDS):
                 since = step - b * ROWS
                 if SUMS_AT <= since < SUMS_AT + NWIN:
                     energy_sums(b, since - SUMS_AT)
-                if since == TOP_AT:
-                    softmax_top(b)
-                if since == NORM_AT:
-                    softmax_norm(b)
+                if since == MAX_AT:
+                    softmax_max(b)
+                if SUB_AT <= since < SUB_AT + K3:
+                    softmax_subtract(b, since - SUB_AT)
+                if EXP_AT <= since < EXP_AT + K3:
+                    softmax_exp(b, since - EXP_AT)
+                if since == TOTAL_AT:
+                    softmax_total(b)
+                if SCALE_AT <= since < SCALE_AT + K3:
+                    softmax_scale(b, since - SCALE_AT)
                 if TURN_AT <= since < TURN_AT + K3:
                     turn_attn(b, since - TURN_AT)
+                if since == STORE_AT:
+                    store_attn(b)
 
             c, stage = divmod(step + LEAD, CHUNK_ROWS)
             if stage == 0:

@@ -36,8 +36,9 @@ QUADRANTS = 4
 LIVE = 4
 
 SLACK = 2
-Q_AHEAD = 4
-K_AHEAD = 6
+PAIR = 2
+Q_AHEAD = 5
+K_AHEAD = 7
 SHIFT_CUT = 112
 K_RING = 12
 LEAD = K_AHEAD + SLACK
@@ -58,7 +59,7 @@ RAW_BUFS = 3
 CHUNK_BUFS = 4
 QK_BUFS = 3
 AV_BUFS = 5
-CODES_BUFS = (LAG + LEAD + CHUNK_ROWS) // CHUNK_ROWS + 1
+CODES_BUFS = (LAG + LEAD) // CHUNK_ROWS + 1
 
 
 PROJECTIONS = 3
@@ -224,19 +225,29 @@ def tile_mutliheadattention2d_kernel(
             )
 
         def mx_passes(step):
-            q_row, k_row, v_row = step + Q_AHEAD, step + K_AHEAD, step - LAG + 1
-            if 0 <= q_row < H or 0 <= k_row < H:
-                for_scalar_of[step] = ps_s.tile([P, 2, W], F32, name="for_scalar")
-            if 0 <= q_row < H:
-                by_channel(for_scalar_of[step][:, 0, :], q_row, Q_IDX)
-            if 0 <= k_row < H:
-                by_pixel(for_scalar_of[step][:, 1, :], k_row, w_codes_pl[:, K_IDX, :], w_scales_pl[:, K_IDX, :])
-            if 0 <= step < H or 0 <= v_row < H:
-                for_vector_of[step] = ps_v.tile([P, 2, C_OUT], F32, name="for_vector")
-            if 0 <= step < H:
-                by_pixel(for_vector_of[step][:, 0, :], step, w_codes_pl[:, Q_IDX, :], w_scales_pl[:, Q_IDX, :])
-            if 0 <= v_row < H:
-                by_pixel(for_vector_of[step][:, 1, :], v_row, w_codes[:, V_IDX, :], w_scales[:, V_IDX, :])
+            q_rows = [t for t in (step + Q_AHEAD, step + Q_AHEAD + 1) if 0 <= t < H]
+            k_rows = [t for t in (step + K_AHEAD, step + K_AHEAD + 1) if 0 <= t < H]
+            if q_rows or k_rows:
+                for_scalar_of[step] = ps_s.tile([P, PAIR, 2, W], F32, name="for_scalar")
+            for t in q_rows:
+                by_channel(for_scalar_of[step][:, t % PAIR, 0, :], t, Q_IDX)
+            for t in k_rows:
+                by_pixel(
+                    for_scalar_of[step][:, t % PAIR, 1, :], t, w_codes_pl[:, K_IDX, :], w_scales_pl[:, K_IDX, :]
+                )
+            pair = (step + 1) // PAIR
+            rows = (step + 1, step + 2)
+            if any(0 <= t < H or 0 <= t + 1 - LAG < H for t in rows):
+                for_vector_of[pair] = ps_v.tile([P, PAIR, 2, C_OUT], F32, name="for_vector")
+            for t in rows:
+                if 0 <= t < H:
+                    by_pixel(
+                        for_vector_of[pair][:, t % PAIR, 0, :], t, w_codes_pl[:, Q_IDX, :], w_scales_pl[:, Q_IDX, :]
+                    )
+                if 0 <= t + 1 - LAG < H:
+                    by_pixel(
+                        for_vector_of[pair][:, t % PAIR, 1, :], t + 1 - LAG, w_codes[:, V_IDX, :], w_scales[:, V_IDX, :]
+                    )
 
         def empty_for_scalar(step):
             q_row, k_row = step + Q_AHEAD, step + K_AHEAD
@@ -244,12 +255,12 @@ def tile_mutliheadattention2d_kernel(
                 c, r = divmod(q_row, CHUNK_ROWS)
                 if r == 0:
                     q_rows_of[c] = sbuf[DOUBLE].tile([P, CHUNK_ROWS, W], F32, name="q_rows")
-                nc.scalar.copy(out=q_rows_of[c][:, r, :], in_=for_scalar_of[step][:, 0, :])
+                nc.scalar.copy(out=q_rows_of[c][:, r : r + PAIR, :], in_=for_scalar_of[step][:, :, 0, :])
             if 0 <= k_row < H:
-                nc.scalar.copy(out=k_ring[:, 1, k_row % K_RING, :], in_=for_scalar_of[step][:, 1, :])
-                if k_row % CHUNK_ROWS == CHUNK_ROWS - 1:
-                    last = k_row % K_RING + 1
-                    slots = slice(last - CHUNK_ROWS, last)
+                slot = k_row % K_RING
+                nc.scalar.copy(out=k_ring[:, 1, slot : slot + PAIR, :], in_=for_scalar_of[step][:, :, 1, :])
+                if (k_row + PAIR) % CHUNK_ROWS == 0:
+                    slots = slice(slot + PAIR - CHUNK_ROWS, slot + PAIR)
                     for low, high in ((0, SHIFT_CUT), (SHIFT_CUT, P - 1)):
                         nc.sync.dma_start(
                             out=k_ring[low + 1 : high + 1, 0, slots, :], in_=k_ring[low:high, 1, slots, :]
@@ -297,7 +308,7 @@ def tile_mutliheadattention2d_kernel(
                         "p (i j) o -> p j i o", j=K3
                     ),
                     in0=k_ring[:, :, slot : slot + count, :],
-                    in1=for_vector_of[t][:, 0, :]
+                    in1=for_vector_of[t // PAIR][:, t % PAIR, 0, :]
                     .unsqueeze(1)
                     .unsqueeze(1)
                     .to_broadcast([P, K3, count, C_OUT]),
@@ -418,7 +429,7 @@ def tile_mutliheadattention2d_kernel(
                         out=av_of[t][:, K3 * i : K3 * i + K3, :].rearrange(
                             "p j (g c) -> p j g c", c=CG
                         ),
-                        in0=for_vector_of[s + LAG - 1][:, 1, :]
+                        in0=for_vector_of[(s + LAG - 1) // PAIR][:, (s + LAG - 1) % PAIR, 1, :]
                         .rearrange("p (g c) -> p g c", c=CG)
                         .unsqueeze(1)
                         .to_broadcast([P, K3, GROUPS, CG]),
@@ -458,8 +469,12 @@ def tile_mutliheadattention2d_kernel(
         quantise(0)
         for step in range(-LEAD, LAST + 1):
             source = step - LAG
-            mx_passes(step)
-            empty_for_scalar(step)
+            if step % PAIR == 1:
+                mx_passes(step)
+                for t in (step + Q_AHEAD - PAIR, step + Q_AHEAD - 1):
+                    if 0 <= t < H:
+                        q_dot_rel(t)
+                empty_for_scalar(step)
             if 0 <= step - 1 < H:
                 energy_products(step - 1)
                 fold(step - 1)
@@ -468,8 +483,6 @@ def tile_mutliheadattention2d_kernel(
                 attn_v_products(source)
             if 0 <= source - 2 < H:
                 attn_v_sums(source - 2)
-            if 0 <= step + Q_AHEAD - 1 < H:
-                q_dot_rel(step + Q_AHEAD - 1)
 
             for b in range(BANDS):
                 since = step - b * ROWS

@@ -90,6 +90,12 @@ def tile_mutliheadattention2d_kernel(
         nc.vector.tensor_copy(out=rotate_down[:, 0 : P - 1], in_=ident[:, 1:P])
         nc.vector.tensor_copy(out=rotate_down[:, P - 1 : P], in_=ident[:, 0:1])
         rotate = (rotate_up, ident, rotate_down)
+        flip = sbuf[SINGLE].tile([P, P], F32, name="flip")
+        for r in range(ROWS):
+            nc.vector.tensor_copy(
+                out=flip[:, r * GROUPS : (r + 1) * GROUPS],
+                in_=ident[:, (ROWS - 1 - r) * GROUPS : (ROWS - r) * GROUPS],
+            )
         k_ring = sbuf[SINGLE].tile([P, K3, K_RING, C_OUT], F32, name="k_ring")
         nc.gpsimd.memset(k_ring[:], 0.0)
 
@@ -114,12 +120,6 @@ def tile_mutliheadattention2d_kernel(
             in0=rel9[:].rearrange("p i j -> p (i j)").unsqueeze(2).to_broadcast([P, NWIN, GROUPS]),
             in1=in_group[:].unsqueeze(1).to_broadcast([P, NWIN, GROUPS]),
             op=ALU.mult,
-        )
-
-        rel_wide = sbuf[SINGLE].tile([P, C_OUT], F32, name="rel_wide")
-        nc.vector.memset(rel_wide[:], 0.0)
-        nc.vector.tensor_copy(
-            out=rel_wide[:, 0 : NWIN * GROUPS], in_=rel_by_place[:].rearrange("p n g -> p (n g)")
         )
 
         w_codes = sbuf[SINGLE].tile([P, PROJECTIONS, C_OUT], U32, name="w_codes", align_bytes=64)
@@ -274,9 +274,9 @@ def tile_mutliheadattention2d_kernel(
             if r == 0:
                 qr_of[c] = ps_qr.tile([P, CHUNK_ROWS, C_OUT], F32, name="qr")
             nc.tensor.matmul(
-                out=qr_of[c][:, r, :],
+                out=qr_of[c][:, r, 0 : NWIN * GROUPS],
                 lhsT=q_rows_of[c][:, r, :],
-                rhs=rel_wide[:],
+                rhs=rel_by_place[:].rearrange("p n g -> p (n g)"),
                 start=True,
                 stop=True,
             )
@@ -407,39 +407,42 @@ def tile_mutliheadattention2d_kernel(
 
         def turn_attn(b, i):
             if i == 0:
-                attn_pix_of[b] = sbuf[DOUBLE].tile([P, NWIN, P], F32, name="attn_pix")
+                attn_pix_of[b] = sbuf[DOUBLE].tile([P, ROWS + 1, NWIN, GROUPS], F32, name="attn_pix")
             a_ps = ps_soft.tile([P, K3, P], F32, name="a_ps", tag="soft")
             for j in range(K3):
                 padded_col = 1 - (j - 1)
                 nc.tensor.transpose(
-                    a_ps[:, j, :], attn_rows_of[b][:, K3 * i + j, padded_col : padded_col + W], ident[:]
+                    a_ps[:, j, :], attn_rows_of[b][:, K3 * i + j, padded_col : padded_col + W], flip[:]
                 )
-            nc.scalar.copy(out=attn_pix_of[b][:, K3 * i : K3 * i + K3, :], in_=a_ps[:])
+            nc.scalar.copy(
+                out=attn_pix_of[b][:, 0:ROWS, K3 * i : K3 * i + K3, :].rearrange("p r n g -> p n r g"),
+                in_=a_ps[:].rearrange("p j (r g) -> p j r g", g=GROUPS),
+            )
 
         def attn_v_products(s):
-            if s == 0:
-                av_of[0] = sbuf[AV_BUFS].tile([P, NWIN, C_OUT], F32, name="av")
-            if s + 1 < H:
-                av_of[s + 1] = sbuf[AV_BUFS].tile([P, NWIN, C_OUT], F32, name="av")
-            for i in range(K3):
-                t = s - i + 1
-                if 0 <= t < H:
-                    first_col = (t % ROWS) * GROUPS
-                    nc.vector.tensor_tensor(
-                        out=av_of[t][:, K3 * i : K3 * i + K3, :].rearrange(
-                            "p j (g c) -> p j g c", c=CG
-                        ),
-                        in0=for_vector_of[(s + LAG - 1) // PAIR][:, (s + LAG - 1) % PAIR, 1, :]
-                        .rearrange("p (g c) -> p g c", c=CG)
-                        .unsqueeze(1)
-                        .to_broadcast([P, K3, GROUPS, CG]),
-                        in1=attn_pix_of[t // ROWS][
-                            :, K3 * i : K3 * i + K3, first_col : first_col + GROUPS
-                        ]
-                        .unsqueeze(3)
-                        .to_broadcast([P, K3, GROUPS, CG]),
-                        op=ALU.mult,
-                    )
+            av = sbuf[AV_BUFS].tile([P, K3, K3, C_OUT], F32, name="av")
+            av_of[s] = av
+            window_rows = [i for i in range(K3) if 0 <= s + 1 - i < H]
+            for b in sorted({(s + 1 - i) // ROWS for i in window_rows}, reverse=True):
+                run = [i for i in window_rows if (s + 1 - i) // ROWS == b]
+                first_i, count = run[0], len(run)
+                stride = (NWIN + K3) * GROUPS
+                start = (ROWS - 1 - (s + 1 - first_i) % ROWS) * NWIN * GROUPS + K3 * first_i * GROUPS
+                nc.vector.tensor_tensor(
+                    out=av[:, first_i : first_i + count, :, :].rearrange("p i j (g c) -> p i j g c", c=CG),
+                    in0=for_vector_of[(s + LAG - 1) // PAIR][:, (s + LAG - 1) % PAIR, 1, :]
+                    .rearrange("p (g c) -> p g c", c=CG)
+                    .unsqueeze(1)
+                    .unsqueeze(1)
+                    .to_broadcast([P, count, K3, GROUPS, CG]),
+                    in1=attn_pix_of[b][:]
+                    .rearrange("p r n g -> p (r n g)")[:, start : start + count * stride]
+                    .rearrange("p (i x) -> p i x", x=stride)[:, :, 0 : K3 * GROUPS]
+                    .rearrange("p i (j g) -> p i j g", g=GROUPS)
+                    .unsqueeze(4)
+                    .to_broadcast([P, count, K3, GROUPS, CG]),
+                    op=ALU.mult,
+                )
 
         def attn_v_sums(t):
             places = [K3 * i + j for i in range(K3) if 0 <= t + i - 1 < H for j in range(K3)]
@@ -449,7 +452,7 @@ def tile_mutliheadattention2d_kernel(
             for n in places:
                 nc.tensor.matmul(
                     out=out_ps_of[c][:, r, :],
-                    lhsT=av_of[t][:, n, :],
+                    lhsT=av_of[t + n // K3 - 1][:, n // K3, n % K3, :],
                     rhs=rotate[n % K3][:],
                     is_transpose=True,
                     start=(n == places[0]),

@@ -43,22 +43,26 @@ SHIFT_CUT = 112
 K_RING = 12
 LEAD = K_AHEAD + SLACK
 SUMS_AT = ROWS + SLACK
-MAX_AT = SUMS_AT + NWIN + 1
+FOLDED = NWIN - K3
+PLANES = [CG + 1] * K3 + [CG_HALF + 1] * FOLDED
+SUM_STEPS = 9
+PLANES_A_STEP = -(-sum(PLANES) // SUM_STEPS)
+MAX_AT = SUMS_AT + SUM_STEPS
 SUB_AT = MAX_AT + 1
-EXP_AT = SUB_AT + SLACK
-TOTAL_AT = EXP_AT + K3 + 1
+EXP_AT = SUB_AT + 1
+TOTAL_AT = EXP_AT + K3
 SCALE_AT = TOTAL_AT + 1
 TURN_AT = SCALE_AT + SLACK
 STORE_AT = TURN_AT + K3 - 1
-LAG = TURN_AT + K3 + SLACK
+LAG = TURN_AT + K3 + 1
 LAST = H + LAG + 1
 
 SINGLE = 1
 DOUBLE = 2
-RAW_BUFS = 3
+RAW_BUFS = 2
 CHUNK_BUFS = 4
 QK_BUFS = 3
-AV_BUFS = 5
+AV_BUFS = 4
 CODES_BUFS = (LAG + LEAD) // CHUNK_ROWS + 1
 
 
@@ -77,8 +81,7 @@ def tile_mutliheadattention2d_kernel(
         sbuf = {n: ctx.enter_context(tc.tile_pool(name="sbuf%d" % n, bufs=n)) for n in depths}
         ps_s = ctx.enter_context(tc.psum_pool(name="ps_s", bufs=2))
         ps_v = ctx.enter_context(tc.psum_pool(name="ps_v", bufs=2))
-        ps_qr = ctx.enter_context(tc.psum_pool(name="ps_qr", bufs=1))
-        ps_soft = ctx.enter_context(tc.psum_pool(name="ps_soft", bufs=1))
+        ps_soft = ctx.enter_context(tc.psum_pool(name="ps_soft", bufs=2))
         ps_out = ctx.enter_context(tc.psum_pool(name="ps_out", bufs=2))
 
         ident = sbuf[SINGLE].tile([P, P], F32, name="ident")
@@ -163,6 +166,7 @@ def tile_mutliheadattention2d_kernel(
         qr_pix_of = {}
         qk_of = {}
         folded_of = {}
+        unfolded_of = {}
         e_ps_of = {}
         top_of = {}
         inverse_of = {}
@@ -271,54 +275,61 @@ def tile_mutliheadattention2d_kernel(
 
         def q_dot_rel(t):
             c, r = divmod(t, CHUNK_ROWS)
-            if r == 0:
-                qr_of[c] = ps_qr.tile([P, CHUNK_ROWS, C_OUT], F32, name="qr")
+            if t % PAIR == 0:
+                qr_of[t] = ps_soft.tile([P, PAIR, C_OUT], F32, name="qr", tag="soft")
+            qr = qr_of[t - t % PAIR]
             nc.tensor.matmul(
-                out=qr_of[c][:, r, 0 : NWIN * GROUPS],
+                out=qr[:, t % PAIR, 0 : NWIN * GROUPS],
                 lhsT=q_rows_of[c][:, r, :],
                 rhs=rel_by_place[:].rearrange("p n g -> p (n g)"),
                 start=True,
                 stop=True,
             )
-            if r == CHUNK_ROWS - 1:
-                b, first_row = divmod(c * CHUNK_ROWS, ROWS)
+            if t % PAIR == PAIR - 1:
+                b, first_row = divmod(t + 1 - PAIR, ROWS)
                 if first_row == 0:
                     qr_pix_of[b] = sbuf[DOUBLE].tile([P, NWIN, ROWS, GROUPS], F32, name="qr_pix")
                 nc.scalar.copy(
-                    out=qr_pix_of[b][:, :, first_row : first_row + CHUNK_ROWS, :].rearrange(
-                        "p n r g -> p r n g"
-                    ),
-                    in_=qr_of[c][:, :, 0 : NWIN * GROUPS].rearrange("p r (n g) -> p r n g", g=GROUPS),
+                    out=qr_pix_of[b][:, :, first_row : first_row + PAIR, :].rearrange("p n r g -> p r n g"),
+                    in_=qr[:, :, 0 : NWIN * GROUPS].rearrange("p r (n g) -> p r n g", g=GROUPS),
                 )
 
         def energy_products(t):
-            qk = sbuf[QK_BUFS].tile([P, NWIN, C_OUT], F32, name="qk")
-            qk_of[t] = qk
-            sources = [s for s in (t - 1, t, t + 1) if 0 <= s < H]
+            q = for_vector_of[t // PAIR][:, t % PAIR, 0, :]
+            b, r = divmod(t, ROWS)
+            if r == 0:
+                unfolded_of[b] = sbuf[DOUBLE].tile([P, K3, CG, ROWS, GROUPS], F32, name="unfolded")
             if t == 0:
-                nc.gpsimd.memset(qk[:, 0:K3, :], 0.0)
+                nc.gpsimd.memset(unfolded_of[b][:, :, :, r, :], 0.0)
+            else:
+                nc.vector.tensor_tensor(
+                    out=unfolded_of[b][:, :, :, r, :],
+                    in0=k_ring[:, :, (t - 1) % K_RING, :].rearrange("p j (c g) -> p j c g", g=GROUPS),
+                    in1=q.rearrange("p (c g) -> p c g", g=GROUPS).unsqueeze(1).to_broadcast([P, K3, CG, GROUPS]),
+                    op=ALU.mult,
+                )
+            qk = sbuf[QK_BUFS].tile([P, FOLDED, C_OUT], F32, name="qk")
+            qk_of[t] = qk
+            sources = [s for s in (t, t + 1) if s < H]
             if t == H - 1:
-                nc.gpsimd.memset(qk[:, NWIN - K3 : NWIN, :], 0.0)
+                nc.gpsimd.memset(qk[:, FOLDED - K3 : FOLDED, :], 0.0)
             laps = sorted({s // K_RING for s in sources})
             for run in [[s for s in sources if s // K_RING == lap] for lap in laps]:
-                first_i, count = run[0] - t + 1, len(run)
+                first_i, count = run[0] - t, len(run)
                 slot = run[0] % K_RING
                 nc.vector.tensor_tensor(
                     out=qk[:, K3 * first_i : K3 * (first_i + count), :].rearrange(
                         "p (i j) o -> p j i o", j=K3
                     ),
                     in0=k_ring[:, :, slot : slot + count, :],
-                    in1=for_vector_of[t // PAIR][:, t % PAIR, 0, :]
-                    .unsqueeze(1)
-                    .unsqueeze(1)
-                    .to_broadcast([P, K3, count, C_OUT]),
+                    in1=q.unsqueeze(1).unsqueeze(1).to_broadcast([P, K3, count, C_OUT]),
                     op=ALU.mult,
                 )
 
         def fold(t):
             b, r = divmod(t, ROWS)
             if r == 0:
-                folded_of[b] = sbuf[DOUBLE].tile([P, NWIN, CG_HALF, ROWS, GROUPS], F32, name="folded")
+                folded_of[b] = sbuf[DOUBLE].tile([P, FOLDED, CG_HALF, ROWS, GROUPS], F32, name="folded")
             planes = qk_of[t][:].rearrange("p n (c g) -> p n c g", g=GROUPS)
             nc.gpsimd.tensor_tensor(
                 out=folded_of[b][:, :, :, r, :],
@@ -327,32 +338,33 @@ def tile_mutliheadattention2d_kernel(
                 op=ALU.add,
             )
 
-        def energy_sums(b, n):
-            i, j = divmod(n, K3)
-            if n == 0:
-                energy_of[b] = sbuf[DOUBLE].tile([P, NWIN, W], F32, name="energy")
-            if j == 0:
-                e_ps_of[(b, i)] = ps_soft.tile([P, K3, W], F32, name="e_ps", tag="soft")
-            e_ps = e_ps_of[(b, i)]
-            for plane in range(CG_HALF):
+        planes = [(n, plane) for n in range(NWIN) for plane in range(PLANES[n])]
+
+        def energy_sums(b, part):
+            for n, plane in planes[part * PLANES_A_STEP : (part + 1) * PLANES_A_STEP]:
+                i, j = divmod(n, K3)
+                if n == 0 and plane == 0:
+                    energy_of[b] = sbuf[SINGLE].tile([P, NWIN, W], F32, name="energy")
+                if j == 0 and plane == 0:
+                    e_ps_of[(b, i)] = ps_soft.tile([P, K3, W], F32, name="e_ps", tag="soft")
+                e_ps = e_ps_of[(b, i)]
+                last = plane == PLANES[n] - 1
+                if last:
+                    columns = qr_pix_of[b][:, n, :, :]
+                elif n < K3:
+                    columns = unfolded_of[b][:, n, plane, :, :]
+                else:
+                    columns = folded_of[b][:, n - K3, plane, :, :]
                 nc.tensor.matmul(
                     out=e_ps[:, j, :],
-                    lhsT=folded_of[b][:, n, plane, :, :].rearrange("p r g -> p (r g)"),
+                    lhsT=columns.rearrange("p r g -> p (r g)"),
                     rhs=ident[:],
                     is_transpose=True,
                     start=(plane == 0),
-                    stop=False,
+                    stop=last,
                 )
-            nc.tensor.matmul(
-                out=e_ps[:, j, :],
-                lhsT=qr_pix_of[b][:, n, :, :].rearrange("p r g -> p (r g)"),
-                rhs=ident[:],
-                is_transpose=True,
-                start=False,
-                stop=True,
-            )
-            if j == K3 - 1:
-                nc.scalar.copy(out=energy_of[b][:, K3 * i : K3 * i + K3, :], in_=e_ps[:])
+                if last and j == K3 - 1:
+                    nc.scalar.copy(out=energy_of[b][:, K3 * i : K3 * i + K3, :], in_=e_ps[:])
 
         def window_row(tile, i):
             return tile[:, K3 * i : K3 * i + K3, :]
@@ -459,7 +471,7 @@ def tile_mutliheadattention2d_kernel(
                     stop=(n == places[-1]),
                 )
             if r == CHUNK_ROWS - 1:
-                out_rows = sbuf[DOUBLE].tile([P, CHUNK_ROWS, W], F32, name="out_rows")
+                out_rows = sbuf[SINGLE].tile([P, CHUNK_ROWS, W], F32, name="out_rows")
                 nc.scalar.copy(out=out_rows[:], in_=out_ps_of[c][:])
                 nc.sync.dma_start(
                     out=out[0, :, c * CHUNK_ROWS : (c + 1) * CHUNK_ROWS, :], in_=out_rows[:]
@@ -489,7 +501,7 @@ def tile_mutliheadattention2d_kernel(
 
             for b in range(BANDS):
                 since = step - b * ROWS
-                if SUMS_AT <= since < SUMS_AT + NWIN:
+                if SUMS_AT <= since < SUMS_AT + SUM_STEPS:
                     energy_sums(b, since - SUMS_AT)
                 if since == MAX_AT:
                     softmax_max(b)

@@ -46,24 +46,30 @@ SUMS_AT = ROWS + SLACK
 FOLDED = NWIN - K3
 PLANES = [CG + 1] * K3 + [CG_HALF + 1] * FOLDED
 SUM_STEPS = 9
-PLANES_A_STEP = -(-sum(PLANES) // SUM_STEPS)
+PLANES_A_STEP = [16 if s % PAIR == 0 else 7 for s in range(SUM_STEPS)]
 MAX_AT = SUMS_AT + SUM_STEPS
 SUB_AT = MAX_AT + 1
-EXP_AT = SUB_AT + 1
+EXP_AT = SUB_AT + SLACK
 TOTAL_AT = EXP_AT + K3
 SCALE_AT = TOTAL_AT + 1
 TURN_AT = SCALE_AT + SLACK
-STORE_AT = TURN_AT + K3 - 1
+STORE_AT = TURN_AT + K3 + 1
+STORE_STEPS = 4
 LAG = TURN_AT + K3 + 1
-LAST = H + LAG + 1
+GP_AHEAD = 3
+GP_EVERY = 4
+GP_FIRST_ROW = H + SLACK + GP_AHEAD - LAG
+GP_PHASE = 2
+LAST = H + LAG + 2
 
 SINGLE = 1
 DOUBLE = 2
 RAW_BUFS = 2
+EARLY_TAGS = ("unfolded", "folded")
 CHUNK_BUFS = 4
 QK_BUFS = 3
-AV_BUFS = 4
-CODES_BUFS = (LAG + LEAD) // CHUNK_ROWS + 1
+AV_BUFS = 6
+CODES_BUFS = (LAG + LEAD + PAIR) // CHUNK_ROWS + 1
 
 
 PROJECTIONS = 3
@@ -84,6 +90,99 @@ def tile_mutliheadattention2d_kernel(
         ps_soft = ctx.enter_context(tc.psum_pool(name="ps_soft", bufs=2))
         ps_out = ctx.enter_context(tc.psum_pool(name="ps_out", bufs=2))
 
+        x_by_word = x[0].rearrange("(p e) h w -> p e (h w)", e=PACK)
+
+        raw_of = {}
+        grouped_of = {}
+        codes_of = {}
+        for_scalar_of = {}
+        for_vector_of = {}
+        q_rows_of = {}
+        qr_of = {}
+        qr_pix_of = {}
+        qk_of = {}
+        folded_of = {}
+        unfolded_of = {}
+        e_ps_of = {}
+        top_of = {}
+        inverse_of = {}
+        energy_of = {}
+        attn_store_of = {}
+        attn_rows_of = {}
+        attn_pix_of = {}
+        av_of = {}
+        v_row_of = {}
+        out_ps_of = {}
+
+        def load_x(c, tag="raw"):
+            raw = sbuf[RAW_BUFS].tile([P, PACK, CHUNK], BF16, name="raw", tag=tag)
+            nc.sync.dma_start(out=raw[:], in_=x_by_word[:, :, c * CHUNK : (c + 1) * CHUNK])
+            raw_of[c] = raw
+
+        def regroup(c, r, copy=nc.scalar.copy):
+            if r % PAIR == 0:
+                grouped_of[c] = sbuf[DOUBLE].tile([P, PAIR * W, PACK], BF16, name="grouped", align_bytes=64)
+            first = r % PAIR * W
+            copy(
+                out=grouped_of[c][:, first : first + W, :].rearrange("p (u i) e -> p u e i", i=RUN),
+                in_=raw_of[c][:, :, r * W : (r + 1) * W].rearrange("p e (u i) -> p u e i", i=RUN),
+            )
+
+        def quantise(c, r):
+            if r == 0:
+                codes = sbuf[CODES_BUFS].tile([P, CHUNK], U32, name="codes", align_bytes=64)
+                scales = sbuf[CODES_BUFS].tile([P, CHUNK], U8, name="scales", align_bytes=64)
+                codes_of[c] = (codes, scales)
+            codes, scales = codes_of[c]
+            nc.vector.quantize_mx(
+                out=codes[:, r * W : (r + PAIR) * W].bitcast(FP8X4),
+                scales=scales[:, r * W : (r + PAIR) * W],
+                in_=grouped_of[c][:].rearrange("p w e -> p (w e)"),
+            )
+
+        load_x(0)
+        w_codes = sbuf[SINGLE].tile([P, PROJECTIONS, C_OUT], U32, name="w_codes", align_bytes=64)
+        w_scales = sbuf[SINGLE].tile([P, PROJECTIONS, C_OUT], U8, name="w_scales", align_bytes=64)
+        nc.vector.memset(w_scales[:].rearrange("p a n -> p (a n)").bitcast(I32), 0)
+        for idx, words, scales in (
+            (K_IDX, wk_words, wk_scales), (Q_IDX, wq_words, wq_scales), (V_IDX, wv_words, wv_scales)
+        ):
+            nc.sync.dma_start(
+                out=w_codes[:, idx, :].bitcast(I32),
+                in_=words[0].rearrange("p n e -> p (n e)").bitcast(I32),
+            )
+            for quad in range(QUADRANTS):
+                first_partition = quad * (P // QUADRANTS)
+                nc.sync.dma_start(
+                    out=w_scales[first_partition : first_partition + LIVE, idx, :].bitcast(I32),
+                    in_=scales[0, quad * LIVE : (quad + 1) * LIVE, :].bitcast(I32),
+                )
+
+        k_ring = sbuf[SINGLE].tile([P, K3, K_RING, C_OUT], F32, name="k_ring")
+        for shifted in (0, K3 - 1):
+            nc.gpsimd.memset(k_ring[:, shifted, :, :], 0.0)
+
+        for c in range(1, RAW_BUFS):
+            load_x(c)
+        for c, tag in enumerate(EARLY_TAGS, RAW_BUFS):
+            load_x(c, tag)
+        for r in range(CHUNK_ROWS):
+            regroup(0, r, nc.scalar.copy if r % PAIR else nc.vector.tensor_copy)
+            if r % PAIR == PAIR - 1:
+                quantise(0, r + 1 - PAIR)
+
+        w_codes_pl = sbuf[SINGLE].tile([P, 2, C_OUT], U32, name="w_codes_pl", align_bytes=64)
+        w_scales_pl = sbuf[SINGLE].tile([P, 2, C_OUT], U8, name="w_scales_pl", align_bytes=64)
+        for idx in (K_IDX, Q_IDX):
+            nc.vector.tensor_copy(
+                out=w_codes_pl[:, idx, :].bitcast(I32).rearrange("p (c g) -> p g c", g=GROUPS),
+                in_=w_codes[:, idx, :].bitcast(I32).rearrange("p (g c) -> p g c", c=CG),
+            )
+            nc.vector.tensor_copy(
+                out=w_scales_pl[:, idx, :].rearrange("p (c g) -> p g c", g=GROUPS),
+                in_=w_scales[:, idx, :].rearrange("p (g c) -> p g c", c=CG),
+            )
+
         ident = sbuf[SINGLE].tile([P, P], F32, name="ident")
         make_identity(nc, ident[:])
         rotate_up = sbuf[SINGLE].tile([P, P], F32, name="rotate_up")
@@ -99,8 +198,6 @@ def tile_mutliheadattention2d_kernel(
                 out=flip[:, r * GROUPS : (r + 1) * GROUPS],
                 in_=ident[:, (ROWS - 1 - r) * GROUPS : (ROWS - r) * GROUPS],
             )
-        k_ring = sbuf[SINGLE].tile([P, K3, K_RING, C_OUT], F32, name="k_ring")
-        nc.gpsimd.memset(k_ring[:], 0.0)
 
         half = C_OUT // 2
         rel3 = sbuf[SINGLE].tile([P, K3], BF16, name="rel3")
@@ -124,80 +221,6 @@ def tile_mutliheadattention2d_kernel(
             in1=in_group[:].unsqueeze(1).to_broadcast([P, NWIN, GROUPS]),
             op=ALU.mult,
         )
-
-        w_codes = sbuf[SINGLE].tile([P, PROJECTIONS, C_OUT], U32, name="w_codes", align_bytes=64)
-        w_scales = sbuf[SINGLE].tile([P, PROJECTIONS, C_OUT], U8, name="w_scales", align_bytes=64)
-        nc.vector.memset(w_scales[:].rearrange("p a n -> p (a n)").bitcast(I32), 0)
-        for idx, (words, scales) in enumerate(
-            ((wq_words, wq_scales), (wk_words, wk_scales), (wv_words, wv_scales))
-        ):
-            nc.sync.dma_start(
-                out=w_codes[:, idx, :].bitcast(I32),
-                in_=words[0].rearrange("p n e -> p (n e)").bitcast(I32),
-            )
-            for quad in range(QUADRANTS):
-                first_partition = quad * (P // QUADRANTS)
-                nc.sync.dma_start(
-                    out=w_scales[first_partition : first_partition + LIVE, idx, :].bitcast(I32),
-                    in_=scales[0, quad * LIVE : (quad + 1) * LIVE, :].bitcast(I32),
-                )
-
-        w_codes_pl = sbuf[SINGLE].tile([P, 2, C_OUT], U32, name="w_codes_pl", align_bytes=64)
-        w_scales_pl = sbuf[SINGLE].tile([P, 2, C_OUT], U8, name="w_scales_pl", align_bytes=64)
-        for idx in (Q_IDX, K_IDX):
-            nc.vector.tensor_copy(
-                out=w_codes_pl[:, idx, :].bitcast(I32).rearrange("p (c g) -> p g c", g=GROUPS),
-                in_=w_codes[:, idx, :].bitcast(I32).rearrange("p (g c) -> p g c", c=CG),
-            )
-            nc.vector.tensor_copy(
-                out=w_scales_pl[:, idx, :].rearrange("p (c g) -> p g c", g=GROUPS),
-                in_=w_scales[:, idx, :].rearrange("p (g c) -> p g c", c=CG),
-            )
-
-        x_by_word = x[0].rearrange("(p e) h w -> p e (h w)", e=PACK)
-
-        raw_of = {}
-        grouped_of = {}
-        codes_of = {}
-        for_scalar_of = {}
-        for_vector_of = {}
-        q_rows_of = {}
-        qr_of = {}
-        qr_pix_of = {}
-        qk_of = {}
-        folded_of = {}
-        unfolded_of = {}
-        e_ps_of = {}
-        top_of = {}
-        inverse_of = {}
-        energy_of = {}
-        attn_rows_of = {}
-        attn_pix_of = {}
-        av_of = {}
-        out_ps_of = {}
-
-        def load_x(c):
-            raw = sbuf[RAW_BUFS].tile([P, PACK, CHUNK], BF16, name="raw")
-            nc.sync.dma_start(out=raw[:], in_=x_by_word[:, :, c * CHUNK : (c + 1) * CHUNK])
-            raw_of[c] = raw
-
-        def regroup(c, r):
-            if r == 0:
-                grouped_of[c] = sbuf[DOUBLE].tile([P, CHUNK, PACK], BF16, name="grouped", align_bytes=64)
-            nc.scalar.copy(
-                out=grouped_of[c][:, r * W : (r + 1) * W, :].rearrange("p (u i) e -> p u e i", i=RUN),
-                in_=raw_of[c][:, :, r * W : (r + 1) * W].rearrange("p e (u i) -> p u e i", i=RUN),
-            )
-
-        def quantise(c):
-            codes = sbuf[CODES_BUFS].tile([P, CHUNK], U32, name="codes", align_bytes=64)
-            scales = sbuf[CODES_BUFS].tile([P, CHUNK], U8, name="scales", align_bytes=64)
-            nc.vector.quantize_mx(
-                out=codes[:].bitcast(FP8X4),
-                scales=scales[:],
-                in_=grouped_of[c][:].rearrange("p w e -> p (w e)"),
-            )
-            codes_of[c] = (codes, scales)
 
         def x_row(t):
             codes, scales = codes_of[t // CHUNK_ROWS]
@@ -228,6 +251,21 @@ def tile_mutliheadattention2d_kernel(
                 stop=True,
             )
 
+        def on_gpsimd(s):
+            return GP_FIRST_ROW <= s < H and s % GP_EVERY == GP_PHASE
+
+        def v_for_vector(t):
+            s = t + 1 - LAG
+            return s if 0 <= s < H and not on_gpsimd(s) else None
+
+        def v_for_gpsimd(step):
+            for s in (step + 1 + GP_AHEAD - LAG, step + 2 + GP_AHEAD - LAG):
+                if on_gpsimd(s):
+                    v_ps = ps_s.tile([P, C_OUT], F32, name="v_ps", tag="for_scalar")
+                    by_pixel(v_ps[:], s, w_codes[:, V_IDX, :], w_scales[:, V_IDX, :])
+                    v_row_of[s] = sbuf[DOUBLE].tile([P, C_OUT], F32, name="v_row")
+                    nc.scalar.copy(out=v_row_of[s][:], in_=v_ps[:])
+
         def mx_passes(step):
             q_rows = [t for t in (step + Q_AHEAD, step + Q_AHEAD + 1) if 0 <= t < H]
             k_rows = [t for t in (step + K_AHEAD, step + K_AHEAD + 1) if 0 <= t < H]
@@ -241,30 +279,29 @@ def tile_mutliheadattention2d_kernel(
                 )
             pair = (step + 1) // PAIR
             rows = (step + 1, step + 2)
-            if any(0 <= t < H or 0 <= t + 1 - LAG < H for t in rows):
+            if any(0 <= t < H or v_for_vector(t) is not None for t in rows):
                 for_vector_of[pair] = ps_v.tile([P, PAIR, 2, C_OUT], F32, name="for_vector")
             for t in rows:
                 if 0 <= t < H:
                     by_pixel(
                         for_vector_of[pair][:, t % PAIR, 0, :], t, w_codes_pl[:, Q_IDX, :], w_scales_pl[:, Q_IDX, :]
                     )
-                if 0 <= t + 1 - LAG < H:
-                    by_pixel(
-                        for_vector_of[pair][:, t % PAIR, 1, :], t + 1 - LAG, w_codes[:, V_IDX, :], w_scales[:, V_IDX, :]
-                    )
+                s = v_for_vector(t)
+                if s is not None:
+                    by_pixel(for_vector_of[pair][:, t % PAIR, 1, :], s, w_codes[:, V_IDX, :], w_scales[:, V_IDX, :])
+            v_for_gpsimd(step)
 
         def empty_for_scalar(step):
             q_row, k_row = step + Q_AHEAD, step + K_AHEAD
             if 0 <= q_row < H:
-                c, r = divmod(q_row, CHUNK_ROWS)
-                if r == 0:
-                    q_rows_of[c] = sbuf[DOUBLE].tile([P, CHUNK_ROWS, W], F32, name="q_rows")
-                nc.scalar.copy(out=q_rows_of[c][:, r : r + PAIR, :], in_=for_scalar_of[step][:, :, 0, :])
+                q_rows_of[q_row] = sbuf[DOUBLE].tile([P, PAIR, W], F32, name="q_rows")
+                nc.scalar.copy(out=q_rows_of[q_row][:], in_=for_scalar_of[step][:, :, 0, :])
             if 0 <= k_row < H:
                 slot = k_row % K_RING
                 nc.scalar.copy(out=k_ring[:, 1, slot : slot + PAIR, :], in_=for_scalar_of[step][:, :, 1, :])
-                if (k_row + PAIR) % CHUNK_ROWS == 0:
-                    slots = slice(slot + PAIR - CHUNK_ROWS, slot + PAIR)
+                shifted_rows = PAIR if k_row < CHUNK_ROWS else CHUNK_ROWS
+                if (k_row + PAIR) % shifted_rows == 0:
+                    slots = slice(slot + PAIR - shifted_rows, slot + PAIR)
                     for low, high in ((0, SHIFT_CUT), (SHIFT_CUT, P - 1)):
                         nc.sync.dma_start(
                             out=k_ring[low + 1 : high + 1, 0, slots, :], in_=k_ring[low:high, 1, slots, :]
@@ -274,13 +311,12 @@ def tile_mutliheadattention2d_kernel(
                         )
 
         def q_dot_rel(t):
-            c, r = divmod(t, CHUNK_ROWS)
             if t % PAIR == 0:
                 qr_of[t] = ps_soft.tile([P, PAIR, C_OUT], F32, name="qr", tag="soft")
             qr = qr_of[t - t % PAIR]
             nc.tensor.matmul(
                 out=qr[:, t % PAIR, 0 : NWIN * GROUPS],
-                lhsT=q_rows_of[c][:, r, :],
+                lhsT=q_rows_of[t - t % PAIR][:, t % PAIR, :],
                 rhs=rel_by_place[:].rearrange("p n g -> p (n g)"),
                 start=True,
                 stop=True,
@@ -341,7 +377,8 @@ def tile_mutliheadattention2d_kernel(
         planes = [(n, plane) for n in range(NWIN) for plane in range(PLANES[n])]
 
         def energy_sums(b, part):
-            for n, plane in planes[part * PLANES_A_STEP : (part + 1) * PLANES_A_STEP]:
+            first = sum(PLANES_A_STEP[:part])
+            for n, plane in planes[first : first + PLANES_A_STEP[part]]:
                 i, j = divmod(n, K3)
                 if n == 0 and plane == 0:
                     energy_of[b] = sbuf[SINGLE].tile([P, NWIN, W], F32, name="energy")
@@ -407,15 +444,19 @@ def tile_mutliheadattention2d_kernel(
                 op=ALU.mult,
             )
 
-        def store_attn(b):
-            attn_store = sbuf[SINGLE].tile([P, W, NWIN], F32, name="attn_store")
+        def store_attn(b, part):
+            if part == 0:
+                attn_store_of[b] = sbuf[SINGLE].tile([P, W, NWIN], F32, name="attn_store")
+            first, last = part * W // STORE_STEPS, (part + 1) * W // STORE_STEPS
             nc.scalar.copy(
-                out=attn_store[:], in_=attn_rows_of[b][:, :, 1 : W + 1].rearrange("p n w -> p w n")
+                out=attn_store_of[b][:, first:last, :],
+                in_=attn_rows_of[b][:, :, 1 + first : 1 + last].rearrange("p n w -> p w n"),
             )
-            nc.sync.dma_start(
-                out=attn[0, :, b * ROWS : (b + 1) * ROWS, :, :].rearrange("g h w n -> h g (w n)"),
-                in_=attn_store[:].rearrange("p w n -> p (w n)"),
-            )
+            if part == STORE_STEPS - 1:
+                nc.sync.dma_start(
+                    out=attn[0, :, b * ROWS : (b + 1) * ROWS, :, :].rearrange("g h w n -> h g (w n)"),
+                    in_=attn_store_of[b][:].rearrange("p w n -> p (w n)"),
+                )
 
         def turn_attn(b, i):
             if i == 0:
@@ -432,7 +473,13 @@ def tile_mutliheadattention2d_kernel(
             )
 
         def attn_v_products(s):
-            av = sbuf[AV_BUFS].tile([P, K3, K3, C_OUT], F32, name="av")
+            if on_gpsimd(s):
+                tag = ("unfolded", "folded")[s // GP_EVERY % 2]
+                av = sbuf[DOUBLE].tile([P, K3, K3, C_OUT], F32, name="av_gp", tag=tag)
+                multiply, v = nc.gpsimd.tensor_tensor, v_row_of[s][:]
+            else:
+                av = sbuf[AV_BUFS].tile([P, K3, K3, C_OUT], F32, name="av")
+                multiply, v = nc.vector.tensor_tensor, for_vector_of[(s + LAG - 1) // PAIR][:, (s + LAG - 1) % PAIR, 1, :]
             av_of[s] = av
             window_rows = [i for i in range(K3) if 0 <= s + 1 - i < H]
             for b in sorted({(s + 1 - i) // ROWS for i in window_rows}, reverse=True):
@@ -440,10 +487,9 @@ def tile_mutliheadattention2d_kernel(
                 first_i, count = run[0], len(run)
                 stride = (NWIN + K3) * GROUPS
                 start = (ROWS - 1 - (s + 1 - first_i) % ROWS) * NWIN * GROUPS + K3 * first_i * GROUPS
-                nc.vector.tensor_tensor(
+                multiply(
                     out=av[:, first_i : first_i + count, :, :].rearrange("p i j (g c) -> p i j g c", c=CG),
-                    in0=for_vector_of[(s + LAG - 1) // PAIR][:, (s + LAG - 1) % PAIR, 1, :]
-                    .rearrange("p (g c) -> p g c", c=CG)
+                    in0=v.rearrange("p (g c) -> p g c", c=CG)
                     .unsqueeze(1)
                     .unsqueeze(1)
                     .to_broadcast([P, count, K3, GROUPS, CG]),
@@ -470,20 +516,29 @@ def tile_mutliheadattention2d_kernel(
                     start=(n == places[0]),
                     stop=(n == places[-1]),
                 )
-            if r == CHUNK_ROWS - 1:
-                out_rows = sbuf[SINGLE].tile([P, CHUNK_ROWS, W], F32, name="out_rows")
-                nc.scalar.copy(out=out_rows[:], in_=out_ps_of[c][:])
-                nc.sync.dma_start(
-                    out=out[0, :, c * CHUNK_ROWS : (c + 1) * CHUNK_ROWS, :], in_=out_rows[:]
-                )
 
-        for c in range(RAW_BUFS):
-            load_x(c)
-        for r in range(CHUNK_ROWS):
-            regroup(0, r)
-        quantise(0)
+        def store_out(c):
+            out_rows = sbuf[SINGLE].tile([P, CHUNK_ROWS, W], F32, name="out_rows")
+            nc.scalar.copy(out=out_rows[:], in_=out_ps_of[c][:])
+            nc.sync.dma_start(out=out[0, :, c * CHUNK_ROWS : (c + 1) * CHUNK_ROWS, :], in_=out_rows[:])
+
+        ctx.enter_context(tc.manual_schedule(engines={mybir.EngineType.Activation, mybir.EngineType.Pool}))
         for step in range(-LEAD, LAST + 1):
             source = step - LAG
+            if 0 <= source - 3 < H and (source - 3) % CHUNK_ROWS == CHUNK_ROWS - 1:
+                store_out((source - 3) // CHUNK_ROWS)
+
+            c, stage = divmod(step + LEAD, CHUNK_ROWS)
+            if stage == 0:
+                if 1 <= c < CHUNKS:
+                    quantise(c, PAIR)
+                if RAW_BUFS + len(EARLY_TAGS) <= c + RAW_BUFS < CHUNKS:
+                    load_x(c + RAW_BUFS)
+            if stage == PAIR and c + 1 < CHUNKS:
+                quantise(c + 1, 0)
+            if c + 1 < CHUNKS:
+                regroup(c + 1, stage)
+
             if step % PAIR == 1:
                 mx_passes(step)
                 for t in (step + Q_AHEAD - PAIR, step + Q_AHEAD - 1):
@@ -494,7 +549,7 @@ def tile_mutliheadattention2d_kernel(
                 energy_products(step - 1)
                 fold(step - 1)
 
-            if 0 <= source < H:
+            if 0 <= source < H and not on_gpsimd(source):
                 attn_v_products(source)
             if 0 <= source - 2 < H:
                 attn_v_sums(source - 2)
@@ -515,14 +570,7 @@ def tile_mutliheadattention2d_kernel(
                     softmax_scale(b, since - SCALE_AT)
                 if TURN_AT <= since < TURN_AT + K3:
                     turn_attn(b, since - TURN_AT)
-                if since == STORE_AT:
-                    store_attn(b)
-
-            c, stage = divmod(step + LEAD, CHUNK_ROWS)
-            if stage == 0:
-                if 1 <= c < CHUNKS:
-                    quantise(c)
-                if c + RAW_BUFS < CHUNKS:
-                    load_x(c + RAW_BUFS)
-            if c + 1 < CHUNKS:
-                regroup(c + 1, stage)
+                if STORE_AT <= since < STORE_AT + STORE_STEPS:
+                    store_attn(b, since - STORE_AT)
+            if on_gpsimd(source + GP_AHEAD):
+                attn_v_products(source + GP_AHEAD)

@@ -41,7 +41,7 @@ Q_AHEAD = 5
 K_AHEAD = 7
 SHIFT_CUT = 112
 K_RING = 12
-LEAD = K_AHEAD + SLACK
+LEAD = K_AHEAD
 SUMS_AT = ROWS + SLACK
 FOLDED = NWIN - K3
 PLANES = [CG + 1] * K3 + [CG_HALF + 1] * FOLDED
@@ -51,7 +51,8 @@ MAX_AT = SUMS_AT + SUM_STEPS
 SUB_AT = MAX_AT + 1
 EXP_AT = SUB_AT + SLACK
 TOTAL_AT = EXP_AT + K3
-SCALE_AT = TOTAL_AT + 1
+INVERSE_AT = TOTAL_AT + 1
+SCALE_AT = INVERSE_AT + 1
 TURN_AT = SCALE_AT + SLACK
 STORE_AT = TURN_AT + K3 + 1
 STORE_STEPS = 4
@@ -105,6 +106,7 @@ def tile_mutliheadattention2d_kernel(
         unfolded_of = {}
         e_ps_of = {}
         top_of = {}
+        total_of = {}
         inverse_of = {}
         energy_of = {}
         attn_store_of = {}
@@ -263,7 +265,7 @@ def tile_mutliheadattention2d_kernel(
                 if on_gpsimd(s):
                     v_ps = ps_s.tile([P, C_OUT], F32, name="v_ps", tag="for_scalar")
                     by_pixel(v_ps[:], s, w_codes[:, V_IDX, :], w_scales[:, V_IDX, :])
-                    v_row_of[s] = sbuf[DOUBLE].tile([P, C_OUT], F32, name="v_row")
+                    v_row_of[s] = sbuf[SINGLE].tile([P, C_OUT], F32, name="v_row")
                     nc.scalar.copy(out=v_row_of[s][:], in_=v_ps[:])
 
         def mx_passes(step):
@@ -407,17 +409,21 @@ def tile_mutliheadattention2d_kernel(
             return tile[:, K3 * i : K3 * i + K3, :]
 
         def softmax_max(b):
-            top = sbuf[SINGLE].tile([P, W], F32, name="top")
-            nc.vector.tensor_reduce(
-                out=top[:], in_=energy_of[b][:].rearrange("p n w -> p w n"), axis=AXIS_X, op=ALU.max
-            )
-            top_of[b] = top
+            tops = sbuf[SINGLE].tile([P, NWIN // 2, W], F32, name="tops")
+            energy = energy_of[b]
+            half = NWIN // 2
+            nc.vector.tensor_max(tops[:], energy[:, 0:half, :], energy[:, half : 2 * half, :])
+            while half > 1:
+                half //= 2
+                nc.vector.tensor_max(tops[:, 0:half, :], tops[:, 0:half, :], tops[:, half : 2 * half, :])
+            nc.vector.tensor_max(tops[:, 0, :], tops[:, 0, :], energy[:, NWIN - 1, :])
+            top_of[b] = tops
 
         def softmax_subtract(b, i):
             nc.gpsimd.tensor_tensor(
                 out=window_row(energy_of[b], i),
                 in0=window_row(energy_of[b], i),
-                in1=top_of[b][:].unsqueeze(1).to_broadcast([P, K3, W]),
+                in1=top_of[b][:, 0:1, :].to_broadcast([P, K3, W]),
                 op=ALU.subtract,
             )
 
@@ -425,13 +431,19 @@ def tile_mutliheadattention2d_kernel(
             nc.scalar.activation(out=window_row(energy_of[b], i), in_=window_row(energy_of[b], i), func=EXP)
 
         def softmax_total(b):
-            total = sbuf[SINGLE].tile([P, W], F32, name="total")
-            nc.vector.tensor_reduce(
-                out=total[:], in_=energy_of[b][:].rearrange("p n w -> p w n"), axis=AXIS_X, op=ALU.add
-            )
-            inverse = sbuf[SINGLE].tile([P, W], F32, name="inverse")
-            nc.vector.reciprocal(out=inverse[:], in_=total[:])
-            inverse_of[b] = inverse
+            total_of[b] = ps_soft.tile([P, W], F32, name="total", tag="soft")
+            for n in range(NWIN):
+                nc.tensor.matmul(
+                    out=total_of[b][:],
+                    lhsT=ident[:],
+                    rhs=energy_of[b][:, n, :],
+                    start=(n == 0),
+                    stop=(n == NWIN - 1),
+                )
+
+        def softmax_inverse(b):
+            inverse_of[b] = sbuf[SINGLE].tile([P, W], F32, name="inverse")
+            nc.vector.reciprocal(out=inverse_of[b][:], in_=total_of[b][:])
 
         def softmax_scale(b, i):
             if i == 0:
@@ -566,6 +578,8 @@ def tile_mutliheadattention2d_kernel(
                     softmax_exp(b, since - EXP_AT)
                 if since == TOTAL_AT:
                     softmax_total(b)
+                if since == INVERSE_AT:
+                    softmax_inverse(b)
                 if SCALE_AT <= since < SCALE_AT + K3:
                     softmax_scale(b, since - SCALE_AT)
                 if TURN_AT <= since < TURN_AT + K3:

@@ -40,6 +40,7 @@ PAIR = 2
 Q_AHEAD = 5
 K_AHEAD = 7
 SHIFT_CUT = 112
+ATTN_RING = 2 * ROWS
 K_RING = 12
 LEAD = K_AHEAD
 SUMS_AT = ROWS + SLACK
@@ -57,10 +58,6 @@ TURN_AT = SCALE_AT + SLACK
 STORE_AT = TURN_AT + K3 + 1
 STORE_STEPS = 4
 LAG = TURN_AT + K3 + 1
-GP_AHEAD = 3
-GP_EVERY = 4
-GP_FIRST_ROW = H + SLACK + GP_AHEAD - LAG
-GP_PHASE = 2
 LAST = H + LAG + 2
 
 SINGLE = 1
@@ -111,9 +108,7 @@ def tile_mutliheadattention2d_kernel(
         energy_of = {}
         attn_store_of = {}
         attn_rows_of = {}
-        attn_pix_of = {}
         av_of = {}
-        v_row_of = {}
         out_ps_of = {}
 
         def load_x(c, tag="raw"):
@@ -130,7 +125,7 @@ def tile_mutliheadattention2d_kernel(
                 in_=raw_of[c][:, :, r * W : (r + 1) * W].rearrange("p e (u i) -> p u e i", i=RUN),
             )
 
-        def quantise(c, r):
+        def quantise(c, r, grouped):
             if r == 0:
                 codes = sbuf[CODES_BUFS].tile([P, CHUNK], U32, name="codes", align_bytes=64)
                 scales = sbuf[CODES_BUFS].tile([P, CHUNK], U8, name="scales", align_bytes=64)
@@ -139,16 +134,23 @@ def tile_mutliheadattention2d_kernel(
             nc.vector.quantize_mx(
                 out=codes[:, r * W : (r + PAIR) * W].bitcast(FP8X4),
                 scales=scales[:, r * W : (r + PAIR) * W],
-                in_=grouped_of[c][:].rearrange("p w e -> p (w e)"),
+                in_=grouped[:].rearrange("p w e -> p (w e)"),
             )
 
         load_x(0)
         w_codes = sbuf[SINGLE].tile([P, PROJECTIONS, C_OUT], U32, name="w_codes", align_bytes=64)
         w_scales = sbuf[SINGLE].tile([P, PROJECTIONS, C_OUT], U8, name="w_scales", align_bytes=64)
         nc.vector.memset(w_scales[:].rearrange("p a n -> p (a n)").bitcast(I32), 0)
+        half = C_OUT // 2
+        rel3 = sbuf[SINGLE].tile([P, K3], BF16, name="rel3")
         for idx, words, scales in (
             (K_IDX, wk_words, wk_scales), (Q_IDX, wq_words, wq_scales), (V_IDX, wv_words, wv_scales)
         ):
+            if idx == Q_IDX:
+                nc.sync.dma_start(out=rel3[0:half, :], in_=rel_t)
+                nc.sync.dma_start(out=rel3[half:P, :], in_=rel_f)
+            if idx == V_IDX:
+                load_x(1)
             nc.sync.dma_start(
                 out=w_codes[:, idx, :].bitcast(I32),
                 in_=words[0].rearrange("p n e -> p (n e)").bitcast(I32),
@@ -160,18 +162,23 @@ def tile_mutliheadattention2d_kernel(
                     in_=scales[0, quad * LIVE : (quad + 1) * LIVE, :].bitcast(I32),
                 )
 
+        wide = sbuf[SINGLE].tile([P, 1 + P + 1], F32, name="wide")
+        ident = wide[:, 1 : 1 + P]
+        make_identity(nc, ident)
+        nc.gpsimd.tensor_copy(out=wide[:, 0:1], in_=wide[:, P : P + 1])
+        nc.gpsimd.tensor_copy(out=wide[:, P + 1 : P + 2], in_=wide[:, 1:2])
+        rotate = [wide[:, j : j + P] for j in range(K3)]
+
         k_ring = sbuf[SINGLE].tile([P, K3, K_RING, C_OUT], F32, name="k_ring")
         for shifted in (0, K3 - 1):
             nc.gpsimd.memset(k_ring[:, shifted, :, :], 0.0)
 
-        for c in range(1, RAW_BUFS):
-            load_x(c)
         for c, tag in enumerate(EARLY_TAGS, RAW_BUFS):
             load_x(c, tag)
         for r in range(CHUNK_ROWS):
             regroup(0, r, nc.scalar.copy if r % PAIR else nc.vector.tensor_copy)
             if r % PAIR == PAIR - 1:
-                quantise(0, r + 1 - PAIR)
+                quantise(0, r + 1 - PAIR, grouped_of[0])
 
         w_codes_pl = sbuf[SINGLE].tile([P, 2, C_OUT], U32, name="w_codes_pl", align_bytes=64)
         w_scales_pl = sbuf[SINGLE].tile([P, 2, C_OUT], U8, name="w_scales_pl", align_bytes=64)
@@ -185,26 +192,6 @@ def tile_mutliheadattention2d_kernel(
                 in_=w_scales[:, idx, :].rearrange("p (g c) -> p g c", c=CG),
             )
 
-        ident = sbuf[SINGLE].tile([P, P], F32, name="ident")
-        make_identity(nc, ident[:])
-        rotate_up = sbuf[SINGLE].tile([P, P], F32, name="rotate_up")
-        nc.vector.tensor_copy(out=rotate_up[:, 1:P], in_=ident[:, 0 : P - 1])
-        nc.vector.tensor_copy(out=rotate_up[:, 0:1], in_=ident[:, P - 1 : P])
-        rotate_down = sbuf[SINGLE].tile([P, P], F32, name="rotate_down")
-        nc.vector.tensor_copy(out=rotate_down[:, 0 : P - 1], in_=ident[:, 1:P])
-        nc.vector.tensor_copy(out=rotate_down[:, P - 1 : P], in_=ident[:, 0:1])
-        rotate = (rotate_up, ident, rotate_down)
-        flip = sbuf[SINGLE].tile([P, P], F32, name="flip")
-        for r in range(ROWS):
-            nc.vector.tensor_copy(
-                out=flip[:, r * GROUPS : (r + 1) * GROUPS],
-                in_=ident[:, (ROWS - 1 - r) * GROUPS : (ROWS - r) * GROUPS],
-            )
-
-        half = C_OUT // 2
-        rel3 = sbuf[SINGLE].tile([P, K3], BF16, name="rel3")
-        nc.sync.dma_start(out=rel3[0:half, :], in_=rel_t)
-        nc.sync.dma_start(out=rel3[half:P, :], in_=rel_f)
         rel9 = sbuf[SINGLE].tile([P, K3, K3], F32, name="rel9")
         nc.vector.tensor_copy(
             out=rel9[0:half], in_=rel3[0:half, :].unsqueeze(2).to_broadcast([half, K3, K3])
@@ -214,7 +201,7 @@ def tile_mutliheadattention2d_kernel(
         )
         in_group = sbuf[SINGLE].tile([P, GROUPS], F32, name="in_group")
         nc.vector.tensor_reduce(
-            out=in_group[:], in_=ident[:].rearrange("p (g c) -> p g c", c=CG), axis=AXIS_X, op=ALU.add
+            out=in_group[:], in_=ident.rearrange("p (g c) -> p g c", c=CG), axis=AXIS_X, op=ALU.add
         )
         rel_by_place = sbuf[SINGLE].tile([P, NWIN, GROUPS], F32, name="rel_by_place")
         nc.vector.tensor_tensor(
@@ -253,21 +240,6 @@ def tile_mutliheadattention2d_kernel(
                 stop=True,
             )
 
-        def on_gpsimd(s):
-            return GP_FIRST_ROW <= s < H and s % GP_EVERY == GP_PHASE
-
-        def v_for_vector(t):
-            s = t + 1 - LAG
-            return s if 0 <= s < H and not on_gpsimd(s) else None
-
-        def v_for_gpsimd(step):
-            for s in (step + 1 + GP_AHEAD - LAG, step + 2 + GP_AHEAD - LAG):
-                if on_gpsimd(s):
-                    v_ps = ps_s.tile([P, C_OUT], F32, name="v_ps", tag="for_scalar")
-                    by_pixel(v_ps[:], s, w_codes[:, V_IDX, :], w_scales[:, V_IDX, :])
-                    v_row_of[s] = sbuf[SINGLE].tile([P, C_OUT], F32, name="v_row")
-                    nc.scalar.copy(out=v_row_of[s][:], in_=v_ps[:])
-
         def mx_passes(step):
             q_rows = [t for t in (step + Q_AHEAD, step + Q_AHEAD + 1) if 0 <= t < H]
             k_rows = [t for t in (step + K_AHEAD, step + K_AHEAD + 1) if 0 <= t < H]
@@ -281,17 +253,16 @@ def tile_mutliheadattention2d_kernel(
                 )
             pair = (step + 1) // PAIR
             rows = (step + 1, step + 2)
-            if any(0 <= t < H or v_for_vector(t) is not None for t in rows):
+            if any(0 <= t < H or 0 <= t + 1 - LAG < H for t in rows):
                 for_vector_of[pair] = ps_v.tile([P, PAIR, 2, C_OUT], F32, name="for_vector")
             for t in rows:
                 if 0 <= t < H:
                     by_pixel(
                         for_vector_of[pair][:, t % PAIR, 0, :], t, w_codes_pl[:, Q_IDX, :], w_scales_pl[:, Q_IDX, :]
                     )
-                s = v_for_vector(t)
-                if s is not None:
+                s = t + 1 - LAG
+                if 0 <= s < H:
                     by_pixel(for_vector_of[pair][:, t % PAIR, 1, :], s, w_codes[:, V_IDX, :], w_scales[:, V_IDX, :])
-            v_for_gpsimd(step)
 
         def empty_for_scalar(step):
             q_row, k_row = step + Q_AHEAD, step + K_AHEAD
@@ -397,7 +368,7 @@ def tile_mutliheadattention2d_kernel(
                 nc.tensor.matmul(
                     out=e_ps[:, j, :],
                     lhsT=columns.rearrange("p r g -> p (r g)"),
-                    rhs=ident[:],
+                    rhs=ident,
                     is_transpose=True,
                     start=(plane == 0),
                     stop=last,
@@ -435,15 +406,15 @@ def tile_mutliheadattention2d_kernel(
             for n in range(NWIN):
                 nc.tensor.matmul(
                     out=total_of[b][:],
-                    lhsT=ident[:],
+                    lhsT=ident,
                     rhs=energy_of[b][:, n, :],
                     start=(n == 0),
                     stop=(n == NWIN - 1),
                 )
 
         def softmax_inverse(b):
-            inverse_of[b] = sbuf[SINGLE].tile([P, W], F32, name="inverse")
-            nc.vector.reciprocal(out=inverse_of[b][:], in_=total_of[b][:])
+            inverse_of[b] = top_of[b][:, 1:2, :]
+            nc.vector.reciprocal(out=top_of[b][:, 1, :], in_=total_of[b][:])
 
         def softmax_scale(b, i):
             if i == 0:
@@ -452,7 +423,7 @@ def tile_mutliheadattention2d_kernel(
             nc.gpsimd.tensor_tensor(
                 out=window_row(attn_rows_of[b], i)[:, :, 1 : W + 1],
                 in0=window_row(energy_of[b], i),
-                in1=inverse_of[b][:].unsqueeze(1).to_broadcast([P, K3, W]),
+                in1=inverse_of[b].to_broadcast([P, K3, W]),
                 op=ALU.mult,
             )
 
@@ -470,49 +441,41 @@ def tile_mutliheadattention2d_kernel(
                     in_=attn_store_of[b][:].rearrange("p w n -> p (w n)"),
                 )
 
+        attn_ring = sbuf[SINGLE].tile([P, ATTN_RING, NWIN, GROUPS], F32, name="attn_ring")
+
         def turn_attn(b, i):
-            if i == 0:
-                attn_pix_of[b] = sbuf[DOUBLE].tile([P, ROWS + 1, NWIN, GROUPS], F32, name="attn_pix")
             a_ps = ps_soft.tile([P, K3, P], F32, name="a_ps", tag="soft")
             for j in range(K3):
                 padded_col = 1 - (j - 1)
                 nc.tensor.transpose(
-                    a_ps[:, j, :], attn_rows_of[b][:, K3 * i + j, padded_col : padded_col + W], flip[:]
+                    a_ps[:, j, :], attn_rows_of[b][:, K3 * i + j, padded_col : padded_col + W], ident
                 )
-            nc.scalar.copy(
-                out=attn_pix_of[b][:, 0:ROWS, K3 * i : K3 * i + K3, :].rearrange("p r n g -> p n r g"),
-                in_=a_ps[:].rearrange("p j (r g) -> p j r g", g=GROUPS),
-            )
+            first = b * ROWS + i - 1
+            sources = [s for s in range(first, first + ROWS) if 0 <= s < H]
+            for lap in sorted({s // ATTN_RING for s in sources}):
+                run = [s for s in sources if s // ATTN_RING == lap]
+                slot, row = run[0] % ATTN_RING, run[0] - first
+                nc.scalar.copy(
+                    out=attn_ring[:, slot : slot + len(run), K3 * i : K3 * i + K3, :].rearrange("p r n g -> p n r g"),
+                    in_=a_ps[:].rearrange("p j (r g) -> p j r g", g=GROUPS)[:, :, row : row + len(run), :],
+                )
 
         def attn_v_products(s):
-            if on_gpsimd(s):
-                tag = ("unfolded", "folded")[s // GP_EVERY % 2]
-                av = sbuf[DOUBLE].tile([P, K3, K3, C_OUT], F32, name="av_gp", tag=tag)
-                multiply, v = nc.gpsimd.tensor_tensor, v_row_of[s][:]
-            else:
-                av = sbuf[AV_BUFS].tile([P, K3, K3, C_OUT], F32, name="av")
-                multiply, v = nc.vector.tensor_tensor, for_vector_of[(s + LAG - 1) // PAIR][:, (s + LAG - 1) % PAIR, 1, :]
+            av = sbuf[AV_BUFS].tile([P, K3, K3, C_OUT], F32, name="av")
             av_of[s] = av
             window_rows = [i for i in range(K3) if 0 <= s + 1 - i < H]
-            for b in sorted({(s + 1 - i) // ROWS for i in window_rows}, reverse=True):
-                run = [i for i in window_rows if (s + 1 - i) // ROWS == b]
-                first_i, count = run[0], len(run)
-                stride = (NWIN + K3) * GROUPS
-                start = (ROWS - 1 - (s + 1 - first_i) % ROWS) * NWIN * GROUPS + K3 * first_i * GROUPS
-                multiply(
-                    out=av[:, first_i : first_i + count, :, :].rearrange("p i j (g c) -> p i j g c", c=CG),
-                    in0=v.rearrange("p (g c) -> p g c", c=CG)
-                    .unsqueeze(1)
-                    .unsqueeze(1)
-                    .to_broadcast([P, count, K3, GROUPS, CG]),
-                    in1=attn_pix_of[b][:]
-                    .rearrange("p r n g -> p (r n g)")[:, start : start + count * stride]
-                    .rearrange("p (i x) -> p i x", x=stride)[:, :, 0 : K3 * GROUPS]
-                    .rearrange("p i (j g) -> p i j g", g=GROUPS)
-                    .unsqueeze(4)
-                    .to_broadcast([P, count, K3, GROUPS, CG]),
-                    op=ALU.mult,
-                )
+            first_i, count = window_rows[0], len(window_rows)
+            nc.vector.tensor_tensor(
+                out=av[:, first_i : first_i + count, :, :].rearrange("p i j (g c) -> p (i j) g c", c=CG),
+                in0=for_vector_of[(s + LAG - 1) // PAIR][:, (s + LAG - 1) % PAIR, 1, :]
+                .rearrange("p (g c) -> p g c", c=CG)
+                .unsqueeze(1)
+                .to_broadcast([P, K3 * count, GROUPS, CG]),
+                in1=attn_ring[:, s % ATTN_RING, K3 * first_i : K3 * (first_i + count), :]
+                .unsqueeze(3)
+                .to_broadcast([P, K3 * count, GROUPS, CG]),
+                op=ALU.mult,
+            )
 
         def attn_v_sums(t):
             places = [K3 * i + j for i in range(K3) if 0 <= t + i - 1 < H for j in range(K3)]
@@ -523,7 +486,7 @@ def tile_mutliheadattention2d_kernel(
                 nc.tensor.matmul(
                     out=out_ps_of[c][:, r, :],
                     lhsT=av_of[t + n // K3 - 1][:, n // K3, n % K3, :],
-                    rhs=rotate[n % K3][:],
+                    rhs=rotate[n % K3],
                     is_transpose=True,
                     start=(n == places[0]),
                     stop=(n == places[-1]),
@@ -542,14 +505,13 @@ def tile_mutliheadattention2d_kernel(
 
             c, stage = divmod(step + LEAD, CHUNK_ROWS)
             if stage == 0:
-                if 1 <= c < CHUNKS:
-                    quantise(c, PAIR)
-                if RAW_BUFS + len(EARLY_TAGS) <= c + RAW_BUFS < CHUNKS:
-                    load_x(c + RAW_BUFS)
-            if stage == PAIR and c + 1 < CHUNKS:
-                quantise(c + 1, 0)
+                ahead = c + RAW_BUFS + (len(EARLY_TAGS) if c < RAW_BUFS else 0)
+                if RAW_BUFS + len(EARLY_TAGS) <= ahead < CHUNKS and not RAW_BUFS <= c < RAW_BUFS + len(EARLY_TAGS):
+                    load_x(ahead)
+            due = (c, PAIR) if stage == 0 else (c + 1, 0) if stage == PAIR else None
+            due_grouped = grouped_of.get(due[0]) if due else None
             if c + 1 < CHUNKS:
-                regroup(c + 1, stage)
+                regroup(c + 1, stage, nc.vector.tensor_copy if step < 0 else nc.scalar.copy)
 
             if step % PAIR == 1:
                 mx_passes(step)
@@ -557,34 +519,37 @@ def tile_mutliheadattention2d_kernel(
                     if 0 <= t < H:
                         q_dot_rel(t)
                 empty_for_scalar(step)
+
+            since_of = [step - b * ROWS for b in range(BANDS)]
+            for b, since in enumerate(since_of):
+                if SUB_AT <= since < SUB_AT + K3:
+                    softmax_subtract(b, since - SUB_AT)
+                if SCALE_AT <= since < SCALE_AT + K3:
+                    softmax_scale(b, since - SCALE_AT)
             if 0 <= step - 1 < H:
                 energy_products(step - 1)
                 fold(step - 1)
 
-            if 0 <= source < H and not on_gpsimd(source):
+            if 0 <= source < H:
                 attn_v_products(source)
             if 0 <= source - 2 < H:
                 attn_v_sums(source - 2)
 
-            for b in range(BANDS):
-                since = step - b * ROWS
+            for b, since in enumerate(since_of):
                 if SUMS_AT <= since < SUMS_AT + SUM_STEPS:
                     energy_sums(b, since - SUMS_AT)
                 if since == MAX_AT:
                     softmax_max(b)
-                if SUB_AT <= since < SUB_AT + K3:
-                    softmax_subtract(b, since - SUB_AT)
                 if EXP_AT <= since < EXP_AT + K3:
                     softmax_exp(b, since - EXP_AT)
                 if since == TOTAL_AT:
                     softmax_total(b)
                 if since == INVERSE_AT:
                     softmax_inverse(b)
-                if SCALE_AT <= since < SCALE_AT + K3:
-                    softmax_scale(b, since - SCALE_AT)
                 if TURN_AT <= since < TURN_AT + K3:
                     turn_attn(b, since - TURN_AT)
                 if STORE_AT <= since < STORE_AT + STORE_STEPS:
                     store_attn(b, since - STORE_AT)
-            if on_gpsimd(source + GP_AHEAD):
-                attn_v_products(source + GP_AHEAD)
+
+            if due and 1 <= due[0] < CHUNKS:
+                quantise(*due, due_grouped)

from contextlib import ExitStack

import concourse.mybir as mybir
from concourse.masks import make_identity

F32 = mybir.dt.float32
BF16 = mybir.dt.bfloat16
U32 = mybir.dt.uint32
U8 = mybir.dt.uint8
I32 = mybir.dt.int32
FP8X4 = mybir.dt.float8_e4m3fn_x4
ALU = mybir.AluOpType
AXIS_X = mybir.AxisListType.X
EXP = mybir.ActivationFunctionType.Exp

P = 128
PACK = 4
RUN = 4
C_IN = P * PACK
C_OUT = 128
H = 128
W = 128
GROUPS = 8
CG = C_OUT // GROUPS
CG_HALF = CG // 2
K3 = 3
NWIN = K3 * K3
ROWS = P // GROUPS
BANDS = H // ROWS
CHUNK_ROWS = 4
CHUNK = CHUNK_ROWS * W
CHUNKS = H // CHUNK_ROWS
PADS = 2
WPAD = W + PADS
QUADRANTS = 4
LIVE = 4

SLACK = 2
PAIR = 2
Q_AHEAD = 5
K_AHEAD = 7
SHIFT_CUT = 112
ATTN_RING = 2 * ROWS
K_RING = 12
LEAD = K_AHEAD
SUMS_AT = ROWS + SLACK
FOLDED = NWIN - K3
PLANES = [CG + 1] * K3 + [CG_HALF + 1] * FOLDED
SUM_STEPS = 9
PLANES_A_STEP = [16 if s % PAIR == 0 else 7 for s in range(SUM_STEPS)]
MAX_AT = SUMS_AT + SUM_STEPS
SUB_AT = MAX_AT + 1
EXP_AT = SUB_AT + SLACK
TOTAL_AT = EXP_AT + K3
INVERSE_AT = TOTAL_AT + 1
SCALE_AT = INVERSE_AT + 1
TURN_AT = SCALE_AT + SLACK
STORE_AT = TURN_AT + K3 + 1
STORE_STEPS = 4
LAG = TURN_AT + K3 + 1
LAST = H + LAG + 2

SINGLE = 1
DOUBLE = 2
RAW_BUFS = 2
EARLY_TAGS = ("unfolded", "folded")
CHUNK_BUFS = 4
QK_BUFS = 3
AV_BUFS = 6
CODES_BUFS = (LAG + LEAD + PAIR) // CHUNK_ROWS + 1


PROJECTIONS = 3
Q_IDX, K_IDX, V_IDX = 0, 1, 2

FLOPS = 2 * C_IN * PROJECTIONS * C_OUT * H * W + 2 * 2 * NWIN * C_OUT * H * W


def tile_mutliheadattention2d_kernel(
    tc, x, wq_words, wq_scales, wk_words, wk_scales, wv_words, wv_scales, rel_t, rel_f, out, attn
):
    nc = tc.nc
    with ExitStack() as ctx:
        depths = sorted({SINGLE, DOUBLE, RAW_BUFS, CHUNK_BUFS, QK_BUFS, AV_BUFS, CODES_BUFS})
        sbuf = {n: ctx.enter_context(tc.tile_pool(name="sbuf%d" % n, bufs=n)) for n in depths}
        ps_s = ctx.enter_context(tc.psum_pool(name="ps_s", bufs=2))
        ps_v = ctx.enter_context(tc.psum_pool(name="ps_v", bufs=2))
        ps_soft = ctx.enter_context(tc.psum_pool(name="ps_soft", bufs=2))
        ps_out = ctx.enter_context(tc.psum_pool(name="ps_out", bufs=2))

        x_by_word = x[0].rearrange("(p e) h w -> p e (h w)", e=PACK)

        raw_of = {}
        grouped_of = {}
        codes_of = {}
        for_scalar_of = {}
        for_vector_of = {}
        q_rows_of = {}
        qr_of = {}
        qr_pix_of = {}
        qk_of = {}
        folded_of = {}
        unfolded_of = {}
        e_ps_of = {}
        top_of = {}
        total_of = {}
        inverse_of = {}
        energy_of = {}
        attn_store_of = {}
        attn_rows_of = {}
        av_of = {}
        out_ps_of = {}

        def load_x(c, tag="raw"):
            raw = sbuf[RAW_BUFS].tile([P, PACK, CHUNK], BF16, name="raw", tag=tag)
            nc.sync.dma_start(out=raw[:], in_=x_by_word[:, :, c * CHUNK : (c + 1) * CHUNK])
            raw_of[c] = raw

        def regroup(c, r, copy=nc.scalar.copy):
            if r % PAIR == 0:
                grouped_of[c] = sbuf[DOUBLE].tile([P, PAIR * W, PACK], BF16, name="grouped", align_bytes=64)
            first = r % PAIR * W
            copy(
                out=grouped_of[c][:, first : first + W, :].rearrange("p (u i) e -> p u e i", i=RUN),
                in_=raw_of[c][:, :, r * W : (r + 1) * W].rearrange("p e (u i) -> p u e i", i=RUN),
            )

        def quantise(c, r, grouped):
            if r == 0:
                codes = sbuf[CODES_BUFS].tile([P, CHUNK], U32, name="codes", align_bytes=64)
                scales = sbuf[CODES_BUFS].tile([P, CHUNK], U8, name="scales", align_bytes=64)
                codes_of[c] = (codes, scales)
            codes, scales = codes_of[c]
            nc.vector.quantize_mx(
                out=codes[:, r * W : (r + PAIR) * W].bitcast(FP8X4),
                scales=scales[:, r * W : (r + PAIR) * W],
                in_=grouped[:].rearrange("p w e -> p (w e)"),
            )

        load_x(0)
        w_codes = sbuf[SINGLE].tile([P, PROJECTIONS, C_OUT], U32, name="w_codes", align_bytes=64)
        w_scales = sbuf[SINGLE].tile([P, PROJECTIONS, C_OUT], U8, name="w_scales", align_bytes=64)
        nc.vector.memset(w_scales[:].rearrange("p a n -> p (a n)").bitcast(I32), 0)
        half = C_OUT // 2
        rel3 = sbuf[SINGLE].tile([P, K3], BF16, name="rel3")
        for idx, words, scales in (
            (K_IDX, wk_words, wk_scales), (Q_IDX, wq_words, wq_scales), (V_IDX, wv_words, wv_scales)
        ):
            if idx == Q_IDX:
                nc.sync.dma_start(out=rel3[0:half, :], in_=rel_t)
                nc.sync.dma_start(out=rel3[half:P, :], in_=rel_f)
            if idx == V_IDX:
                load_x(1)
            nc.sync.dma_start(
                out=w_codes[:, idx, :].bitcast(I32),
                in_=words[0].rearrange("p n e -> p (n e)").bitcast(I32),
            )
            for quad in range(QUADRANTS):
                first_partition = quad * (P // QUADRANTS)
                nc.sync.dma_start(
                    out=w_scales[first_partition : first_partition + LIVE, idx, :].bitcast(I32),
                    in_=scales[0, quad * LIVE : (quad + 1) * LIVE, :].bitcast(I32),
                )

        wide = sbuf[SINGLE].tile([P, 1 + P + 1], F32, name="wide")
        ident = wide[:, 1 : 1 + P]
        make_identity(nc, ident)
        nc.gpsimd.tensor_copy(out=wide[:, 0:1], in_=wide[:, P : P + 1])
        nc.gpsimd.tensor_copy(out=wide[:, P + 1 : P + 2], in_=wide[:, 1:2])
        rotate = [wide[:, j : j + P] for j in range(K3)]

        k_ring = sbuf[SINGLE].tile([P, K3, K_RING, C_OUT], F32, name="k_ring")
        for shifted in (0, K3 - 1):
            nc.gpsimd.memset(k_ring[:, shifted, :, :], 0.0)

        for c, tag in enumerate(EARLY_TAGS, RAW_BUFS):
            load_x(c, tag)
        for r in range(CHUNK_ROWS):
            regroup(0, r, nc.scalar.copy if r % PAIR else nc.vector.tensor_copy)
            if r % PAIR == PAIR - 1:
                quantise(0, r + 1 - PAIR, grouped_of[0])

        w_codes_pl = sbuf[SINGLE].tile([P, 2, C_OUT], U32, name="w_codes_pl", align_bytes=64)
        w_scales_pl = sbuf[SINGLE].tile([P, 2, C_OUT], U8, name="w_scales_pl", align_bytes=64)
        for idx in (K_IDX, Q_IDX):
            nc.vector.tensor_copy(
                out=w_codes_pl[:, idx, :].bitcast(I32).rearrange("p (c g) -> p g c", g=GROUPS),
                in_=w_codes[:, idx, :].bitcast(I32).rearrange("p (g c) -> p g c", c=CG),
            )
            nc.vector.tensor_copy(
                out=w_scales_pl[:, idx, :].rearrange("p (c g) -> p g c", g=GROUPS),
                in_=w_scales[:, idx, :].rearrange("p (g c) -> p g c", c=CG),
            )

        rel9 = sbuf[SINGLE].tile([P, K3, K3], F32, name="rel9")
        nc.vector.tensor_copy(
            out=rel9[0:half], in_=rel3[0:half, :].unsqueeze(2).to_broadcast([half, K3, K3])
        )
        nc.vector.tensor_copy(
            out=rel9[half:P], in_=rel3[half:P, :].unsqueeze(1).to_broadcast([half, K3, K3])
        )
        in_group = sbuf[SINGLE].tile([P, GROUPS], F32, name="in_group")
        nc.vector.tensor_reduce(
            out=in_group[:], in_=ident.rearrange("p (g c) -> p g c", c=CG), axis=AXIS_X, op=ALU.add
        )
        rel_by_place = sbuf[SINGLE].tile([P, NWIN, GROUPS], F32, name="rel_by_place")
        nc.vector.tensor_tensor(
            out=rel_by_place[:],
            in0=rel9[:].rearrange("p i j -> p (i j)").unsqueeze(2).to_broadcast([P, NWIN, GROUPS]),
            in1=in_group[:].unsqueeze(1).to_broadcast([P, NWIN, GROUPS]),
            op=ALU.mult,
        )

        def x_row(t):
            codes, scales = codes_of[t // CHUNK_ROWS]
            cols = slice((t % CHUNK_ROWS) * W, (t % CHUNK_ROWS + 1) * W)
            return codes[:, cols].bitcast(FP8X4), scales[:, cols]

        def by_channel(out, t, idx):
            x_codes, x_scales = x_row(t)
            nc.tensor.matmul_mx(
                out=out,
                lhsT=w_codes[:, idx, :].bitcast(FP8X4),
                lhsT_scale=w_scales[:, idx, :],
                rhs=x_codes,
                rhs_scale=x_scales,
                start=True,
                stop=True,
            )

        def by_pixel(out, t, codes_ap, scales_ap):
            x_codes, x_scales = x_row(t)
            nc.tensor.matmul_mx(
                out=out,
                lhsT=x_codes,
                lhsT_scale=x_scales,
                rhs=codes_ap.bitcast(FP8X4),
                rhs_scale=scales_ap,
                start=True,
                stop=True,
            )

        def mx_passes(step):
            q_rows = [t for t in (step + Q_AHEAD, step + Q_AHEAD + 1) if 0 <= t < H]
            k_rows = [t for t in (step + K_AHEAD, step + K_AHEAD + 1) if 0 <= t < H]
            if q_rows or k_rows:
                for_scalar_of[step] = ps_s.tile([P, PAIR, 2, W], F32, name="for_scalar")
            for t in q_rows:
                by_channel(for_scalar_of[step][:, t % PAIR, 0, :], t, Q_IDX)
            for t in k_rows:
                by_pixel(
                    for_scalar_of[step][:, t % PAIR, 1, :], t, w_codes_pl[:, K_IDX, :], w_scales_pl[:, K_IDX, :]
                )
            pair = (step + 1) // PAIR
            rows = (step + 1, step + 2)
            if any(0 <= t < H or 0 <= t + 1 - LAG < H for t in rows):
                for_vector_of[pair] = ps_v.tile([P, PAIR, 2, C_OUT], F32, name="for_vector")
            for t in rows:
                if 0 <= t < H:
                    by_pixel(
                        for_vector_of[pair][:, t % PAIR, 0, :], t, w_codes_pl[:, Q_IDX, :], w_scales_pl[:, Q_IDX, :]
                    )
                s = t + 1 - LAG
                if 0 <= s < H:
                    by_pixel(for_vector_of[pair][:, t % PAIR, 1, :], s, w_codes[:, V_IDX, :], w_scales[:, V_IDX, :])

        def empty_for_scalar(step):
            q_row, k_row = step + Q_AHEAD, step + K_AHEAD
            if 0 <= q_row < H:
                q_rows_of[q_row] = sbuf[DOUBLE].tile([P, PAIR, W], F32, name="q_rows")
                nc.scalar.copy(out=q_rows_of[q_row][:], in_=for_scalar_of[step][:, :, 0, :])
            if 0 <= k_row < H:
                slot = k_row % K_RING
                nc.scalar.copy(out=k_ring[:, 1, slot : slot + PAIR, :], in_=for_scalar_of[step][:, :, 1, :])
                shifted_rows = PAIR if k_row < CHUNK_ROWS else CHUNK_ROWS
                if (k_row + PAIR) % shifted_rows == 0:
                    slots = slice(slot + PAIR - shifted_rows, slot + PAIR)
                    for low, high in ((0, SHIFT_CUT), (SHIFT_CUT, P - 1)):
                        nc.sync.dma_start(
                            out=k_ring[low + 1 : high + 1, 0, slots, :], in_=k_ring[low:high, 1, slots, :]
                        )
                        nc.sync.dma_start(
                            out=k_ring[low:high, 2, slots, :], in_=k_ring[low + 1 : high + 1, 1, slots, :]
                        )

        def q_dot_rel(t):
            if t % PAIR == 0:
                qr_of[t] = ps_soft.tile([P, PAIR, C_OUT], F32, name="qr", tag="soft")
            qr = qr_of[t - t % PAIR]
            nc.tensor.matmul(
                out=qr[:, t % PAIR, 0 : NWIN * GROUPS],
                lhsT=q_rows_of[t - t % PAIR][:, t % PAIR, :],
                rhs=rel_by_place[:].rearrange("p n g -> p (n g)"),
                start=True,
                stop=True,
            )
            if t % PAIR == PAIR - 1:
                b, first_row = divmod(t + 1 - PAIR, ROWS)
                if first_row == 0:
                    qr_pix_of[b] = sbuf[DOUBLE].tile([P, NWIN, ROWS, GROUPS], F32, name="qr_pix")
                nc.scalar.copy(
                    out=qr_pix_of[b][:, :, first_row : first_row + PAIR, :].rearrange("p n r g -> p r n g"),
                    in_=qr[:, :, 0 : NWIN * GROUPS].rearrange("p r (n g) -> p r n g", g=GROUPS),
                )

        def energy_products(t):
            q = for_vector_of[t // PAIR][:, t % PAIR, 0, :]
            b, r = divmod(t, ROWS)
            if r == 0:
                unfolded_of[b] = sbuf[DOUBLE].tile([P, K3, CG, ROWS, GROUPS], F32, name="unfolded")
            if t == 0:
                nc.gpsimd.memset(unfolded_of[b][:, :, :, r, :], 0.0)
            else:
                nc.vector.tensor_tensor(
                    out=unfolded_of[b][:, :, :, r, :],
                    in0=k_ring[:, :, (t - 1) % K_RING, :].rearrange("p j (c g) -> p j c g", g=GROUPS),
                    in1=q.rearrange("p (c g) -> p c g", g=GROUPS).unsqueeze(1).to_broadcast([P, K3, CG, GROUPS]),
                    op=ALU.mult,
                )
            qk = sbuf[QK_BUFS].tile([P, FOLDED, C_OUT], F32, name="qk")
            qk_of[t] = qk
            sources = [s for s in (t, t + 1) if s < H]
            if t == H - 1:
                nc.gpsimd.memset(qk[:, FOLDED - K3 : FOLDED, :], 0.0)
            laps = sorted({s // K_RING for s in sources})
            for run in [[s for s in sources if s // K_RING == lap] for lap in laps]:
                first_i, count = run[0] - t, len(run)
                slot = run[0] % K_RING
                nc.vector.tensor_tensor(
                    out=qk[:, K3 * first_i : K3 * (first_i + count), :].rearrange(
                        "p (i j) o -> p j i o", j=K3
                    ),
                    in0=k_ring[:, :, slot : slot + count, :],
                    in1=q.unsqueeze(1).unsqueeze(1).to_broadcast([P, K3, count, C_OUT]),
                    op=ALU.mult,
                )

        def fold(t):
            b, r = divmod(t, ROWS)
            if r == 0:
                folded_of[b] = sbuf[DOUBLE].tile([P, FOLDED, CG_HALF, ROWS, GROUPS], F32, name="folded")
            planes = qk_of[t][:].rearrange("p n (c g) -> p n c g", g=GROUPS)
            nc.gpsimd.tensor_tensor(
                out=folded_of[b][:, :, :, r, :],
                in0=planes[:, :, 0:CG_HALF, :],
                in1=planes[:, :, CG_HALF:CG, :],
                op=ALU.add,
            )

        planes = [(n, plane) for n in range(NWIN) for plane in range(PLANES[n])]

        def energy_sums(b, part):
            first = sum(PLANES_A_STEP[:part])
            for n, plane in planes[first : first + PLANES_A_STEP[part]]:
                i, j = divmod(n, K3)
                if n == 0 and plane == 0:
                    energy_of[b] = sbuf[SINGLE].tile([P, NWIN, W], F32, name="energy")
                if j == 0 and plane == 0:
                    e_ps_of[(b, i)] = ps_soft.tile([P, K3, W], F32, name="e_ps", tag="soft")
                e_ps = e_ps_of[(b, i)]
                last = plane == PLANES[n] - 1
                if last:
                    columns = qr_pix_of[b][:, n, :, :]
                elif n < K3:
                    columns = unfolded_of[b][:, n, plane, :, :]
                else:
                    columns = folded_of[b][:, n - K3, plane, :, :]
                nc.tensor.matmul(
                    out=e_ps[:, j, :],
                    lhsT=columns.rearrange("p r g -> p (r g)"),
                    rhs=ident,
                    is_transpose=True,
                    start=(plane == 0),
                    stop=last,
                )
                if last and j == K3 - 1:
                    nc.scalar.copy(out=energy_of[b][:, K3 * i : K3 * i + K3, :], in_=e_ps[:])

        def window_row(tile, i):
            return tile[:, K3 * i : K3 * i + K3, :]

        def softmax_max(b):
            tops = sbuf[SINGLE].tile([P, NWIN // 2, W], F32, name="tops")
            energy = energy_of[b]
            half = NWIN // 2
            nc.vector.tensor_max(tops[:], energy[:, 0:half, :], energy[:, half : 2 * half, :])
            while half > 1:
                half //= 2
                nc.vector.tensor_max(tops[:, 0:half, :], tops[:, 0:half, :], tops[:, half : 2 * half, :])
            nc.vector.tensor_max(tops[:, 0, :], tops[:, 0, :], energy[:, NWIN - 1, :])
            top_of[b] = tops

        def softmax_subtract(b, i):
            nc.gpsimd.tensor_tensor(
                out=window_row(energy_of[b], i),
                in0=window_row(energy_of[b], i),
                in1=top_of[b][:, 0:1, :].to_broadcast([P, K3, W]),
                op=ALU.subtract,
            )

        def softmax_exp(b, i):
            nc.scalar.activation(out=window_row(energy_of[b], i), in_=window_row(energy_of[b], i), func=EXP)

        def softmax_total(b):
            total_of[b] = ps_soft.tile([P, W], F32, name="total", tag="soft")
            for n in range(NWIN):
                nc.tensor.matmul(
                    out=total_of[b][:],
                    lhsT=ident,
                    rhs=energy_of[b][:, n, :],
                    start=(n == 0),
                    stop=(n == NWIN - 1),
                )

        def softmax_inverse(b):
            inverse_of[b] = top_of[b][:, 1:2, :]
            nc.vector.reciprocal(out=top_of[b][:, 1, :], in_=total_of[b][:])

        def softmax_scale(b, i):
            if i == 0:
                attn_rows_of[b] = sbuf[SINGLE].tile([P, NWIN, WPAD], F32, name="attn_rows")
                nc.gpsimd.memset(attn_rows_of[b][:, :, 0 : WPAD : WPAD - 1], 0.0)
            nc.gpsimd.tensor_tensor(
                out=window_row(attn_rows_of[b], i)[:, :, 1 : W + 1],
                in0=window_row(energy_of[b], i),
                in1=inverse_of[b].to_broadcast([P, K3, W]),
                op=ALU.mult,
            )

        def store_attn(b, part):
            if part == 0:
                attn_store_of[b] = sbuf[SINGLE].tile([P, W, NWIN], F32, name="attn_store")
            first, last = part * W // STORE_STEPS, (part + 1) * W // STORE_STEPS
            nc.scalar.copy(
                out=attn_store_of[b][:, first:last, :],
                in_=attn_rows_of[b][:, :, 1 + first : 1 + last].rearrange("p n w -> p w n"),
            )
            if part == STORE_STEPS - 1:
                nc.sync.dma_start(
                    out=attn[0, :, b * ROWS : (b + 1) * ROWS, :, :].rearrange("g h w n -> h g (w n)"),
                    in_=attn_store_of[b][:].rearrange("p w n -> p (w n)"),
                )

        attn_ring = sbuf[SINGLE].tile([P, ATTN_RING, NWIN, GROUPS], F32, name="attn_ring")

        def turn_attn(b, i):
            a_ps = ps_soft.tile([P, K3, P], F32, name="a_ps", tag="soft")
            for j in range(K3):
                padded_col = 1 - (j - 1)
                nc.tensor.transpose(
                    a_ps[:, j, :], attn_rows_of[b][:, K3 * i + j, padded_col : padded_col + W], ident
                )
            first = b * ROWS + i - 1
            sources = [s for s in range(first, first + ROWS) if 0 <= s < H]
            for lap in sorted({s // ATTN_RING for s in sources}):
                run = [s for s in sources if s // ATTN_RING == lap]
                slot, row = run[0] % ATTN_RING, run[0] - first
                nc.scalar.copy(
                    out=attn_ring[:, slot : slot + len(run), K3 * i : K3 * i + K3, :].rearrange("p r n g -> p n r g"),
                    in_=a_ps[:].rearrange("p j (r g) -> p j r g", g=GROUPS)[:, :, row : row + len(run), :],
                )

        def attn_v_products(s):
            av = sbuf[AV_BUFS].tile([P, K3, K3, C_OUT], F32, name="av")
            av_of[s] = av
            window_rows = [i for i in range(K3) if 0 <= s + 1 - i < H]
            first_i, count = window_rows[0], len(window_rows)
            nc.vector.tensor_tensor(
                out=av[:, first_i : first_i + count, :, :].rearrange("p i j (g c) -> p (i j) g c", c=CG),
                in0=for_vector_of[(s + LAG - 1) // PAIR][:, (s + LAG - 1) % PAIR, 1, :]
                .rearrange("p (g c) -> p g c", c=CG)
                .unsqueeze(1)
                .to_broadcast([P, K3 * count, GROUPS, CG]),
                in1=attn_ring[:, s % ATTN_RING, K3 * first_i : K3 * (first_i + count), :]
                .unsqueeze(3)
                .to_broadcast([P, K3 * count, GROUPS, CG]),
                op=ALU.mult,
            )

        def attn_v_sums(t):
            places = [K3 * i + j for i in range(K3) if 0 <= t + i - 1 < H for j in range(K3)]
            c, r = divmod(t, CHUNK_ROWS)
            if r == 0:
                out_ps_of[c] = ps_out.tile([P, CHUNK_ROWS, W], F32, name="out_ps")
            for n in places:
                nc.tensor.matmul(
                    out=out_ps_of[c][:, r, :],
                    lhsT=av_of[t + n // K3 - 1][:, n // K3, n % K3, :],
                    rhs=rotate[n % K3],
                    is_transpose=True,
                    start=(n == places[0]),
                    stop=(n == places[-1]),
                )

        def store_out(c):
            out_rows = sbuf[SINGLE].tile([P, CHUNK_ROWS, W], F32, name="out_rows")
            nc.scalar.copy(out=out_rows[:], in_=out_ps_of[c][:])
            nc.sync.dma_start(out=out[0, :, c * CHUNK_ROWS : (c + 1) * CHUNK_ROWS, :], in_=out_rows[:])

        ctx.enter_context(tc.manual_schedule(engines={mybir.EngineType.Activation, mybir.EngineType.Pool}))
        for step in range(-LEAD, LAST + 1):
            source = step - LAG
            if 0 <= source - 3 < H and (source - 3) % CHUNK_ROWS == CHUNK_ROWS - 1:
                store_out((source - 3) // CHUNK_ROWS)

            c, stage = divmod(step + LEAD, CHUNK_ROWS)
            if stage == 0:
                ahead = c + RAW_BUFS + (len(EARLY_TAGS) if c < RAW_BUFS else 0)
                if RAW_BUFS + len(EARLY_TAGS) <= ahead < CHUNKS and not RAW_BUFS <= c < RAW_BUFS + len(EARLY_TAGS):
                    load_x(ahead)
            due = (c, PAIR) if stage == 0 else (c + 1, 0) if stage == PAIR else None
            due_grouped = grouped_of.get(due[0]) if due else None
            if c + 1 < CHUNKS:
                regroup(c + 1, stage, nc.vector.tensor_copy if step < 0 else nc.scalar.copy)

            if step % PAIR == 1:
                mx_passes(step)
                for t in (step + Q_AHEAD - PAIR, step + Q_AHEAD - 1):
                    if 0 <= t < H:
                        q_dot_rel(t)
                empty_for_scalar(step)

            since_of = [step - b * ROWS for b in range(BANDS)]
            for b, since in enumerate(since_of):
                if SUB_AT <= since < SUB_AT + K3:
                    softmax_subtract(b, since - SUB_AT)
                if SCALE_AT <= since < SCALE_AT + K3:
                    softmax_scale(b, since - SCALE_AT)
            if 0 <= step - 1 < H:
                energy_products(step - 1)
                fold(step - 1)

            if 0 <= source < H:
                attn_v_products(source)
            if 0 <= source - 2 < H:
                attn_v_sums(source - 2)

            for b, since in enumerate(since_of):
                if SUMS_AT <= since < SUMS_AT + SUM_STEPS:
                    energy_sums(b, since - SUMS_AT)
                if since == MAX_AT:
                    softmax_max(b)
                if EXP_AT <= since < EXP_AT + K3:
                    softmax_exp(b, since - EXP_AT)
                if since == TOTAL_AT:
                    softmax_total(b)
                if since == INVERSE_AT:
                    softmax_inverse(b)
                if TURN_AT <= since < TURN_AT + K3:
                    turn_attn(b, since - TURN_AT)
                if STORE_AT <= since < STORE_AT + STORE_STEPS:
                    store_attn(b, since - STORE_AT)

            if due and 1 <= due[0] < CHUNKS:
                quantise(*due, due_grouped)
